import numpy as np
import ml_dtypes


def mxq(x, axis, fmt="e4m3"):
    dtype, down = {"e4m3": (ml_dtypes.float8_e4m3fn, 7), "e5m2": (ml_dtypes.float8_e5m2, 14)}[fmt]
    v = np.moveaxis(np.asarray(x, np.float32).astype(ml_dtypes.bfloat16).astype(np.float64), axis, -1)
    blocks = v.reshape(v.shape[:-1] + (-1, 32))
    amax = np.abs(blocks).max(-1, keepdims=True)
    byte = np.maximum(np.where(amax > 0, np.frexp(amax)[1] - 1 + 127, 0) - down, 1)
    scale = np.exp2(byte - 127.0)
    codes = (blocks / scale).astype(np.float32).astype(dtype).astype(np.float64)
    return np.moveaxis((codes * scale).reshape(v.shape), -1, axis)


WIDE = False


def mx_kscale(k):
    if not WIDE:
        return np.ones(k)
    levels = np.array([10, -10, 5, -5, 0])
    a = np.random.permutation(np.resize(levels, k // 512 * 4)).reshape(k // 512, 4)
    idx = np.arange(k)
    return np.exp2(a[idx // 512, idx % 128 // 32])


BF16 = ml_dtypes.bfloat16


def bf(x):
    return np.asarray(x, np.float32).astype(BF16)


def f64(x):
    return np.asarray(x).astype(np.float64)


E2M1 = np.array([0.0, 0.5, 1.0, 1.5, 2.0, 3.0, 4.0, 6.0, -0.0, -0.5, -1.0, -1.5, -2.0, -3.0, -4.0, -6.0])


def pack_weight(w, fmt):
    k, n = w.shape
    w = f64(bf(w)).reshape(k // 32, 32, n)
    amax = np.abs(w).max(1)
    if fmt == "e4m3":
        byte = np.frexp(amax)[1] - 1 + 127 - 7
    else:
        mant, ex = np.frexp(amax / 6.0)
        byte = np.where(mant > 0.5, ex, ex - 1) + 127
    byte = np.clip(np.where(amax > 0, byte, 1), 1, 254)
    scaled = (w * np.exp2(127.0 - byte)[:, None, :]).reshape(k, n).astype(np.float32)
    by_word = np.ascontiguousarray(scaled.reshape(k // 512, 128, 4, n).transpose(0, 1, 3, 2))
    if fmt == "e4m3":
        words = by_word.astype(ml_dtypes.float8_e4m3fn).view(np.uint8)
    else:
        c = by_word.astype(ml_dtypes.float4_e2m1fn).view(np.uint8) & 0xF
        words = c[..., 0::2] | (c[..., 1::2] << 4)
    return np.ascontiguousarray(words), np.ascontiguousarray(byte.astype(np.uint8).reshape(k // 512, 16, n))


def unpack_weight(words, scales, fmt):
    g, p, n, _ = words.shape
    if fmt == "e4m3":
        vals = np.ascontiguousarray(words).view(ml_dtypes.float8_e4m3fn).astype(np.float64)
    else:
        nib = np.empty((g, p, n, 4), np.uint8)
        nib[..., 0::2] = words & 0xF
        nib[..., 1::2] = words >> 4
        vals = E2M1[nib]
    vals = vals * np.repeat(np.exp2(scales.astype(np.float64) - 127.0), 8, axis=1)[..., None]
    return vals.transpose(0, 1, 3, 2).reshape(g * 512, n)


B, D_IN, D_H, C = 512, 1024, 4096, 128
TAU, T1, T2 = 0.5, 3, 3
G, GB = 3.0, 3.0
FMT = "e4m3"


def inv_apprx(v, t, m):
    a = 2.0 - (2.0 / m) * v
    b = 1.0 - (2.0 / m) * v
    for _ in range(t):
        b = b * b
        a = a * (1.0 + b)
    return (2.0 / m) * a


def comp_max_tau(p, tau, t1, t2):
    res = np.concatenate([p, np.full((p.shape[0], 1), tau)], axis=1)
    for i in range(t1):
        res = res * res
        sum_res = res.sum(axis=1)
        m = (2.0 + tau * tau) if i == 0 else 2.0
        res = res * inv_apprx(sum_res, t2, m)[:, None]
    return res[:, -1]


def softmax(z):
    e = np.exp(z - z.max(-1, keepdims=True))
    return e / e.sum(-1, keepdims=True)


def mlp(xq, W1_words, W1_scales, b1, W2_words, W2_scales, b2):
    h = np.maximum((xq @ unpack_weight(W1_words, W1_scales, FMT)) + f64(b1), 0.0)
    return softmax((mxq(h, 1, "e4m3") @ unpack_weight(W2_words, W2_scales, FMT)) + f64(b2))


def setup_inputs():
    s, t = mx_kscale(D_IN), mx_kscale(D_H)
    x = bf(np.random.standard_normal((B, D_IN)) * s)
    W1o_words, W1o_scales = pack_weight(np.random.standard_normal((D_IN, D_H)) / np.sqrt(D_IN) / s[:, None] * t, FMT)
    b1o = bf(np.random.standard_normal(D_H) * 0.2 * t)
    W2o_words, W2o_scales = pack_weight(np.random.standard_normal((D_H, C)) * G / np.sqrt(D_H) / t[:, None], FMT)
    b2o = bf(np.random.standard_normal(C) * GB)
    W1f_words, W1f_scales = pack_weight(np.random.standard_normal((D_IN, D_H)) / np.sqrt(D_IN) / s[:, None] * t, FMT)
    b1f = bf(np.random.standard_normal(D_H) * 0.2 * t)
    W2f_words, W2f_scales = pack_weight(np.random.standard_normal((D_H, C)) * G / np.sqrt(D_H) / t[:, None], FMT)
    b2f = bf(np.random.standard_normal(C) * GB)
    return {"x": x,
            "W1o_words": W1o_words, "W1o_scales": W1o_scales,
            "b1o": b1o,
            "W2o_words": W2o_words, "W2o_scales": W2o_scales,
            "b2o": b2o,
            "W1f_words": W1f_words, "W1f_scales": W1f_scales,
            "b1f": b1f,
            "W2f_words": W2f_words, "W2f_scales": W2f_scales,
            "b2f": b2f}


def reference(x, W1o_words, W1o_scales, b1o, W2o_words, W2o_scales, b2o, W1f_words, W1f_scales, b1f, W2f_words, W2f_scales, b2f):
    xq = mxq(f64(x), 1, "e4m3")
    x1 = mlp(xq, W1o_words, W1o_scales, b1o, W2o_words, W2o_scales, b2o)
    x2 = mlp(xq, W1f_words, W1f_scales, b1f, W2f_words, W2f_scales, b2f)
    cond_in = comp_max_tau(x1, TAU, T1, T2)
    return x1 * (1.0 - cond_in[:, None]) + x2 * cond_in[:, None]

@@ -1,0 +1,283 @@
+from contextlib import ExitStack
+
+import concourse.mybir as mybir
+from concourse.masks import make_identity
+
+F32 = mybir.dt.float32
+BF16 = mybir.dt.bfloat16
+I32 = mybir.dt.int32
+U32 = mybir.dt.uint32
+U8 = mybir.dt.uint8
+FP8X4 = mybir.dt.float8_e4m3fn_x4
+ALU = mybir.AluOpType
+ACT = mybir.ActivationFunctionType
+
+P = 128
+K_PASS = 512
+TOKENS, D_IN, D_H, CLASSES = 512, 1024, 4096, 128
+TOKEN_TILES = TOKENS // P
+X_GROUPS = D_IN // K_PASS
+H_GROUPS = D_H // K_PASS
+TAU, GATE_ROUNDS, INVERSE_STEPS = 0.5, 3, 3
+
+FLOPS = 2 * (2 * TOKENS * D_IN * D_H + 2 * TOKENS * D_H * CLASSES)
+
+
+def tile_combnethe_pa_kernel(
+    tc, x, W1o_words, W1o_scales, b1o, W2o_words, W2o_scales, b2o,
+    W1f_words, W1f_scales, b1f, W2f_words, W2f_scales, b2f, out,
+):
+    nc = tc.nc
+    given = (
+        dict(w1=W1o_words, s1=W1o_scales, b1=b1o, w2=W2o_words, s2=W2o_scales, b2=b2o),
+        dict(w1=W1f_words, s1=W1f_scales, b1=b1f, w2=W2f_words, s2=W2f_scales, b2=b2f),
+    )
+    NETS = len(given)
+
+    with ExitStack() as ctx:
+        keep = ctx.enter_context(tc.tile_pool(name="keep", bufs=1))
+        ring = ctx.enter_context(tc.tile_pool(name="ring", bufs=8))
+        sums_psum = ctx.enter_context(tc.psum_pool(name="sums_psum", bufs=4))
+        turn_psum = ctx.enter_context(tc.psum_pool(name="turn_psum", bufs=3))
+        head_psum = ctx.enter_context(tc.psum_pool(name="head_psum", bufs=1))
+
+        w1_planes = []
+        w2_planes = []
+        for v in range(NETS):
+            w1_planes.append(keep.tile([P, D_H], U8, name="w1_planes%d" % v, align_bytes=64))
+            w2_planes.append(keep.tile([P, H_GROUPS, CLASSES], U8, name="w2_planes%d" % v, align_bytes=64))
+            nc.vector.memset(w1_planes[v][:].bitcast(I32), 0)
+            nc.vector.memset(w2_planes[v][:].rearrange("p g c -> p (g c)").bitcast(I32), 0)
+
+        warm_in = keep.tile([P, 1], F32, name="warm_in")
+        warm_out = keep.tile([P, 1], F32, name="warm_out")
+        nc.vector.memset(warm_in[:], 0.0)
+        nc.scalar.activation(out=warm_out[:], in_=warm_in[:], func=ACT.Exp)
+
+        ident = keep.tile([P, P], F32, name="ident")
+        make_identity(nc, ident[:])
+
+        x_rows = []
+        x_view = x.rearrange("(t p) k -> p t k", p=P)
+        for half in range(2):
+            x_rows.append(keep.tile([P, 2, D_IN], BF16, name="x_rows%d" % half))
+            nc.scalar.dma_start(out=x_rows[half][:], in_=x_view[:, 2 * half : 2 * half + 2, :])
+
+        w1 = [[], []]
+        w2 = []
+        b1 = []
+        b2 = []
+        for v in range(NETS):
+            for quadrant in range(4):
+                nc.sync.dma_start(
+                    out=w1_planes[v][32 * quadrant : 32 * quadrant + 4 * X_GROUPS, :].bitcast(I32),
+                    in_=given[v]["s1"][:, 4 * quadrant : 4 * quadrant + 4, :].bitcast(I32),
+                )
+            b1.append(keep.tile([P, D_H], BF16, name="b1_%d" % v))
+            nc.scalar.dma_start(out=b1[v][:], in_=given[v]["b1"].partition_broadcast(P))
+            w1_bytes = given[v]["w1"].rearrange("g p n t -> p g (n t)")
+            for piece in range(H_GROUPS):
+                w1[v].append(keep.tile([P, X_GROUPS, K_PASS], U32, name="w1_%d_%d" % (v, piece), align_bytes=64))
+                nc.sync.dma_start(
+                    out=w1[v][piece][:].bitcast(I32),
+                    in_=w1_bytes[:, :, 4 * K_PASS * piece : 4 * K_PASS * (piece + 1)].bitcast(I32),
+                )
+            b2.append(keep.tile([P, CLASSES], BF16, name="b2_%d" % v))
+            nc.scalar.dma_start(out=b2[v][:], in_=given[v]["b2"].partition_broadcast(P))
+            for quadrant in range(4):
+                nc.sync.dma_start(
+                    out=w2_planes[v][32 * quadrant : 32 * quadrant + 4, :, :].bitcast(I32),
+                    in_=given[v]["s2"][:, 4 * quadrant : 4 * quadrant + 4, :].rearrange("g r c -> r g c").bitcast(I32),
+                )
+            w2.append(keep.tile([P, H_GROUPS, CLASSES], U32, name="w2_%d" % v, align_bytes=64))
+            nc.sync.dma_start(
+                out=w2[v][:].bitcast(I32),
+                in_=given[v]["w2"].rearrange("g p n t -> p g (n t)").bitcast(I32),
+            )
+
+        x_codes = []
+        x_planes = []
+        for tt in range(TOKEN_TILES):
+            x_words = x_rows[tt // 2][:, tt % 2, :].bitcast(F32)
+            turned = turn_psum.tile([P, 2 * X_GROUPS, P], F32, name="turned")
+            for g in range(X_GROUPS):
+                for u in range(2):
+                    nc.tensor.transpose(
+                        turned[:, 2 * g + u, :], x_words[:, 256 * g + u : 256 * (g + 1) : 2], ident[:]
+                    )
+            x_grouped = ring.tile([P, X_GROUPS, P, 4], BF16, name="x_grouped", align_bytes=64)
+            nc.vector.tensor_copy(
+                out=x_grouped[:].bitcast(F32), in_=turned[:].rearrange("p (g u) k -> p g k u", u=2)
+            )
+            x_codes.append(keep.tile([P, X_GROUPS, P], U32, name="x_codes%d" % tt, align_bytes=64))
+            x_planes.append(keep.tile([P, X_GROUPS, P], U8, name="x_planes%d" % tt, align_bytes=64))
+            nc.vector.quantize_mx(
+                out=x_codes[tt][:].rearrange("p g k -> p (g k)").bitcast(FP8X4),
+                scales=x_planes[tt][:].rearrange("p g k -> p (g k)"),
+                in_=x_grouped[:].rearrange("p g k t -> p (g k t)"),
+            )
+
+        h_codes = [[], []]
+        h_planes = [[], []]
+        for v in range(NETS):
+            for tt in range(TOKEN_TILES):
+                h_codes[v].append(keep.tile([P, H_GROUPS, P], U32, name="h_codes%d_%d" % (v, tt), align_bytes=64))
+                h_planes[v].append(keep.tile([P, H_GROUPS, P], U8, name="h_planes%d_%d" % (v, tt), align_bytes=64))
+
+        rounds = [(0, [(tt, piece) for tt in range(TOKEN_TILES)]) for piece in range(H_GROUPS)]
+        rounds += [
+            (1, [(tt, piece) for piece in range(4 * half, 4 * half + 4)])
+            for tt in range(TOKEN_TILES)
+            for half in range(2)
+        ]
+        h_rows = {}
+        h_grouped = {}
+
+        def first_layer(r):
+            v, blocks = rounds[r]
+            for tt, piece in blocks:
+                sums = sums_psum.tile([P, K_PASS], F32, name="sums")
+                for g in range(X_GROUPS):
+                    nc.tensor.matmul_mx(
+                        out=sums[:],
+                        lhsT=x_codes[tt][:, g, :].bitcast(FP8X4),
+                        lhsT_scale=x_planes[tt][:, g, :],
+                        rhs=w1[v][piece][:, g, :].bitcast(FP8X4),
+                        rhs_scale=w1_planes[v][4 * g : P, K_PASS * piece : K_PASS * (piece + 1)],
+                        start=(g == 0),
+                        stop=(g == X_GROUPS - 1),
+                    )
+                rows = ring.tile([P, K_PASS], BF16, name="rows")
+                nc.vector.tensor_tensor(
+                    out=rows[:].rearrange("k (u p e) -> k u p e", u=2, e=2),
+                    in0=sums[:].rearrange("k (p u e) -> k u p e", u=2, e=2),
+                    in1=b1[v][:, K_PASS * piece : K_PASS * (piece + 1)].rearrange("k (p u e) -> k u p e", u=2, e=2),
+                    op=ALU.add,
+                )
+                h_rows[(r, tt, piece)] = rows
+
+        def turn(r):
+            v, blocks = rounds[r]
+            for first in range(0, len(blocks), 2):
+                turned = turn_psum.tile([P, 4, P], F32, name="turned")
+                pair = blocks[first : first + 2]
+                for i, (tt, piece) in enumerate(pair):
+                    words = h_rows[(r, tt, piece)][:].bitcast(F32)
+                    for u in range(2):
+                        nc.tensor.transpose(turned[:, 2 * i + u, :], words[:, P * u : P * (u + 1)], ident[:])
+                for i, (tt, piece) in enumerate(pair):
+                    grouped = ring.tile([P, P, 4], BF16, name="grouped", align_bytes=64)
+                    nc.scalar.activation(
+                        out=grouped[:].rearrange("p k (u e) -> p k u e", u=2),
+                        in_=turned[:, 2 * i : 2 * i + 2, :].bitcast(BF16).rearrange("p u (k e) -> p k u e", e=2),
+                        func=ACT.Relu,
+                    )
+                    h_grouped[(r, tt, piece)] = grouped
+
+        def quantise(r):
+            v, blocks = rounds[r]
+            for tt, piece in blocks:
+                nc.vector.quantize_mx(
+                    out=h_codes[v][tt][:, piece, :].bitcast(FP8X4),
+                    scales=h_planes[v][tt][:, piece, :],
+                    in_=h_grouped[(r, tt, piece)][:].rearrange("p k t -> p (k t)"),
+                )
+
+        neg_max = [keep.tile([P, TOKEN_TILES], F32, name="neg_max%d" % v) for v in range(NETS)]
+        exp_sum = [keep.tile([P, TOKEN_TILES], F32, name="exp_sum%d" % v) for v in range(NETS)]
+        inv_sum = [keep.tile([P, TOKEN_TILES], F32, name="inv_sum%d" % v) for v in range(NETS)]
+        exps = {}
+        x1 = {}
+
+        def head(v, token_tiles):
+            logits_psum = head_psum.tile([P, len(token_tiles), CLASSES], F32, name="logits_psum")
+            for i, tt in enumerate(token_tiles):
+                for g in range(H_GROUPS):
+                    nc.tensor.matmul_mx(
+                        out=logits_psum[:, i, :],
+                        lhsT=h_codes[v][tt][:, g, :].bitcast(FP8X4),
+                        lhsT_scale=h_planes[v][tt][:, g, :],
+                        rhs=w2[v][:, g, :].bitcast(FP8X4),
+                        rhs_scale=w2_planes[v][:, g, :],
+                        start=(g == 0),
+                        stop=(g == H_GROUPS - 1),
+                    )
+            for i, tt in enumerate(token_tiles):
+                column = slice(tt, tt + 1)
+                logits = keep.tile([P, CLASSES], F32, name="logits%d_%d" % (v, tt))
+                nc.vector.tensor_tensor(out=logits[:], in0=logits_psum[:, i, :], in1=b2[v][:], op=ALU.add)
+                nc.vector.tensor_reduce(
+                    out=neg_max[v][:, column], in_=logits[:], axis=mybir.AxisListType.X, op=ALU.max, negate=True
+                )
+                exps[(v, tt)] = keep.tile([P, CLASSES], F32, name="exps%d_%d" % (v, tt))
+                nc.scalar.activation(
+                    out=exps[(v, tt)][:], in_=logits[:], func=ACT.Exp,
+                    bias=neg_max[v][:, column], accum_out=exp_sum[v][:, column],
+                )
+                nc.vector.reciprocal(out=inv_sum[v][:, column], in_=exp_sum[v][:, column])
+
+        def inverse(value, m, name):
+            a = keep.tile([P, TOKEN_TILES], F32, name="a_" + name)
+            b = keep.tile([P, TOKEN_TILES], F32, name="b_" + name)
+            b_plus_1 = keep.tile([P, TOKEN_TILES], F32, name="b_plus_1_" + name)
+            nc.gpsimd.tensor_scalar(out=a[:], in0=value[:], scalar1=-2.0 / m, scalar2=2.0, op0=ALU.mult, op1=ALU.add)
+            nc.gpsimd.tensor_scalar(out=b[:], in0=value[:], scalar1=-2.0 / m, scalar2=1.0, op0=ALU.mult, op1=ALU.add)
+            for step in range(INVERSE_STEPS):
+                nc.gpsimd.tensor_tensor(out=b[:], in0=b[:], in1=b[:], op=ALU.mult)
+                nc.gpsimd.tensor_scalar(out=b_plus_1[:], in0=b[:], scalar1=1.0, scalar2=1.0, op0=ALU.mult, op1=ALU.add)
+                nc.gpsimd.tensor_tensor(out=a[:], in0=a[:], in1=b_plus_1[:], op=ALU.mult)
+            nc.gpsimd.tensor_scalar(out=a[:], in0=a[:], scalar1=2.0 / m, scalar2=0.0, op0=ALU.mult, op1=ALU.add)
+            return a
+
+        def gate():
+            for tt in range(TOKEN_TILES):
+                x1[tt] = keep.tile([P, CLASSES], F32, name="x1_%d" % tt)
+                nc.scalar.activation(out=x1[tt][:], in_=exps[(0, tt)][:], func=ACT.Copy, scale=inv_sum[0][:, tt : tt + 1])
+            last = keep.tile([P, TOKEN_TILES], F32, name="last")
+            nc.gpsimd.memset(last[:], TAU)
+            res = [exps[(0, tt)] for tt in range(TOKEN_TILES)]
+            factor = inv_sum[0]
+            for i in range(GATE_ROUNDS):
+                row_sum = keep.tile([P, TOKEN_TILES], F32, name="row_sum%d" % i)
+                squared = []
+                for tt in range(TOKEN_TILES):
+                    squared.append(keep.tile([P, CLASSES], F32, name="squared%d_%d" % (i, tt)))
+                    nc.scalar.activation(
+                        out=squared[tt][:], in_=res[tt][:], func=ACT.Square,
+                        scale=factor[:, tt : tt + 1], accum_out=row_sum[:, tt : tt + 1],
+                    )
+                nc.gpsimd.tensor_tensor(out=last[:], in0=last[:], in1=last[:], op=ALU.mult)
+                nc.gpsimd.tensor_tensor(out=row_sum[:], in0=row_sum[:], in1=last[:], op=ALU.add)
+                factor = inverse(row_sum, (2.0 + TAU * TAU) if i == 0 else 2.0, "%d" % i)
+                nc.gpsimd.tensor_tensor(out=last[:], in0=last[:], in1=factor[:], op=ALU.mult)
+                res = squared
+            return last
+
+        def blend(tt, cond):
+            column = slice(tt, tt + 1)
+            diff = keep.tile([P, CLASSES], F32, name="diff%d" % tt)
+            nc.vector.scalar_tensor_tensor(
+                out=diff[:], in0=exps[(1, tt)][:], scalar=inv_sum[1][:, column], in1=x1[tt][:],
+                op0=ALU.mult, op1=ALU.subtract,
+            )
+            mixed = keep.tile([P, CLASSES], F32, name="mixed%d" % tt)
+            nc.vector.scalar_tensor_tensor(
+                out=mixed[:], in0=diff[:], scalar=cond[:, column], in1=x1[tt][:], op0=ALU.mult, op1=ALU.add
+            )
+            nc.sync.dma_start(out=out[P * tt : P * (tt + 1), :], in_=mixed[:])
+
+        cond = None
+        for r in range(len(rounds) + 2):
+            if r < len(rounds):
+                first_layer(r)
+            if 0 <= r - 1 < len(rounds):
+                turn(r - 1)
+            if 0 <= r - 2 < len(rounds):
+                quantise(r - 2)
+                v, blocks = rounds[r - 2]
+                if v == 0 and r - 2 == H_GROUPS - 1:
+                    head(0, list(range(TOKEN_TILES)))
+                    cond = gate()
+                if v == 1 and blocks[-1][1] == H_GROUPS - 1:
+                    head(1, [blocks[-1][0]])
+                    blend(blocks[-1][0], cond)

@@ -37,9 +37,17 @@ def tile_combnethe_pa_kernel(
     with ExitStack() as ctx:
         keep = ctx.enter_context(tc.tile_pool(name="keep", bufs=1))
         ring = ctx.enter_context(tc.tile_pool(name="ring", bufs=8))
+        round_ring = ctx.enter_context(tc.tile_pool(name="round_ring", bufs=3))
+        ctx.enter_context(tc.manual_schedule())
         sums_psum = ctx.enter_context(tc.psum_pool(name="sums_psum", bufs=4))
         turn_psum = ctx.enter_context(tc.psum_pool(name="turn_psum", bufs=3))
         head_psum = ctx.enter_context(tc.psum_pool(name="head_psum", bufs=1))
+
+        x_rows = []
+        x_view = x.rearrange("(t p) k -> p t k", p=P)
+        for half in range(2):
+            x_rows.append(keep.tile([P, 2, D_IN], BF16, name="x_rows%d" % half))
+            nc.scalar.dma_start(out=x_rows[half][:], in_=x_view[:, 2 * half : 2 * half + 2, :])
 
         w1_planes = []
         w2_planes = []
@@ -49,19 +57,8 @@ def tile_combnethe_pa_kernel(
             nc.vector.memset(w1_planes[v][:].bitcast(I32), 0)
             nc.vector.memset(w2_planes[v][:].rearrange("p g c -> p (g c)").bitcast(I32), 0)
 
-        warm_in = keep.tile([P, 1], F32, name="warm_in")
-        warm_out = keep.tile([P, 1], F32, name="warm_out")
-        nc.vector.memset(warm_in[:], 0.0)
-        nc.scalar.activation(out=warm_out[:], in_=warm_in[:], func=ACT.Exp)
-
         ident = keep.tile([P, P], F32, name="ident")
         make_identity(nc, ident[:])
-
-        x_rows = []
-        x_view = x.rearrange("(t p) k -> p t k", p=P)
-        for half in range(2):
-            x_rows.append(keep.tile([P, 2, D_IN], BF16, name="x_rows%d" % half))
-            nc.scalar.dma_start(out=x_rows[half][:], in_=x_view[:, 2 * half : 2 * half + 2, :])
 
         w1 = [[], []]
         w2 = []
@@ -74,7 +71,8 @@ def tile_combnethe_pa_kernel(
                     in_=given[v]["s1"][:, 4 * quadrant : 4 * quadrant + 4, :].bitcast(I32),
                 )
             b1.append(keep.tile([P, D_H], BF16, name="b1_%d" % v))
-            nc.scalar.dma_start(out=b1[v][:], in_=given[v]["b1"].partition_broadcast(P))
+            bias_queue = nc.scalar if v == 0 else nc.sync
+            bias_queue.dma_start(out=b1[v][:], in_=given[v]["b1"].partition_broadcast(P))
             w1_bytes = given[v]["w1"].rearrange("g p n t -> p g (n t)")
             for piece in range(H_GROUPS):
                 w1[v].append(keep.tile([P, X_GROUPS, K_PASS], U32, name="w1_%d_%d" % (v, piece), align_bytes=64))
@@ -83,7 +81,7 @@ def tile_combnethe_pa_kernel(
                     in_=w1_bytes[:, :, 4 * K_PASS * piece : 4 * K_PASS * (piece + 1)].bitcast(I32),
                 )
             b2.append(keep.tile([P, CLASSES], BF16, name="b2_%d" % v))
-            nc.scalar.dma_start(out=b2[v][:], in_=given[v]["b2"].partition_broadcast(P))
+            nc.sync.dma_start(out=b2[v][:], in_=given[v]["b2"].partition_broadcast(P))
             for quadrant in range(4):
                 nc.sync.dma_start(
                     out=w2_planes[v][32 * quadrant : 32 * quadrant + 4, :, :].bitcast(I32),
@@ -94,6 +92,11 @@ def tile_combnethe_pa_kernel(
                 out=w2[v][:].bitcast(I32),
                 in_=given[v]["w2"].rearrange("g p n t -> p g (n t)").bitcast(I32),
             )
+
+        warm_in = keep.tile([P, 1], F32, name="warm_in")
+        warm_out = keep.tile([P, 1], F32, name="warm_out")
+        nc.vector.memset(warm_in[:], 0.0)
+        nc.scalar.activation(out=warm_out[:], in_=warm_in[:], func=ACT.Exp)
 
         x_codes = []
         x_planes = []
@@ -117,25 +120,25 @@ def tile_combnethe_pa_kernel(
                 in_=x_grouped[:].rearrange("p g k t -> p (g k t)"),
             )
 
-        h_codes = [[], []]
-        h_planes = [[], []]
-        for v in range(NETS):
-            for tt in range(TOKEN_TILES):
-                h_codes[v].append(keep.tile([P, H_GROUPS, P], U32, name="h_codes%d_%d" % (v, tt), align_bytes=64))
-                h_planes[v].append(keep.tile([P, H_GROUPS, P], U8, name="h_planes%d_%d" % (v, tt), align_bytes=64))
-
         rounds = [(0, [(tt, piece) for tt in range(TOKEN_TILES)]) for piece in range(H_GROUPS)]
         rounds += [
             (1, [(tt, piece) for piece in range(4 * half, 4 * half + 4)])
             for tt in range(TOKEN_TILES)
             for half in range(2)
         ]
+        BLOCKS = 4
         h_rows = {}
         h_grouped = {}
+        h_codes = {}
+        h_planes = {}
+        place = {}
+        for r in range(len(rounds)):
+            for i, (tt, piece) in enumerate(rounds[r][1]):
+                place[(rounds[r][0], tt, piece)] = (r, i)
 
         def first_layer(r):
             v, blocks = rounds[r]
-            for tt, piece in blocks:
+            for i, (tt, piece) in enumerate(blocks):
                 sums = sums_psum.tile([P, K_PASS], F32, name="sums")
                 for g in range(X_GROUPS):
                     nc.tensor.matmul_mx(
@@ -154,130 +157,171 @@ def tile_combnethe_pa_kernel(
                     in1=b1[v][:, K_PASS * piece : K_PASS * (piece + 1)].rearrange("k (p u e) -> k u p e", u=2, e=2),
                     op=ALU.add,
                 )
-                h_rows[(r, tt, piece)] = rows
+                h_rows[(r, i)] = rows
 
         def turn(r):
-            v, blocks = rounds[r]
-            for first in range(0, len(blocks), 2):
+            h_grouped[r] = round_ring.tile([P, BLOCKS, P, 4], BF16, name="grouped", align_bytes=64)
+            for first in range(0, BLOCKS, 2):
                 turned = turn_psum.tile([P, 4, P], F32, name="turned")
-                pair = blocks[first : first + 2]
-                for i, (tt, piece) in enumerate(pair):
-                    words = h_rows[(r, tt, piece)][:].bitcast(F32)
+                for i in range(2):
+                    words = h_rows[(r, first + i)][:].bitcast(F32)
                     for u in range(2):
                         nc.tensor.transpose(turned[:, 2 * i + u, :], words[:, P * u : P * (u + 1)], ident[:])
-                for i, (tt, piece) in enumerate(pair):
-                    grouped = ring.tile([P, P, 4], BF16, name="grouped", align_bytes=64)
+                for i in range(2):
                     nc.scalar.activation(
-                        out=grouped[:].rearrange("p k (u e) -> p k u e", u=2),
+                        out=h_grouped[r][:, first + i, :, :].rearrange("p k (u e) -> p k u e", u=2),
                         in_=turned[:, 2 * i : 2 * i + 2, :].bitcast(BF16).rearrange("p u (k e) -> p k u e", e=2),
                         func=ACT.Relu,
                     )
-                    h_grouped[(r, tt, piece)] = grouped
 
         def quantise(r):
-            v, blocks = rounds[r]
-            for tt, piece in blocks:
-                nc.vector.quantize_mx(
-                    out=h_codes[v][tt][:, piece, :].bitcast(FP8X4),
-                    scales=h_planes[v][tt][:, piece, :],
-                    in_=h_grouped[(r, tt, piece)][:].rearrange("p k t -> p (k t)"),
-                )
+            h_codes[r] = keep.tile([P, BLOCKS, P], U32, name="h_codes%d" % r, align_bytes=64)
+            h_planes[r] = keep.tile([P, BLOCKS, P], U8, name="h_planes%d" % r, align_bytes=64)
+            nc.vector.quantize_mx(
+                out=h_codes[r][:].rearrange("p i k -> p (i k)").bitcast(FP8X4),
+                scales=h_planes[r][:].rearrange("p i k -> p (i k)"),
+                in_=h_grouped[r][:].rearrange("p i k t -> p (i k t)"),
+            )
 
         neg_max = [keep.tile([P, TOKEN_TILES], F32, name="neg_max%d" % v) for v in range(NETS)]
         exp_sum = [keep.tile([P, TOKEN_TILES], F32, name="exp_sum%d" % v) for v in range(NETS)]
         inv_sum = [keep.tile([P, TOKEN_TILES], F32, name="inv_sum%d" % v) for v in range(NETS)]
+        logits_psum = {}
         exps = {}
-        x1 = {}
 
-        def head(v, token_tiles):
-            logits_psum = head_psum.tile([P, len(token_tiles), CLASSES], F32, name="logits_psum")
-            for i, tt in enumerate(token_tiles):
+        def second_layer(v, token_tiles):
+            logits_psum[v] = head_psum.tile([P, TOKEN_TILES, CLASSES], F32, name="logits_psum")
+            for tt in token_tiles:
                 for g in range(H_GROUPS):
+                    r, i = place[(v, tt, g)]
                     nc.tensor.matmul_mx(
-                        out=logits_psum[:, i, :],
-                        lhsT=h_codes[v][tt][:, g, :].bitcast(FP8X4),
-                        lhsT_scale=h_planes[v][tt][:, g, :],
+                        out=logits_psum[v][:, tt, :],
+                        lhsT=h_codes[r][:, i, :].bitcast(FP8X4),
+                        lhsT_scale=h_planes[r][:, i, :],
                         rhs=w2[v][:, g, :].bitcast(FP8X4),
                         rhs_scale=w2_planes[v][:, g, :],
                         start=(g == 0),
                         stop=(g == H_GROUPS - 1),
                     )
-            for i, tt in enumerate(token_tiles):
-                column = slice(tt, tt + 1)
-                logits = keep.tile([P, CLASSES], F32, name="logits%d_%d" % (v, tt))
-                nc.vector.tensor_tensor(out=logits[:], in0=logits_psum[:, i, :], in1=b2[v][:], op=ALU.add)
-                nc.vector.tensor_reduce(
-                    out=neg_max[v][:, column], in_=logits[:], axis=mybir.AxisListType.X, op=ALU.max, negate=True
-                )
-                exps[(v, tt)] = keep.tile([P, CLASSES], F32, name="exps%d_%d" % (v, tt))
-                nc.scalar.activation(
-                    out=exps[(v, tt)][:], in_=logits[:], func=ACT.Exp,
-                    bias=neg_max[v][:, column], accum_out=exp_sum[v][:, column],
-                )
-                nc.vector.reciprocal(out=inv_sum[v][:, column], in_=exp_sum[v][:, column])
 
-        def inverse(value, m, name):
-            a = keep.tile([P, TOKEN_TILES], F32, name="a_" + name)
-            b = keep.tile([P, TOKEN_TILES], F32, name="b_" + name)
-            b_plus_1 = keep.tile([P, TOKEN_TILES], F32, name="b_plus_1_" + name)
-            nc.gpsimd.tensor_scalar(out=a[:], in0=value[:], scalar1=-2.0 / m, scalar2=2.0, op0=ALU.mult, op1=ALU.add)
-            nc.gpsimd.tensor_scalar(out=b[:], in0=value[:], scalar1=-2.0 / m, scalar2=1.0, op0=ALU.mult, op1=ALU.add)
+        def exponentials(v, tt):
+            column = slice(tt, tt + 1)
+            logits = keep.tile([P, CLASSES], F32, name="logits%d_%d" % (v, tt))
+            nc.vector.tensor_tensor(out=logits[:], in0=logits_psum[v][:, tt, :], in1=b2[v][:], op=ALU.add)
+            nc.vector.tensor_reduce(
+                out=neg_max[v][:, column], in_=logits[:], axis=mybir.AxisListType.X, op=ALU.max, negate=True
+            )
+            exps[(v, tt)] = keep.tile([P, CLASSES], F32, name="exps%d_%d" % (v, tt))
+            nc.scalar.activation(
+                out=exps[(v, tt)][:], in_=logits[:], func=ACT.Exp,
+                bias=neg_max[v][:, column], accum_out=exp_sum[v][:, column],
+            )
+
+        power = {}
+        power_sum = [keep.tile([P, TOKEN_TILES], F32, name="power_sum%d" % i) for i in range(GATE_ROUNDS)]
+        factor = keep.tile([P, TOKEN_TILES], F32, name="factor")
+        factor_sq = keep.tile([P, TOKEN_TILES], F32, name="factor_sq")
+        row_sum = keep.tile([P, TOKEN_TILES], F32, name="row_sum")
+        a = keep.tile([P, TOKEN_TILES], F32, name="a")
+        b = keep.tile([P, TOKEN_TILES], F32, name="b")
+        b_plus_1 = keep.tile([P, TOKEN_TILES], F32, name="b_plus_1")
+        cond = keep.tile([P, TOKEN_TILES], F32, name="cond")
+        weight1 = keep.tile([P, TOKEN_TILES], F32, name="weight1")
+        weight2 = keep.tile([P, TOKEN_TILES], F32, name="weight2")
+        share1 = {}
+
+        def gate_powers(i):
+            for tt in range(TOKEN_TILES):
+                column = slice(tt, tt + 1)
+                power[(i, tt)] = keep.tile([P, CLASSES], F32, name="power%d_%d" % (i, tt))
+                if i == 0:
+                    nc.scalar.activation(
+                        out=power[(i, tt)][:], in_=exps[(0, tt)][:], func=ACT.Square,
+                        scale=inv_sum[0][:, column], accum_out=power_sum[i][:, column],
+                    )
+                else:
+                    nc.scalar.activation(
+                        out=power[(i, tt)][:], in_=power[(i - 1, tt)][:], func=ACT.Square,
+                        accum_out=power_sum[i][:, column],
+                    )
+
+        def gate_round(i):
+            m = (2.0 + TAU * TAU) if i == 0 else 2.0
+            tau_power = TAU ** (2 ** (i + 1))
+            nc.gpsimd.tensor_scalar(
+                out=row_sum[:], in0=power_sum[i][:], scalar1=1.0, scalar2=tau_power, op0=ALU.mult, op1=ALU.add
+            )
+            if i > 0:
+                nc.gpsimd.tensor_tensor(out=factor_sq[:], in0=factor[:], in1=factor[:], op=ALU.mult)
+                nc.gpsimd.tensor_tensor(out=row_sum[:], in0=row_sum[:], in1=factor_sq[:], op=ALU.mult)
+            nc.gpsimd.tensor_scalar(out=a[:], in0=row_sum[:], scalar1=-2.0 / m, scalar2=2.0, op0=ALU.mult, op1=ALU.add)
+            nc.gpsimd.tensor_scalar(out=b[:], in0=row_sum[:], scalar1=-2.0 / m, scalar2=1.0, op0=ALU.mult, op1=ALU.add)
             for step in range(INVERSE_STEPS):
                 nc.gpsimd.tensor_tensor(out=b[:], in0=b[:], in1=b[:], op=ALU.mult)
                 nc.gpsimd.tensor_scalar(out=b_plus_1[:], in0=b[:], scalar1=1.0, scalar2=1.0, op0=ALU.mult, op1=ALU.add)
                 nc.gpsimd.tensor_tensor(out=a[:], in0=a[:], in1=b_plus_1[:], op=ALU.mult)
-            nc.gpsimd.tensor_scalar(out=a[:], in0=a[:], scalar1=2.0 / m, scalar2=0.0, op0=ALU.mult, op1=ALU.add)
-            return a
+            nc.gpsimd.tensor_scalar(out=factor[:], in0=a[:], scalar1=2.0 / m, scalar2=0.0, op0=ALU.mult, op1=ALU.add)
+            if i > 0:
+                nc.gpsimd.tensor_tensor(out=factor[:], in0=factor[:], in1=factor_sq[:], op=ALU.mult)
 
-        def gate():
-            for tt in range(TOKEN_TILES):
-                x1[tt] = keep.tile([P, CLASSES], F32, name="x1_%d" % tt)
-                nc.scalar.activation(out=x1[tt][:], in_=exps[(0, tt)][:], func=ACT.Copy, scale=inv_sum[0][:, tt : tt + 1])
-            last = keep.tile([P, TOKEN_TILES], F32, name="last")
-            nc.gpsimd.memset(last[:], TAU)
-            res = [exps[(0, tt)] for tt in range(TOKEN_TILES)]
-            factor = inv_sum[0]
-            for i in range(GATE_ROUNDS):
-                row_sum = keep.tile([P, TOKEN_TILES], F32, name="row_sum%d" % i)
-                squared = []
-                for tt in range(TOKEN_TILES):
-                    squared.append(keep.tile([P, CLASSES], F32, name="squared%d_%d" % (i, tt)))
-                    nc.scalar.activation(
-                        out=squared[tt][:], in_=res[tt][:], func=ACT.Square,
-                        scale=factor[:, tt : tt + 1], accum_out=row_sum[:, tt : tt + 1],
-                    )
-                nc.gpsimd.tensor_tensor(out=last[:], in0=last[:], in1=last[:], op=ALU.mult)
-                nc.gpsimd.tensor_tensor(out=row_sum[:], in0=row_sum[:], in1=last[:], op=ALU.add)
-                factor = inverse(row_sum, (2.0 + TAU * TAU) if i == 0 else 2.0, "%d" % i)
-                nc.gpsimd.tensor_tensor(out=last[:], in0=last[:], in1=factor[:], op=ALU.mult)
-                res = squared
-            return last
-
-        def blend(tt, cond):
-            column = slice(tt, tt + 1)
-            diff = keep.tile([P, CLASSES], F32, name="diff%d" % tt)
-            nc.vector.scalar_tensor_tensor(
-                out=diff[:], in0=exps[(1, tt)][:], scalar=inv_sum[1][:, column], in1=x1[tt][:],
-                op0=ALU.mult, op1=ALU.subtract,
+        def gate_end():
+            nc.gpsimd.tensor_scalar(
+                out=cond[:], in0=factor[:], scalar1=TAU ** (2 ** GATE_ROUNDS), scalar2=0.0, op0=ALU.mult, op1=ALU.add
             )
+            nc.gpsimd.tensor_scalar(out=weight1[:], in0=cond[:], scalar1=-1.0, scalar2=1.0, op0=ALU.mult, op1=ALU.add)
+            nc.gpsimd.tensor_tensor(out=weight1[:], in0=weight1[:], in1=inv_sum[0][:], op=ALU.mult)
+            for tt in range(TOKEN_TILES):
+                share1[tt] = keep.tile([P, CLASSES], F32, name="share1_%d" % tt)
+                nc.gpsimd.tensor_scalar(
+                    out=share1[tt][:], in0=exps[(0, tt)][:], scalar1=weight1[:, tt : tt + 1], scalar2=0.0,
+                    op0=ALU.mult, op1=ALU.add,
+                )
+
+        def blend(tt):
+            column = slice(tt, tt + 1)
+            nc.vector.reciprocal(out=inv_sum[1][:, column], in_=exp_sum[1][:, column])
+            nc.vector.tensor_tensor(out=weight2[:, column], in0=inv_sum[1][:, column], in1=cond[:, column], op=ALU.mult)
             mixed = keep.tile([P, CLASSES], F32, name="mixed%d" % tt)
             nc.vector.scalar_tensor_tensor(
-                out=mixed[:], in0=diff[:], scalar=cond[:, column], in1=x1[tt][:], op0=ALU.mult, op1=ALU.add
+                out=mixed[:], in0=exps[(1, tt)][:], scalar=weight2[:, column], in1=share1[tt][:],
+                op0=ALU.mult, op1=ALU.add,
             )
             nc.sync.dma_start(out=out[P * tt : P * (tt + 1), :], in_=mixed[:])
 
-        cond = None
-        for r in range(len(rounds) + 2):
-            if r < len(rounds):
-                first_layer(r)
-            if 0 <= r - 1 < len(rounds):
-                turn(r - 1)
-            if 0 <= r - 2 < len(rounds):
-                quantise(r - 2)
-                v, blocks = rounds[r - 2]
-                if v == 0 and r - 2 == H_GROUPS - 1:
-                    head(0, list(range(TOKEN_TILES)))
-                    cond = gate()
-                if v == 1 and blocks[-1][1] == H_GROUPS - 1:
-                    head(1, [blocks[-1][0]])
-                    blend(blocks[-1][0], cond)
+        LAG = 3
+        LAST_O = H_GROUPS - 1
+        GATE_STEP = LAST_O + LAG + 1
+        BLEND_STEP = GATE_STEP + GATE_ROUNDS + 2
+        for s in range(len(rounds) + LAG + 2):
+            done = s - LAG
+            done_f = [tt for tt in range(TOKEN_TILES) if place[(1, tt, H_GROUPS - 1)][0] == done]
+            before_f = [tt for tt in range(TOKEN_TILES) if place[(1, tt, H_GROUPS - 1)][0] == done - 1]
+            if s < len(rounds):
+                first_layer(s)
+            if done == LAST_O:
+                second_layer(0, list(range(TOKEN_TILES)))
+            if done_f:
+                second_layer(1, done_f)
+            if 0 <= s - 1 < len(rounds):
+                turn(s - 1)
+            if 0 <= s - 2 < len(rounds):
+                quantise(s - 2)
+            if done == LAST_O:
+                for tt in range(TOKEN_TILES):
+                    exponentials(0, tt)
+            for tt in done_f:
+                exponentials(1, tt)
+            if s == GATE_STEP:
+                nc.vector.reciprocal(out=inv_sum[0][:], in_=exp_sum[0][:])
+            if 0 <= s - GATE_STEP < GATE_ROUNDS:
+                gate_powers(s - GATE_STEP)
+                gate_round(s - GATE_STEP)
+            if s == GATE_STEP + GATE_ROUNDS:
+                gate_end()
+            if s == BLEND_STEP:
+                for tt in range(TOKEN_TILES):
+                    if place[(1, tt, H_GROUPS - 1)][0] < done - 1:
+                        blend(tt)
+            if s >= BLEND_STEP:
+                for tt in before_f:
+                    blend(tt)

@@ -38,6 +38,7 @@ def tile_combnethe_pa_kernel(
         keep = ctx.enter_context(tc.tile_pool(name="keep", bufs=1))
         ring = ctx.enter_context(tc.tile_pool(name="ring", bufs=8))
         round_ring = ctx.enter_context(tc.tile_pool(name="round_ring", bufs=3))
+        copy_ring = ctx.enter_context(tc.tile_pool(name="copy_ring", bufs=3))
         ctx.enter_context(tc.manual_schedule())
         sums_psum = ctx.enter_context(tc.psum_pool(name="sums_psum", bufs=4))
         turn_psum = ctx.enter_context(tc.psum_pool(name="turn_psum", bufs=3))
@@ -109,9 +110,7 @@ def tile_combnethe_pa_kernel(
                         turned[:, 2 * g + u, :], x_words[:, 256 * g + u : 256 * (g + 1) : 2], ident[:]
                     )
             x_grouped = ring.tile([P, X_GROUPS, P, 4], BF16, name="x_grouped", align_bytes=64)
-            nc.vector.tensor_copy(
-                out=x_grouped[:].bitcast(F32), in_=turned[:].rearrange("p (g u) k -> p g k u", u=2)
-            )
+            nc.scalar.copy(out=x_grouped[:].bitcast(F32), in_=turned[:].rearrange("p (g u) k -> p g k u", u=2))
             x_codes.append(keep.tile([P, X_GROUPS, P], U32, name="x_codes%d" % tt, align_bytes=64))
             x_planes.append(keep.tile([P, X_GROUPS, P], U8, name="x_planes%d" % tt, align_bytes=64))
             nc.vector.quantize_mx(
@@ -127,6 +126,9 @@ def tile_combnethe_pa_kernel(
             for half in range(2)
         ]
         BLOCKS = 4
+        LAG = 3
+        GATE_STEP = H_GROUPS - 1 + LAG + 1
+        HELPED_ROUNDS = GATE_STEP - 1
         h_rows = {}
         h_grouped = {}
         h_codes = {}
@@ -151,12 +153,16 @@ def tile_combnethe_pa_kernel(
                         stop=(g == X_GROUPS - 1),
                     )
                 rows = ring.tile([P, K_PASS], BF16, name="rows")
-                nc.vector.tensor_tensor(
-                    out=rows[:].rearrange("k (u p e) -> k u p e", u=2, e=2),
-                    in0=sums[:].rearrange("k (p u e) -> k u p e", u=2, e=2),
-                    in1=b1[v][:, K_PASS * piece : K_PASS * (piece + 1)].rearrange("k (p u e) -> k u p e", u=2, e=2),
-                    op=ALU.add,
-                )
+                rows_view = rows[:].rearrange("k (u p e) -> k u p e", u=2, e=2)
+                sums_view = sums[:].rearrange("k (p u e) -> k u p e", u=2, e=2)
+                bias_view = b1[v][:, K_PASS * piece : K_PASS * (piece + 1)].rearrange("k (p u e) -> k u p e", u=2, e=2)
+                if i == 0 and r < HELPED_ROUNDS:
+                    sums_copy = copy_ring.tile([P, K_PASS], F32, name="sums_copy")
+                    copy_view = sums_copy[:].rearrange("k (u p e) -> k u p e", u=2, e=2)
+                    nc.scalar.copy(out=copy_view, in_=sums_view)
+                    nc.gpsimd.tensor_tensor(out=rows_view, in0=copy_view, in1=bias_view, op=ALU.add)
+                else:
+                    nc.vector.tensor_tensor(out=rows_view, in0=sums_view, in1=bias_view, op=ALU.add)
                 h_rows[(r, i)] = rows
 
         def turn(r):
@@ -187,7 +193,8 @@ def tile_combnethe_pa_kernel(
         exp_sum = [keep.tile([P, TOKEN_TILES], F32, name="exp_sum%d" % v) for v in range(NETS)]
         inv_sum = [keep.tile([P, TOKEN_TILES], F32, name="inv_sum%d" % v) for v in range(NETS)]
         logits_psum = {}
-        exps = {}
+        logits = [keep.tile([P, TOKEN_TILES, CLASSES], F32, name="logits%d" % v) for v in range(NETS)]
+        exps = [keep.tile([P, TOKEN_TILES, CLASSES], F32, name="exps%d" % v) for v in range(NETS)]
 
         def second_layer(v, token_tiles):
             logits_psum[v] = head_psum.tile([P, TOKEN_TILES, CLASSES], F32, name="logits_psum")
@@ -204,18 +211,20 @@ def tile_combnethe_pa_kernel(
                         stop=(g == H_GROUPS - 1),
                     )
 
-        def exponentials(v, tt):
-            column = slice(tt, tt + 1)
-            logits = keep.tile([P, CLASSES], F32, name="logits%d_%d" % (v, tt))
-            nc.vector.tensor_tensor(out=logits[:], in0=logits_psum[v][:, tt, :], in1=b2[v][:], op=ALU.add)
+        def exponentials(v, token_tiles):
+            some = slice(token_tiles[0], token_tiles[-1] + 1)
+            nc.vector.tensor_tensor(
+                out=logits[v][:, some, :], in0=logits_psum[v][:, some, :],
+                in1=b2[v][:].unsqueeze(1).to_broadcast([P, len(token_tiles), CLASSES]), op=ALU.add,
+            )
             nc.vector.tensor_reduce(
-                out=neg_max[v][:, column], in_=logits[:], axis=mybir.AxisListType.X, op=ALU.max, negate=True
+                out=neg_max[v][:, some], in_=logits[v][:, some, :], axis=mybir.AxisListType.X, op=ALU.max, negate=True
             )
-            exps[(v, tt)] = keep.tile([P, CLASSES], F32, name="exps%d_%d" % (v, tt))
-            nc.scalar.activation(
-                out=exps[(v, tt)][:], in_=logits[:], func=ACT.Exp,
-                bias=neg_max[v][:, column], accum_out=exp_sum[v][:, column],
-            )
+            for tt in token_tiles:
+                nc.scalar.activation(
+                    out=exps[v][:, tt, :], in_=logits[v][:, tt, :], func=ACT.Exp,
+                    bias=neg_max[v][:, tt : tt + 1], accum_out=exp_sum[v][:, tt : tt + 1],
+                )
 
         power = {}
         power_sum = [keep.tile([P, TOKEN_TILES], F32, name="power_sum%d" % i) for i in range(GATE_ROUNDS)]
@@ -236,7 +245,7 @@ def tile_combnethe_pa_kernel(
                 power[(i, tt)] = keep.tile([P, CLASSES], F32, name="power%d_%d" % (i, tt))
                 if i == 0:
                     nc.scalar.activation(
-                        out=power[(i, tt)][:], in_=exps[(0, tt)][:], func=ACT.Square,
+                        out=power[(i, tt)][:], in_=exps[0][:, tt, :], func=ACT.Square,
                         scale=inv_sum[0][:, column], accum_out=power_sum[i][:, column],
                     )
                 else:
@@ -273,7 +282,7 @@ def tile_combnethe_pa_kernel(
             for tt in range(TOKEN_TILES):
                 share1[tt] = keep.tile([P, CLASSES], F32, name="share1_%d" % tt)
                 nc.gpsimd.tensor_scalar(
-                    out=share1[tt][:], in0=exps[(0, tt)][:], scalar1=weight1[:, tt : tt + 1], scalar2=0.0,
+                    out=share1[tt][:], in0=exps[0][:, tt, :], scalar1=weight1[:, tt : tt + 1], scalar2=0.0,
                     op0=ALU.mult, op1=ALU.add,
                 )
 
@@ -283,34 +292,29 @@ def tile_combnethe_pa_kernel(
             nc.vector.tensor_tensor(out=weight2[:, column], in0=inv_sum[1][:, column], in1=cond[:, column], op=ALU.mult)
             mixed = keep.tile([P, CLASSES], F32, name="mixed%d" % tt)
             nc.vector.scalar_tensor_tensor(
-                out=mixed[:], in0=exps[(1, tt)][:], scalar=weight2[:, column], in1=share1[tt][:],
+                out=mixed[:], in0=exps[1][:, tt, :], scalar=weight2[:, column], in1=share1[tt][:],
                 op0=ALU.mult, op1=ALU.add,
             )
             nc.sync.dma_start(out=out[P * tt : P * (tt + 1), :], in_=mixed[:])
 
-        LAG = 3
-        LAST_O = H_GROUPS - 1
-        GATE_STEP = LAST_O + LAG + 1
         BLEND_STEP = GATE_STEP + GATE_ROUNDS + 2
+        last_round = [place[(1, tt, H_GROUPS - 1)][0] for tt in range(TOKEN_TILES)]
         for s in range(len(rounds) + LAG + 2):
-            done = s - LAG
-            done_f = [tt for tt in range(TOKEN_TILES) if place[(1, tt, H_GROUPS - 1)][0] == done]
-            before_f = [tt for tt in range(TOKEN_TILES) if place[(1, tt, H_GROUPS - 1)][0] == done - 1]
+            finished = [tt for tt in range(TOKEN_TILES) if last_round[tt] + LAG == s]
             if s < len(rounds):
                 first_layer(s)
-            if done == LAST_O:
-                second_layer(0, list(range(TOKEN_TILES)))
-            if done_f:
-                second_layer(1, done_f)
             if 0 <= s - 1 < len(rounds):
                 turn(s - 1)
+            if s == GATE_STEP - 1:
+                second_layer(0, list(range(TOKEN_TILES)))
+            if finished:
+                second_layer(1, finished)
             if 0 <= s - 2 < len(rounds):
                 quantise(s - 2)
-            if done == LAST_O:
-                for tt in range(TOKEN_TILES):
-                    exponentials(0, tt)
-            for tt in done_f:
-                exponentials(1, tt)
+            if s == GATE_STEP - 1:
+                exponentials(0, list(range(TOKEN_TILES)))
+            if finished:
+                exponentials(1, finished)
             if s == GATE_STEP:
                 nc.vector.reciprocal(out=inv_sum[0][:], in_=exp_sum[0][:])
             if 0 <= s - GATE_STEP < GATE_ROUNDS:
@@ -318,10 +322,6 @@ def tile_combnethe_pa_kernel(
                 gate_round(s - GATE_STEP)
             if s == GATE_STEP + GATE_ROUNDS:
                 gate_end()
-            if s == BLEND_STEP:
-                for tt in range(TOKEN_TILES):
-                    if place[(1, tt, H_GROUPS - 1)][0] < done - 1:
-                        blend(tt)
-            if s >= BLEND_STEP:
-                for tt in before_f:
+            for tt in range(TOKEN_TILES):
+                if s == max(last_round[tt] + LAG + 1, BLEND_STEP):
                     blend(tt)

@@ -18,6 +18,8 @@ TOKENS, D_IN, D_H, CLASSES = 512, 1024, 4096, 128
 TOKEN_TILES = TOKENS // P
 X_GROUPS = D_IN // K_PASS
 H_GROUPS = D_H // K_PASS
+BLOCKS = K_PASS // P
+W1_PIECE = 1024
 TAU, GATE_ROUNDS, INVERSE_STEPS = 0.5, 3, 3
 
 FLOPS = 2 * (2 * TOKENS * D_IN * D_H + 2 * TOKENS * D_H * CLASSES)
@@ -36,13 +38,11 @@ def tile_combnethe_pa_kernel(
 
     with ExitStack() as ctx:
         keep = ctx.enter_context(tc.tile_pool(name="keep", bufs=1))
-        ring = ctx.enter_context(tc.tile_pool(name="ring", bufs=8))
-        round_ring = ctx.enter_context(tc.tile_pool(name="round_ring", bufs=3))
-        copy_ring = ctx.enter_context(tc.tile_pool(name="copy_ring", bufs=3))
-        ctx.enter_context(tc.manual_schedule())
+        block_ring = ctx.enter_context(tc.tile_pool(name="block_ring", bufs=4 * BLOCKS))
+        group_ring = ctx.enter_context(tc.tile_pool(name="group_ring", bufs=4))
         sums_psum = ctx.enter_context(tc.psum_pool(name="sums_psum", bufs=4))
-        turn_psum = ctx.enter_context(tc.psum_pool(name="turn_psum", bufs=3))
         head_psum = ctx.enter_context(tc.psum_pool(name="head_psum", bufs=1))
+        ctx.enter_context(tc.manual_schedule())
 
         x_rows = []
         x_view = x.rearrange("(t p) k -> p t k", p=P)
@@ -50,6 +50,8 @@ def tile_combnethe_pa_kernel(
             x_rows.append(keep.tile([P, 2, D_IN], BF16, name="x_rows%d" % half))
             nc.scalar.dma_start(out=x_rows[half][:], in_=x_view[:, 2 * half : 2 * half + 2, :])
 
+        b1_rows = keep.tile([P, P], BF16, name="b1_rows")
+        nc.vector.memset(b1_rows[:], 0.0)
         w1_planes = []
         w2_planes = []
         for v in range(NETS):
@@ -63,164 +65,158 @@ def tile_combnethe_pa_kernel(
 
         w1 = [[], []]
         w2 = []
-        b1 = []
         b2 = []
+        for v in range(NETS):
+            rows_of_net = D_H // P
+            nc.gpsimd.dma_start(
+                out=b1_rows[rows_of_net * v : rows_of_net * (v + 1), :],
+                in_=given[v]["b1"].rearrange("(j m) -> j m", m=P),
+            )
         for v in range(NETS):
             for quadrant in range(4):
                 nc.sync.dma_start(
                     out=w1_planes[v][32 * quadrant : 32 * quadrant + 4 * X_GROUPS, :].bitcast(I32),
                     in_=given[v]["s1"][:, 4 * quadrant : 4 * quadrant + 4, :].bitcast(I32),
                 )
-            b1.append(keep.tile([P, D_H], BF16, name="b1_%d" % v))
-            bias_queue = nc.scalar if v == 0 else nc.sync
-            bias_queue.dma_start(out=b1[v][:], in_=given[v]["b1"].partition_broadcast(P))
             w1_bytes = given[v]["w1"].rearrange("g p n t -> p g (n t)")
-            for piece in range(H_GROUPS):
-                w1[v].append(keep.tile([P, X_GROUPS, K_PASS], U32, name="w1_%d_%d" % (v, piece), align_bytes=64))
-                nc.sync.dma_start(
-                    out=w1[v][piece][:].bitcast(I32),
-                    in_=w1_bytes[:, :, 4 * K_PASS * piece : 4 * K_PASS * (piece + 1)].bitcast(I32),
-                )
-            b2.append(keep.tile([P, CLASSES], BF16, name="b2_%d" % v))
-            nc.sync.dma_start(out=b2[v][:], in_=given[v]["b2"].partition_broadcast(P))
+            for piece in range(D_H // W1_PIECE):
+                w1[v].append(keep.tile([P, X_GROUPS, W1_PIECE], U32, name="w1_%d_%d" % (v, piece), align_bytes=64))
+                piece_bytes = w1_bytes[:, :, 4 * W1_PIECE * piece : 4 * W1_PIECE * (piece + 1)]
+                if v == 0:
+                    nc.sync.dma_start(out=w1[v][piece][:].bitcast(I32), in_=piece_bytes.bitcast(I32))
+                else:
+                    nc.gpsimd.dma_start(out=w1[v][piece][:].bitcast(F32), in_=piece_bytes.bitcast(F32))
             for quadrant in range(4):
                 nc.sync.dma_start(
                     out=w2_planes[v][32 * quadrant : 32 * quadrant + 4, :, :].bitcast(I32),
                     in_=given[v]["s2"][:, 4 * quadrant : 4 * quadrant + 4, :].rearrange("g r c -> r g c").bitcast(I32),
                 )
             w2.append(keep.tile([P, H_GROUPS, CLASSES], U32, name="w2_%d" % v, align_bytes=64))
-            nc.sync.dma_start(
-                out=w2[v][:].bitcast(I32),
-                in_=given[v]["w2"].rearrange("g p n t -> p g (n t)").bitcast(I32),
+            nc.gpsimd.dma_start(
+                out=w2[v][:].bitcast(F32),
+                in_=given[v]["w2"].rearrange("g p n t -> p g (n t)").bitcast(F32),
             )
+            b2.append(keep.tile([P, CLASSES], BF16, name="b2_%d" % v))
+            nc.gpsimd.dma_start(out=b2[v][:], in_=given[v]["b2"].partition_broadcast(P))
 
         warm_in = keep.tile([P, 1], F32, name="warm_in")
         warm_out = keep.tile([P, 1], F32, name="warm_out")
         nc.vector.memset(warm_in[:], 0.0)
         nc.scalar.activation(out=warm_out[:], in_=warm_in[:], func=ACT.Exp)
 
-        x_codes = []
-        x_planes = []
+        b1_wide = keep.tile([P, P], F32, name="b1_wide")
+        nc.vector.tensor_copy(out=b1_wide[:], in_=b1_rows[:])
+        b1_turned = sums_psum.tile([P, K_PASS], F32, name="sums")
+        nc.tensor.transpose(b1_turned[:, 0:P], b1_wide[:], ident[:])
+        b1_cols = keep.tile([P, P], F32, name="b1_cols")
+        nc.vector.tensor_copy(out=b1_cols[:], in_=b1_turned[:, 0:P])
+
+        x_grouped = keep.tile([P, X_GROUPS, TOKENS, 4], BF16, name="x_grouped", align_bytes=64)
+        x_codes = keep.tile([P, X_GROUPS, TOKENS], U32, name="x_codes", align_bytes=64)
+        x_planes = keep.tile([P, X_GROUPS, TOKENS], U8, name="x_planes", align_bytes=64)
         for tt in range(TOKEN_TILES):
             x_words = x_rows[tt // 2][:, tt % 2, :].bitcast(F32)
-            turned = turn_psum.tile([P, 2 * X_GROUPS, P], F32, name="turned")
+            x_turned = sums_psum.tile([P, K_PASS], F32, name="sums")
             for g in range(X_GROUPS):
                 for u in range(2):
                     nc.tensor.transpose(
-                        turned[:, 2 * g + u, :], x_words[:, 256 * g + u : 256 * (g + 1) : 2], ident[:]
+                        x_turned[:, P * (2 * g + u) : P * (2 * g + u + 1)],
+                        x_words[:, 256 * g + u : 256 * (g + 1) : 2],
+                        ident[:],
                     )
-            x_grouped = ring.tile([P, X_GROUPS, P, 4], BF16, name="x_grouped", align_bytes=64)
-            nc.scalar.copy(out=x_grouped[:].bitcast(F32), in_=turned[:].rearrange("p (g u) k -> p g k u", u=2))
-            x_codes.append(keep.tile([P, X_GROUPS, P], U32, name="x_codes%d" % tt, align_bytes=64))
-            x_planes.append(keep.tile([P, X_GROUPS, P], U8, name="x_planes%d" % tt, align_bytes=64))
+            nc.scalar.copy(
+                out=x_grouped[:, :, P * tt : P * (tt + 1), :].bitcast(F32),
+                in_=x_turned[:].rearrange("p (g u k) -> p g k u", g=X_GROUPS, u=2),
+            )
+        for g in range(X_GROUPS):
             nc.vector.quantize_mx(
-                out=x_codes[tt][:].rearrange("p g k -> p (g k)").bitcast(FP8X4),
-                scales=x_planes[tt][:].rearrange("p g k -> p (g k)"),
-                in_=x_grouped[:].rearrange("p g k t -> p (g k t)"),
+                out=x_codes[:, g, :].bitcast(FP8X4),
+                scales=x_planes[:, g, :],
+                in_=x_grouped[:, g, :, :].rearrange("p k t -> p (k t)"),
             )
 
-        rounds = [(0, [(tt, piece) for tt in range(TOKEN_TILES)]) for piece in range(H_GROUPS)]
-        rounds += [
-            (1, [(tt, piece) for piece in range(4 * half, 4 * half + 4)])
-            for tt in range(TOKEN_TILES)
-            for half in range(2)
-        ]
-        BLOCKS = 4
-        LAG = 3
-        GATE_STEP = H_GROUPS - 1 + LAG + 1
-        HELPED_ROUNDS = GATE_STEP - 1
-        h_rows = {}
+        groups = [(v, g2) for v in range(NETS) for g2 in range(H_GROUPS)]
+        h_blocks = {}
+        h_lined = {}
         h_grouped = {}
         h_codes = {}
         h_planes = {}
-        place = {}
-        for r in range(len(rounds)):
-            for i, (tt, piece) in enumerate(rounds[r][1]):
-                place[(rounds[r][0], tt, piece)] = (r, i)
 
-        def first_layer(r):
-            v, blocks = rounds[r]
-            for i, (tt, piece) in enumerate(blocks):
-                sums = sums_psum.tile([P, K_PASS], F32, name="sums")
+        def first_layer(s):
+            v, g2 = groups[s]
+            h_lined[s] = group_ring.tile([P, 4, TOKENS], BF16, name="lined")
+            for jj in range(BLOCKS):
+                j = BLOCKS * g2 + jj
+                column = P * j
+                piece, inside = column // W1_PIECE, column % W1_PIECE
+                sums = sums_psum.tile([P, TOKENS], F32, name="sums")
                 for g in range(X_GROUPS):
                     nc.tensor.matmul_mx(
                         out=sums[:],
-                        lhsT=x_codes[tt][:, g, :].bitcast(FP8X4),
-                        lhsT_scale=x_planes[tt][:, g, :],
-                        rhs=w1[v][piece][:, g, :].bitcast(FP8X4),
-                        rhs_scale=w1_planes[v][4 * g : P, K_PASS * piece : K_PASS * (piece + 1)],
+                        lhsT=w1[v][piece][:, g, inside : inside + P].bitcast(FP8X4),
+                        lhsT_scale=w1_planes[v][4 * g : P, column : column + P],
+                        rhs=x_codes[:, g, :].bitcast(FP8X4),
+                        rhs_scale=x_planes[:, g, :],
                         start=(g == 0),
                         stop=(g == X_GROUPS - 1),
                     )
-                rows = ring.tile([P, K_PASS], BF16, name="rows")
-                rows_view = rows[:].rearrange("k (u p e) -> k u p e", u=2, e=2)
-                sums_view = sums[:].rearrange("k (p u e) -> k u p e", u=2, e=2)
-                bias_view = b1[v][:, K_PASS * piece : K_PASS * (piece + 1)].rearrange("k (p u e) -> k u p e", u=2, e=2)
-                if i == 0 and r < HELPED_ROUNDS:
-                    sums_copy = copy_ring.tile([P, K_PASS], F32, name="sums_copy")
-                    copy_view = sums_copy[:].rearrange("k (u p e) -> k u p e", u=2, e=2)
-                    nc.scalar.copy(out=copy_view, in_=sums_view)
-                    nc.gpsimd.tensor_tensor(out=rows_view, in0=copy_view, in1=bias_view, op=ALU.add)
-                else:
-                    nc.vector.tensor_tensor(out=rows_view, in0=sums_view, in1=bias_view, op=ALU.add)
-                h_rows[(r, i)] = rows
-
-        def turn(r):
-            h_grouped[r] = round_ring.tile([P, BLOCKS, P, 4], BF16, name="grouped", align_bytes=64)
-            for first in range(0, BLOCKS, 2):
-                turned = turn_psum.tile([P, 4, P], F32, name="turned")
-                for i in range(2):
-                    words = h_rows[(r, first + i)][:].bitcast(F32)
-                    for u in range(2):
-                        nc.tensor.transpose(turned[:, 2 * i + u, :], words[:, P * u : P * (u + 1)], ident[:])
-                for i in range(2):
-                    nc.scalar.activation(
-                        out=h_grouped[r][:, first + i, :, :].rearrange("p k (u e) -> p k u e", u=2),
-                        in_=turned[:, 2 * i : 2 * i + 2, :].bitcast(BF16).rearrange("p u (k e) -> p k u e", e=2),
-                        func=ACT.Relu,
+                bias = b1_cols[:, (D_H // P) * v + j : (D_H // P) * v + j + 1]
+                block = block_ring.tile([P, TOKENS], BF16, name="block")
+                if jj == 0 and s % 2 == 0:
+                    nc.vector.tensor_scalar(
+                        out=block[:], in0=sums[:], scalar1=bias, scalar2=0.0, op0=ALU.add, op1=ALU.max
                     )
+                else:
+                    nc.scalar.activation(out=block[:], in_=sums[:], func=ACT.Relu, bias=bias)
+                queue = nc.sync if jj < BLOCKS // 2 else nc.scalar
+                queue.dma_start(out=h_lined[s][32 * jj : 32 * (jj + 1), :, :], in_=block[:])
+                h_blocks[(s, jj)] = block
 
-        def quantise(r):
-            h_codes[r] = keep.tile([P, BLOCKS, P], U32, name="h_codes%d" % r, align_bytes=64)
-            h_planes[r] = keep.tile([P, BLOCKS, P], U8, name="h_planes%d" % r, align_bytes=64)
+        def regroup(s):
+            h_grouped[s] = group_ring.tile([P, TOKENS, 4], BF16, name="grouped", align_bytes=64)
+            nc.vector.tensor_copy(
+                out=h_grouped[s][:].rearrange("p (c i) t -> p c t i", i=4),
+                in_=h_lined[s][:].rearrange("p t (c i) -> p c t i", i=4),
+            )
+
+        def quantise(s):
+            h_codes[s] = keep.tile([P, TOKENS], U32, name="h_codes%d" % s, align_bytes=64)
+            h_planes[s] = keep.tile([P, TOKENS], U8, name="h_planes%d" % s, align_bytes=64)
             nc.vector.quantize_mx(
-                out=h_codes[r][:].rearrange("p i k -> p (i k)").bitcast(FP8X4),
-                scales=h_planes[r][:].rearrange("p i k -> p (i k)"),
-                in_=h_grouped[r][:].rearrange("p i k t -> p (i k t)"),
+                out=h_codes[s][:].bitcast(FP8X4),
+                scales=h_planes[s][:],
+                in_=h_grouped[s][:].rearrange("p k t -> p (k t)"),
             )
 
         neg_max = [keep.tile([P, TOKEN_TILES], F32, name="neg_max%d" % v) for v in range(NETS)]
         exp_sum = [keep.tile([P, TOKEN_TILES], F32, name="exp_sum%d" % v) for v in range(NETS)]
         inv_sum = [keep.tile([P, TOKEN_TILES], F32, name="inv_sum%d" % v) for v in range(NETS)]
-        logits_psum = {}
         logits = [keep.tile([P, TOKEN_TILES, CLASSES], F32, name="logits%d" % v) for v in range(NETS)]
         exps = [keep.tile([P, TOKEN_TILES, CLASSES], F32, name="exps%d" % v) for v in range(NETS)]
+        logits_psum = {}
 
-        def second_layer(v, token_tiles):
-            logits_psum[v] = head_psum.tile([P, TOKEN_TILES, CLASSES], F32, name="logits_psum")
-            for tt in token_tiles:
-                for g in range(H_GROUPS):
-                    r, i = place[(v, tt, g)]
-                    nc.tensor.matmul_mx(
-                        out=logits_psum[v][:, tt, :],
-                        lhsT=h_codes[r][:, i, :].bitcast(FP8X4),
-                        lhsT_scale=h_planes[r][:, i, :],
-                        rhs=w2[v][:, g, :].bitcast(FP8X4),
-                        rhs_scale=w2_planes[v][:, g, :],
-                        start=(g == 0),
-                        stop=(g == H_GROUPS - 1),
-                    )
+        def second_layer(s):
+            v, g2 = groups[s]
+            for tt in range(TOKEN_TILES):
+                if g2 == 0:
+                    logits_psum[(v, tt)] = head_psum.tile([P, CLASSES], F32, name="logits_psum%d" % tt)
+                nc.tensor.matmul_mx(
+                    out=logits_psum[(v, tt)][:],
+                    lhsT=h_codes[s][:, P * tt : P * (tt + 1)].bitcast(FP8X4),
+                    lhsT_scale=h_planes[s][:, P * tt : P * (tt + 1)],
+                    rhs=w2[v][:, g2, :].bitcast(FP8X4),
+                    rhs_scale=w2_planes[v][:, g2, :],
+                    start=(g2 == 0),
+                    stop=(g2 == H_GROUPS - 1),
+                )
 
-        def exponentials(v, token_tiles):
-            some = slice(token_tiles[0], token_tiles[-1] + 1)
-            nc.vector.tensor_tensor(
-                out=logits[v][:, some, :], in0=logits_psum[v][:, some, :],
-                in1=b2[v][:].unsqueeze(1).to_broadcast([P, len(token_tiles), CLASSES]), op=ALU.add,
-            )
+        def exponentials(v):
+            for tt in range(TOKEN_TILES):
+                nc.vector.tensor_tensor(out=logits[v][:, tt, :], in0=logits_psum[(v, tt)][:], in1=b2[v][:], op=ALU.add)
             nc.vector.tensor_reduce(
-                out=neg_max[v][:, some], in_=logits[v][:, some, :], axis=mybir.AxisListType.X, op=ALU.max, negate=True
+                out=neg_max[v][:], in_=logits[v][:], axis=mybir.AxisListType.X, op=ALU.max, negate=True
             )
-            for tt in token_tiles:
+            for tt in range(TOKEN_TILES):
                 nc.scalar.activation(
                     out=exps[v][:, tt, :], in_=logits[v][:, tt, :], func=ACT.Exp,
                     bias=neg_max[v][:, tt : tt + 1], accum_out=exp_sum[v][:, tt : tt + 1],
@@ -297,24 +293,21 @@ def tile_combnethe_pa_kernel(
             )
             nc.sync.dma_start(out=out[P * tt : P * (tt + 1), :], in_=mixed[:])
 
-        BLEND_STEP = GATE_STEP + GATE_ROUNDS + 2
-        last_round = [place[(1, tt, H_GROUPS - 1)][0] for tt in range(TOKEN_TILES)]
-        for s in range(len(rounds) + LAG + 2):
-            finished = [tt for tt in range(TOKEN_TILES) if last_round[tt] + LAG == s]
-            if s < len(rounds):
+        REGROUP_LAG, QUANTISE_LAG, SECOND_LAG = 3, 4, 5
+        HEAD_O = H_GROUPS - 1 + SECOND_LAG
+        HEAD_F = len(groups) - 1 + SECOND_LAG
+        GATE_STEP = HEAD_O + 1
+        for s in range(HEAD_F + 1):
+            if s < len(groups):
                 first_layer(s)
-            if 0 <= s - 1 < len(rounds):
-                turn(s - 1)
-            if s == GATE_STEP - 1:
-                second_layer(0, list(range(TOKEN_TILES)))
-            if finished:
-                second_layer(1, finished)
-            if 0 <= s - 2 < len(rounds):
-                quantise(s - 2)
-            if s == GATE_STEP - 1:
-                exponentials(0, list(range(TOKEN_TILES)))
-            if finished:
-                exponentials(1, finished)
+            if 0 <= s - SECOND_LAG:
+                second_layer(s - SECOND_LAG)
+            if 0 <= s - REGROUP_LAG < len(groups):
+                regroup(s - REGROUP_LAG)
+            if 0 <= s - QUANTISE_LAG < len(groups):
+                quantise(s - QUANTISE_LAG)
+            if s == HEAD_O:
+                exponentials(0)
             if s == GATE_STEP:
                 nc.vector.reciprocal(out=inv_sum[0][:], in_=exp_sum[0][:])
             if 0 <= s - GATE_STEP < GATE_ROUNDS:
@@ -322,6 +315,6 @@ def tile_combnethe_pa_kernel(
                 gate_round(s - GATE_STEP)
             if s == GATE_STEP + GATE_ROUNDS:
                 gate_end()
-            for tt in range(TOKEN_TILES):
-                if s == max(last_round[tt] + LAG + 1, BLEND_STEP):
-                    blend(tt)
+        exponentials(1)
+        for tt in range(TOKEN_TILES):
+            blend(tt)

@@ -40,76 +40,98 @@ def tile_combnethe_pa_kernel(
         keep = ctx.enter_context(tc.tile_pool(name="keep", bufs=1))
         block_ring = ctx.enter_context(tc.tile_pool(name="block_ring", bufs=4 * BLOCKS))
         group_ring = ctx.enter_context(tc.tile_pool(name="group_ring", bufs=4))
+        raw_ring = ctx.enter_context(tc.tile_pool(name="raw_ring", bufs=D_H // W1_PIECE))
         sums_psum = ctx.enter_context(tc.psum_pool(name="sums_psum", bufs=4))
         head_psum = ctx.enter_context(tc.psum_pool(name="head_psum", bufs=1))
         ctx.enter_context(tc.manual_schedule())
 
+        b1_rows = keep.tile([P, K_PASS], BF16, name="b1_rows")
+        nc.vector.memset(b1_rows[:], 0.0)
+        for v in range(NETS):
+            nc.scalar.dma_start(
+                out=b1_rows[H_GROUPS * v : H_GROUPS * (v + 1), :],
+                in_=given[v]["b1"].rearrange("(g n) -> g n", n=K_PASS),
+            )
         x_rows = []
         x_view = x.rearrange("(t p) k -> p t k", p=P)
         for half in range(2):
             x_rows.append(keep.tile([P, 2, D_IN], BF16, name="x_rows%d" % half))
             nc.scalar.dma_start(out=x_rows[half][:], in_=x_view[:, 2 * half : 2 * half + 2, :])
 
-        b1_rows = keep.tile([P, P], BF16, name="b1_rows")
-        nc.vector.memset(b1_rows[:], 0.0)
-        w1_planes = []
+        w1_planes_raw = []
         w2_planes = []
         for v in range(NETS):
-            w1_planes.append(keep.tile([P, D_H], U8, name="w1_planes%d" % v, align_bytes=64))
+            w1_planes_raw.append(keep.tile([P, D_H], U8, name="w1_planes_raw%d" % v))
             w2_planes.append(keep.tile([P, H_GROUPS, CLASSES], U8, name="w2_planes%d" % v, align_bytes=64))
-            nc.vector.memset(w1_planes[v][:].bitcast(I32), 0)
+            nc.vector.memset(w1_planes_raw[v][:].bitcast(I32), 0)
             nc.vector.memset(w2_planes[v][:].rearrange("p g c -> p (g c)").bitcast(I32), 0)
 
         ident = keep.tile([P, P], F32, name="ident")
         make_identity(nc, ident[:])
 
-        w1 = [[], []]
+        w1_raw = {}
+
+        def load_w1(v, piece):
+            w1_raw[(v, piece)] = raw_ring.tile([P, X_GROUPS, W1_PIECE], U32, name="w1_raw")
+            w1_bytes = given[v]["w1"].rearrange("g p n t -> p g (n t)")
+            nc.sync.dma_start(
+                out=w1_raw[(v, piece)][:].bitcast(I32),
+                in_=w1_bytes[:, :, 4 * W1_PIECE * piece : 4 * W1_PIECE * (piece + 1)].bitcast(I32),
+            )
+
         w2 = []
         b2 = []
         for v in range(NETS):
-            rows_of_net = D_H // P
-            nc.gpsimd.dma_start(
-                out=b1_rows[rows_of_net * v : rows_of_net * (v + 1), :],
-                in_=given[v]["b1"].rearrange("(j m) -> j m", m=P),
-            )
-        for v in range(NETS):
             for quadrant in range(4):
                 nc.sync.dma_start(
-                    out=w1_planes[v][32 * quadrant : 32 * quadrant + 4 * X_GROUPS, :].bitcast(I32),
+                    out=w1_planes_raw[v][32 * quadrant : 32 * quadrant + 4 * X_GROUPS, :].bitcast(I32),
                     in_=given[v]["s1"][:, 4 * quadrant : 4 * quadrant + 4, :].bitcast(I32),
                 )
-            w1_bytes = given[v]["w1"].rearrange("g p n t -> p g (n t)")
-            for piece in range(D_H // W1_PIECE):
-                w1[v].append(keep.tile([P, X_GROUPS, W1_PIECE], U32, name="w1_%d_%d" % (v, piece), align_bytes=64))
-                piece_bytes = w1_bytes[:, :, 4 * W1_PIECE * piece : 4 * W1_PIECE * (piece + 1)]
-                if v == 0:
-                    nc.sync.dma_start(out=w1[v][piece][:].bitcast(I32), in_=piece_bytes.bitcast(I32))
-                else:
-                    nc.gpsimd.dma_start(out=w1[v][piece][:].bitcast(F32), in_=piece_bytes.bitcast(F32))
+            if v == 0:
+                for piece in range(D_H // W1_PIECE):
+                    load_w1(v, piece)
+        for v in range(NETS):
             for quadrant in range(4):
                 nc.sync.dma_start(
                     out=w2_planes[v][32 * quadrant : 32 * quadrant + 4, :, :].bitcast(I32),
                     in_=given[v]["s2"][:, 4 * quadrant : 4 * quadrant + 4, :].rearrange("g r c -> r g c").bitcast(I32),
                 )
             w2.append(keep.tile([P, H_GROUPS, CLASSES], U32, name="w2_%d" % v, align_bytes=64))
-            nc.gpsimd.dma_start(
-                out=w2[v][:].bitcast(F32),
-                in_=given[v]["w2"].rearrange("g p n t -> p g (n t)").bitcast(F32),
-            )
+            for w in range(2):
+                for jj in range(BLOCKS):
+                    nc.sync.dma_start(
+                        out=w2[v][4 * w + jj : P : 8, :, :].bitcast(I32),
+                        in_=given[v]["w2"][:, 2 * jj + w : P : 8, :, :].rearrange("g i c t -> i g (c t)").bitcast(I32),
+                    )
             b2.append(keep.tile([P, CLASSES], BF16, name="b2_%d" % v))
-            nc.gpsimd.dma_start(out=b2[v][:], in_=given[v]["b2"].partition_broadcast(P))
+            nc.scalar.dma_start(out=b2[v][:], in_=given[v]["b2"].partition_broadcast(P))
 
         warm_in = keep.tile([P, 1], F32, name="warm_in")
         warm_out = keep.tile([P, 1], F32, name="warm_out")
         nc.vector.memset(warm_in[:], 0.0)
         nc.scalar.activation(out=warm_out[:], in_=warm_in[:], func=ACT.Exp)
 
-        b1_wide = keep.tile([P, P], F32, name="b1_wide")
-        nc.vector.tensor_copy(out=b1_wide[:], in_=b1_rows[:])
+        RUN = 8
+        RUNS = P // RUN
+        w1_planes = [keep.tile([P, D_H], U8, name="w1_planes%d" % v, align_bytes=64) for v in range(NETS)]
+
+        def sort_planes(v):
+            nc.vector.tensor_copy(
+                out=w1_planes[v][:].bitcast(I32).rearrange("p (G j i r) -> p G j i r", j=BLOCKS, i=RUNS, r=RUN // 4),
+                in_=w1_planes_raw[v][:].bitcast(I32).rearrange("p (G i j r) -> p G j i r", j=BLOCKS, i=RUNS, r=RUN // 4),
+            )
+
+        b1_wide = keep.tile([P, K_PASS], F32, name="b1_wide")
+        nc.vector.tensor_copy(
+            out=b1_wide[:].rearrange("q (j i r) -> q j i r", j=BLOCKS, r=RUN),
+            in_=b1_rows[:].rearrange("q (i j r) -> q j i r", j=BLOCKS, r=RUN),
+        )
         b1_turned = sums_psum.tile([P, K_PASS], F32, name="sums")
-        nc.tensor.transpose(b1_turned[:, 0:P], b1_wide[:], ident[:])
-        b1_cols = keep.tile([P, P], F32, name="b1_cols")
-        nc.vector.tensor_copy(out=b1_cols[:], in_=b1_turned[:, 0:P])
+        for jj in range(BLOCKS):
+            nc.tensor.transpose(b1_turned[:, P * jj : P * (jj + 1)], b1_wide[:, P * jj : P * (jj + 1)], ident[:])
+        b1_cols = keep.tile([P, BLOCKS, P], F32, name="b1_cols")
+        nc.vector.tensor_copy(out=b1_cols[:].rearrange("m j q -> m (j q)"), in_=b1_turned[:])
+        sort_planes(0)
 
         x_grouped = keep.tile([P, X_GROUPS, TOKENS, 4], BF16, name="x_grouped", align_bytes=64)
         x_codes = keep.tile([P, X_GROUPS, TOKENS], U32, name="x_codes", align_bytes=64)
@@ -136,41 +158,44 @@ def tile_combnethe_pa_kernel(
             )
 
         groups = [(v, g2) for v in range(NETS) for g2 in range(H_GROUPS)]
-        h_blocks = {}
+        w1_sorted = {}
         h_lined = {}
         h_grouped = {}
         h_codes = {}
         h_planes = {}
 
+        def sort_w1(s):
+            v, g2 = groups[s]
+            piece, inside = (K_PASS * g2) // W1_PIECE, (K_PASS * g2) % W1_PIECE
+            w1_sorted[s] = keep.tile([P, X_GROUPS, K_PASS], U32, name="w1_sorted%d" % s, align_bytes=64)
+            nc.vector.tensor_copy(
+                out=w1_sorted[s][:].bitcast(I32).rearrange("p g (j i r) -> p g j i r", j=BLOCKS, r=RUN),
+                in_=w1_raw[(v, piece)][:, :, inside : inside + K_PASS]
+                .bitcast(I32)
+                .rearrange("p g (i j r) -> p g j i r", j=BLOCKS, r=RUN),
+            )
+
         def first_layer(s):
             v, g2 = groups[s]
             h_lined[s] = group_ring.tile([P, 4, TOKENS], BF16, name="lined")
             for jj in range(BLOCKS):
-                j = BLOCKS * g2 + jj
-                column = P * j
-                piece, inside = column // W1_PIECE, column % W1_PIECE
                 sums = sums_psum.tile([P, TOKENS], F32, name="sums")
                 for g in range(X_GROUPS):
                     nc.tensor.matmul_mx(
                         out=sums[:],
-                        lhsT=w1[v][piece][:, g, inside : inside + P].bitcast(FP8X4),
-                        lhsT_scale=w1_planes[v][4 * g : P, column : column + P],
+                        lhsT=w1_sorted[s][:, g, P * jj : P * (jj + 1)].bitcast(FP8X4),
+                        lhsT_scale=w1_planes[v][4 * g : P, K_PASS * g2 + P * jj : K_PASS * g2 + P * (jj + 1)],
                         rhs=x_codes[:, g, :].bitcast(FP8X4),
                         rhs_scale=x_planes[:, g, :],
                         start=(g == 0),
                         stop=(g == X_GROUPS - 1),
                     )
-                bias = b1_cols[:, (D_H // P) * v + j : (D_H // P) * v + j + 1]
                 block = block_ring.tile([P, TOKENS], BF16, name="block")
-                if jj == 0 and s % 2 == 0:
-                    nc.vector.tensor_scalar(
-                        out=block[:], in0=sums[:], scalar1=bias, scalar2=0.0, op0=ALU.add, op1=ALU.max
-                    )
-                else:
-                    nc.scalar.activation(out=block[:], in_=sums[:], func=ACT.Relu, bias=bias)
-                queue = nc.sync if jj < BLOCKS // 2 else nc.scalar
-                queue.dma_start(out=h_lined[s][32 * jj : 32 * (jj + 1), :, :], in_=block[:])
-                h_blocks[(s, jj)] = block
+                nc.scalar.activation(
+                    out=block[:], in_=sums[:], func=ACT.Relu,
+                    bias=b1_cols[:, jj, H_GROUPS * v + g2 : H_GROUPS * v + g2 + 1],
+                )
+                nc.sync.dma_start(out=h_lined[s][jj : P : BLOCKS, :, :], in_=block[:])
 
         def regroup(s):
             h_grouped[s] = group_ring.tile([P, TOKENS, 4], BF16, name="grouped", align_bytes=64)
@@ -180,8 +205,8 @@ def tile_combnethe_pa_kernel(
             )
 
         def quantise(s):
-            h_codes[s] = keep.tile([P, TOKENS], U32, name="h_codes%d" % s, align_bytes=64)
-            h_planes[s] = keep.tile([P, TOKENS], U8, name="h_planes%d" % s, align_bytes=64)
+            h_codes[s] = group_ring.tile([P, TOKENS], U32, name="h_codes", align_bytes=64)
+            h_planes[s] = group_ring.tile([P, TOKENS], U8, name="h_planes", align_bytes=64)
             nc.vector.quantize_mx(
                 out=h_codes[s][:].bitcast(FP8X4),
                 scales=h_planes[s][:],
@@ -297,7 +322,20 @@ def tile_combnethe_pa_kernel(
         HEAD_O = H_GROUPS - 1 + SECOND_LAG
         HEAD_F = len(groups) - 1 + SECOND_LAG
         GATE_STEP = HEAD_O + 1
+        SORT_AHEAD = 2
+
+        def prepare_w1(s):
+            if s == H_GROUPS:
+                sort_planes(1)
+            sort_w1(s)
+            if s < H_GROUPS and (K_PASS * (s + 1)) % W1_PIECE == 0:
+                load_w1(1, (K_PASS * s) // W1_PIECE)
+
+        for s in range(SORT_AHEAD):
+            prepare_w1(s)
         for s in range(HEAD_F + 1):
+            if s + SORT_AHEAD < len(groups):
+                prepare_w1(s + SORT_AHEAD)
             if s < len(groups):
                 first_layer(s)
             if 0 <= s - SECOND_LAG:

@@ -18,8 +18,6 @@ TOKENS, D_IN, D_H, CLASSES = 512, 1024, 4096, 128
 TOKEN_TILES = TOKENS // P
 X_GROUPS = D_IN // K_PASS
 H_GROUPS = D_H // K_PASS
-BLOCKS = K_PASS // P
-W1_PIECE = 1024
 TAU, GATE_ROUNDS, INVERSE_STEPS = 0.5, 3, 3
 
 FLOPS = 2 * (2 * TOKENS * D_IN * D_H + 2 * TOKENS * D_H * CLASSES)
@@ -38,19 +36,24 @@ def tile_combnethe_pa_kernel(
 
     with ExitStack() as ctx:
         keep = ctx.enter_context(tc.tile_pool(name="keep", bufs=1))
-        block_ring = ctx.enter_context(tc.tile_pool(name="block_ring", bufs=4 * BLOCKS))
-        group_ring = ctx.enter_context(tc.tile_pool(name="group_ring", bufs=4))
-        raw_ring = ctx.enter_context(tc.tile_pool(name="raw_ring", bufs=D_H // W1_PIECE))
-        sums_psum = ctx.enter_context(tc.psum_pool(name="sums_psum", bufs=4))
-        head_psum = ctx.enter_context(tc.psum_pool(name="head_psum", bufs=1))
+        ring = ctx.enter_context(tc.tile_pool(name="ring", bufs=8))
+        round_ring = ctx.enter_context(tc.tile_pool(name="round_ring", bufs=3))
         ctx.enter_context(tc.manual_schedule())
+        sums_psum = ctx.enter_context(tc.psum_pool(name="sums_psum", bufs=4))
+        turn_psum = ctx.enter_context(tc.psum_pool(name="turn_psum", bufs=3))
+        head_psum = ctx.enter_context(tc.psum_pool(name="head_psum", bufs=1))
 
-        b1_rows = keep.tile([P, K_PASS], BF16, name="b1_rows")
-        nc.vector.memset(b1_rows[:], 0.0)
+        B2_ROW = NETS * H_GROUPS
+        bias_rows = keep.tile([P, K_PASS], BF16, name="bias_rows")
+        nc.vector.memset(bias_rows[:], 0.0)
         for v in range(NETS):
             nc.scalar.dma_start(
-                out=b1_rows[H_GROUPS * v : H_GROUPS * (v + 1), :],
+                out=bias_rows[H_GROUPS * v : H_GROUPS * (v + 1), :],
                 in_=given[v]["b1"].rearrange("(g n) -> g n", n=K_PASS),
+            )
+            nc.scalar.dma_start(
+                out=bias_rows[B2_ROW : B2_ROW + 1, CLASSES * v : CLASSES * (v + 1)],
+                in_=given[v]["b2"].rearrange("(o c) -> o c", o=1),
             )
         x_rows = []
         x_view = x.rearrange("(t p) k -> p t k", p=P)
@@ -58,194 +61,194 @@ def tile_combnethe_pa_kernel(
             x_rows.append(keep.tile([P, 2, D_IN], BF16, name="x_rows%d" % half))
             nc.scalar.dma_start(out=x_rows[half][:], in_=x_view[:, 2 * half : 2 * half + 2, :])
 
-        w1_planes_raw = []
+        w1_planes = []
         w2_planes = []
         for v in range(NETS):
-            w1_planes_raw.append(keep.tile([P, D_H], U8, name="w1_planes_raw%d" % v))
+            w1_planes.append(keep.tile([P, D_H], U8, name="w1_planes%d" % v, align_bytes=64))
             w2_planes.append(keep.tile([P, H_GROUPS, CLASSES], U8, name="w2_planes%d" % v, align_bytes=64))
-            nc.vector.memset(w1_planes_raw[v][:].bitcast(I32), 0)
+            nc.vector.memset(w1_planes[v][:].bitcast(I32), 0)
             nc.vector.memset(w2_planes[v][:].rearrange("p g c -> p (g c)").bitcast(I32), 0)
 
         ident = keep.tile([P, P], F32, name="ident")
         make_identity(nc, ident[:])
+        ident_bf16 = keep.tile([P, P], BF16, name="ident_bf16")
+        make_identity(nc, ident_bf16[:])
 
-        w1_raw = {}
-
-        def load_w1(v, piece):
-            w1_raw[(v, piece)] = raw_ring.tile([P, X_GROUPS, W1_PIECE], U32, name="w1_raw")
-            w1_bytes = given[v]["w1"].rearrange("g p n t -> p g (n t)")
-            nc.sync.dma_start(
-                out=w1_raw[(v, piece)][:].bitcast(I32),
-                in_=w1_bytes[:, :, 4 * W1_PIECE * piece : 4 * W1_PIECE * (piece + 1)].bitcast(I32),
-            )
-
+        w1 = [[], []]
         w2 = []
-        b2 = []
+        b1 = []
+        b2 = keep.tile([P, NETS, CLASSES], F32, name="b2")
         for v in range(NETS):
             for quadrant in range(4):
                 nc.sync.dma_start(
-                    out=w1_planes_raw[v][32 * quadrant : 32 * quadrant + 4 * X_GROUPS, :].bitcast(I32),
+                    out=w1_planes[v][32 * quadrant : 32 * quadrant + 4 * X_GROUPS, :].bitcast(I32),
                     in_=given[v]["s1"][:, 4 * quadrant : 4 * quadrant + 4, :].bitcast(I32),
                 )
-            if v == 0:
-                for piece in range(D_H // W1_PIECE):
-                    load_w1(v, piece)
-        for v in range(NETS):
+            b1.append(keep.tile([P, H_GROUPS, K_PASS], BF16, name="b1_%d" % v))
+            w1_bytes = given[v]["w1"].rearrange("g p n t -> p g (n t)")
+            for piece in range(H_GROUPS):
+                w1[v].append(keep.tile([P, X_GROUPS, K_PASS], U32, name="w1_%d_%d" % (v, piece), align_bytes=64))
+                nc.sync.dma_start(
+                    out=w1[v][piece][:].bitcast(I32),
+                    in_=w1_bytes[:, :, 4 * K_PASS * piece : 4 * K_PASS * (piece + 1)].bitcast(I32),
+                )
             for quadrant in range(4):
                 nc.sync.dma_start(
                     out=w2_planes[v][32 * quadrant : 32 * quadrant + 4, :, :].bitcast(I32),
                     in_=given[v]["s2"][:, 4 * quadrant : 4 * quadrant + 4, :].rearrange("g r c -> r g c").bitcast(I32),
                 )
             w2.append(keep.tile([P, H_GROUPS, CLASSES], U32, name="w2_%d" % v, align_bytes=64))
-            for w in range(2):
-                for jj in range(BLOCKS):
-                    nc.sync.dma_start(
-                        out=w2[v][4 * w + jj : P : 8, :, :].bitcast(I32),
-                        in_=given[v]["w2"][:, 2 * jj + w : P : 8, :, :].rearrange("g i c t -> i g (c t)").bitcast(I32),
-                    )
-            b2.append(keep.tile([P, CLASSES], BF16, name="b2_%d" % v))
-            nc.scalar.dma_start(out=b2[v][:], in_=given[v]["b2"].partition_broadcast(P))
+            nc.sync.dma_start(
+                out=w2[v][:].bitcast(I32),
+                in_=given[v]["w2"].rearrange("g p n t -> p g (n t)").bitcast(I32),
+            )
 
         warm_in = keep.tile([P, 1], F32, name="warm_in")
         warm_out = keep.tile([P, 1], F32, name="warm_out")
         nc.vector.memset(warm_in[:], 0.0)
         nc.scalar.activation(out=warm_out[:], in_=warm_in[:], func=ACT.Exp)
 
-        RUN = 8
-        RUNS = P // RUN
-        w1_planes = [keep.tile([P, D_H], U8, name="w1_planes%d" % v, align_bytes=64) for v in range(NETS)]
+        def spread(row):
+            wide = sums_psum.tile([P, K_PASS], F32, name="sums")
+            nc.tensor.matmul(
+                out=wide[:], lhsT=ident_bf16[:, row : row + 1].to_broadcast([P, P]), rhs=bias_rows[:],
+                start=True, stop=True,
+            )
+            return wide
 
-        def sort_planes(v):
-            nc.vector.tensor_copy(
-                out=w1_planes[v][:].bitcast(I32).rearrange("p (G j i r) -> p G j i r", j=BLOCKS, i=RUNS, r=RUN // 4),
-                in_=w1_planes_raw[v][:].bitcast(I32).rearrange("p (G i j r) -> p G j i r", j=BLOCKS, i=RUNS, r=RUN // 4),
+        def spread_b1(v, piece):
+            wide = spread(H_GROUPS * v + piece)
+            nc.scalar.copy(
+                out=b1[v][:, piece, :].rearrange("k (u p e) -> k u p e", u=2, e=2),
+                in_=wide[:].rearrange("k (p u e) -> k u p e", u=2, e=2),
             )
 
-        b1_wide = keep.tile([P, K_PASS], F32, name="b1_wide")
-        nc.vector.tensor_copy(
-            out=b1_wide[:].rearrange("q (j i r) -> q j i r", j=BLOCKS, r=RUN),
-            in_=b1_rows[:].rearrange("q (i j r) -> q j i r", j=BLOCKS, r=RUN),
-        )
-        b1_turned = sums_psum.tile([P, K_PASS], F32, name="sums")
-        for jj in range(BLOCKS):
-            nc.tensor.transpose(b1_turned[:, P * jj : P * (jj + 1)], b1_wide[:, P * jj : P * (jj + 1)], ident[:])
-        b1_cols = keep.tile([P, BLOCKS, P], F32, name="b1_cols")
-        nc.vector.tensor_copy(out=b1_cols[:].rearrange("m j q -> m (j q)"), in_=b1_turned[:])
-        sort_planes(0)
+        def spread_b2():
+            wide = spread(B2_ROW)
+            nc.scalar.copy(out=b2[:].rearrange("k v c -> k (v c)"), in_=wide[:, 0 : NETS * CLASSES])
 
-        x_grouped = keep.tile([P, X_GROUPS, TOKENS, 4], BF16, name="x_grouped", align_bytes=64)
-        x_codes = keep.tile([P, X_GROUPS, TOKENS], U32, name="x_codes", align_bytes=64)
-        x_planes = keep.tile([P, X_GROUPS, TOKENS], U8, name="x_planes", align_bytes=64)
+        AHEAD = 2
+        for piece in range(AHEAD):
+            spread_b1(0, piece)
+
+        x_codes = []
+        x_planes = []
         for tt in range(TOKEN_TILES):
             x_words = x_rows[tt // 2][:, tt % 2, :].bitcast(F32)
-            x_turned = sums_psum.tile([P, K_PASS], F32, name="sums")
+            turned = turn_psum.tile([P, 2 * X_GROUPS, P], F32, name="turned")
             for g in range(X_GROUPS):
                 for u in range(2):
                     nc.tensor.transpose(
-                        x_turned[:, P * (2 * g + u) : P * (2 * g + u + 1)],
-                        x_words[:, 256 * g + u : 256 * (g + 1) : 2],
-                        ident[:],
+                        turned[:, 2 * g + u, :], x_words[:, 256 * g + u : 256 * (g + 1) : 2], ident[:]
                     )
-            nc.scalar.copy(
-                out=x_grouped[:, :, P * tt : P * (tt + 1), :].bitcast(F32),
-                in_=x_turned[:].rearrange("p (g u k) -> p g k u", g=X_GROUPS, u=2),
+            x_grouped = ring.tile([P, X_GROUPS, P, 4], BF16, name="x_grouped", align_bytes=64)
+            nc.vector.tensor_copy(
+                out=x_grouped[:].bitcast(F32), in_=turned[:].rearrange("p (g u) k -> p g k u", u=2)
             )
-        for g in range(X_GROUPS):
+            x_codes.append(keep.tile([P, X_GROUPS, P], U32, name="x_codes%d" % tt, align_bytes=64))
+            x_planes.append(keep.tile([P, X_GROUPS, P], U8, name="x_planes%d" % tt, align_bytes=64))
             nc.vector.quantize_mx(
-                out=x_codes[:, g, :].bitcast(FP8X4),
-                scales=x_planes[:, g, :],
-                in_=x_grouped[:, g, :, :].rearrange("p k t -> p (k t)"),
+                out=x_codes[tt][:].rearrange("p g k -> p (g k)").bitcast(FP8X4),
+                scales=x_planes[tt][:].rearrange("p g k -> p (g k)"),
+                in_=x_grouped[:].rearrange("p g k t -> p (g k t)"),
             )
 
-        groups = [(v, g2) for v in range(NETS) for g2 in range(H_GROUPS)]
-        w1_sorted = {}
-        h_lined = {}
+        rounds = [(0, [(tt, piece) for tt in range(TOKEN_TILES)]) for piece in range(H_GROUPS)]
+        rounds += [
+            (1, [(tt, piece) for piece in range(4 * half, 4 * half + 4)])
+            for tt in range(TOKEN_TILES)
+            for half in range(2)
+        ]
+        BLOCKS = 4
+        h_rows = {}
         h_grouped = {}
         h_codes = {}
         h_planes = {}
+        place = {}
+        for r in range(len(rounds)):
+            for i, (tt, piece) in enumerate(rounds[r][1]):
+                place[(rounds[r][0], tt, piece)] = (r, i)
 
-        def sort_w1(s):
-            v, g2 = groups[s]
-            piece, inside = (K_PASS * g2) // W1_PIECE, (K_PASS * g2) % W1_PIECE
-            w1_sorted[s] = keep.tile([P, X_GROUPS, K_PASS], U32, name="w1_sorted%d" % s, align_bytes=64)
-            nc.vector.tensor_copy(
-                out=w1_sorted[s][:].bitcast(I32).rearrange("p g (j i r) -> p g j i r", j=BLOCKS, r=RUN),
-                in_=w1_raw[(v, piece)][:, :, inside : inside + K_PASS]
-                .bitcast(I32)
-                .rearrange("p g (i j r) -> p g j i r", j=BLOCKS, r=RUN),
-            )
-
-        def first_layer(s):
-            v, g2 = groups[s]
-            h_lined[s] = group_ring.tile([P, 4, TOKENS], BF16, name="lined")
-            for jj in range(BLOCKS):
-                sums = sums_psum.tile([P, TOKENS], F32, name="sums")
+        def first_layer(r):
+            v, blocks = rounds[r]
+            for i, (tt, piece) in enumerate(blocks):
+                sums = sums_psum.tile([P, K_PASS], F32, name="sums")
                 for g in range(X_GROUPS):
                     nc.tensor.matmul_mx(
                         out=sums[:],
-                        lhsT=w1_sorted[s][:, g, P * jj : P * (jj + 1)].bitcast(FP8X4),
-                        lhsT_scale=w1_planes[v][4 * g : P, K_PASS * g2 + P * jj : K_PASS * g2 + P * (jj + 1)],
-                        rhs=x_codes[:, g, :].bitcast(FP8X4),
-                        rhs_scale=x_planes[:, g, :],
+                        lhsT=x_codes[tt][:, g, :].bitcast(FP8X4),
+                        lhsT_scale=x_planes[tt][:, g, :],
+                        rhs=w1[v][piece][:, g, :].bitcast(FP8X4),
+                        rhs_scale=w1_planes[v][4 * g : P, K_PASS * piece : K_PASS * (piece + 1)],
                         start=(g == 0),
                         stop=(g == X_GROUPS - 1),
                     )
-                block = block_ring.tile([P, TOKENS], BF16, name="block")
-                nc.scalar.activation(
-                    out=block[:], in_=sums[:], func=ACT.Relu,
-                    bias=b1_cols[:, jj, H_GROUPS * v + g2 : H_GROUPS * v + g2 + 1],
+                rows = ring.tile([P, K_PASS], BF16, name="rows")
+                nc.vector.tensor_tensor(
+                    out=rows[:].rearrange("k (u p e) -> k u p e", u=2, e=2),
+                    in0=sums[:].rearrange("k (p u e) -> k u p e", u=2, e=2),
+                    in1=b1[v][:, piece, :].rearrange("k (u p e) -> k u p e", u=2, e=2),
+                    op=ALU.add,
                 )
-                nc.sync.dma_start(out=h_lined[s][jj : P : BLOCKS, :, :], in_=block[:])
+                h_rows[(r, i)] = rows
 
-        def regroup(s):
-            h_grouped[s] = group_ring.tile([P, TOKENS, 4], BF16, name="grouped", align_bytes=64)
-            nc.vector.tensor_copy(
-                out=h_grouped[s][:].rearrange("p (c i) t -> p c t i", i=4),
-                in_=h_lined[s][:].rearrange("p t (c i) -> p c t i", i=4),
-            )
+        def turn(r):
+            h_grouped[r] = round_ring.tile([P, BLOCKS, P, 4], BF16, name="grouped", align_bytes=64)
+            for first in range(0, BLOCKS, 2):
+                turned = turn_psum.tile([P, 4, P], F32, name="turned")
+                for i in range(2):
+                    words = h_rows[(r, first + i)][:].bitcast(F32)
+                    for u in range(2):
+                        nc.tensor.transpose(turned[:, 2 * i + u, :], words[:, P * u : P * (u + 1)], ident[:])
+                for i in range(2):
+                    nc.scalar.activation(
+                        out=h_grouped[r][:, first + i, :, :].rearrange("p k (u e) -> p k u e", u=2),
+                        in_=turned[:, 2 * i : 2 * i + 2, :].bitcast(BF16).rearrange("p u (k e) -> p k u e", e=2),
+                        func=ACT.Relu,
+                    )
 
-        def quantise(s):
-            h_codes[s] = group_ring.tile([P, TOKENS], U32, name="h_codes", align_bytes=64)
-            h_planes[s] = group_ring.tile([P, TOKENS], U8, name="h_planes", align_bytes=64)
+        def quantise(r):
+            h_codes[r] = keep.tile([P, BLOCKS, P], U32, name="h_codes%d" % r, align_bytes=64)
+            h_planes[r] = keep.tile([P, BLOCKS, P], U8, name="h_planes%d" % r, align_bytes=64)
             nc.vector.quantize_mx(
-                out=h_codes[s][:].bitcast(FP8X4),
-                scales=h_planes[s][:],
-                in_=h_grouped[s][:].rearrange("p k t -> p (k t)"),
+                out=h_codes[r][:].rearrange("p i k -> p (i k)").bitcast(FP8X4),
+                scales=h_planes[r][:].rearrange("p i k -> p (i k)"),
+                in_=h_grouped[r][:].rearrange("p i k t -> p (i k t)"),
             )
 
         neg_max = [keep.tile([P, TOKEN_TILES], F32, name="neg_max%d" % v) for v in range(NETS)]
         exp_sum = [keep.tile([P, TOKEN_TILES], F32, name="exp_sum%d" % v) for v in range(NETS)]
         inv_sum = [keep.tile([P, TOKEN_TILES], F32, name="inv_sum%d" % v) for v in range(NETS)]
-        logits = [keep.tile([P, TOKEN_TILES, CLASSES], F32, name="logits%d" % v) for v in range(NETS)]
-        exps = [keep.tile([P, TOKEN_TILES, CLASSES], F32, name="exps%d" % v) for v in range(NETS)]
         logits_psum = {}
+        exps = {}
 
-        def second_layer(s):
-            v, g2 = groups[s]
-            for tt in range(TOKEN_TILES):
-                if g2 == 0:
-                    logits_psum[(v, tt)] = head_psum.tile([P, CLASSES], F32, name="logits_psum%d" % tt)
-                nc.tensor.matmul_mx(
-                    out=logits_psum[(v, tt)][:],
-                    lhsT=h_codes[s][:, P * tt : P * (tt + 1)].bitcast(FP8X4),
-                    lhsT_scale=h_planes[s][:, P * tt : P * (tt + 1)],
-                    rhs=w2[v][:, g2, :].bitcast(FP8X4),
-                    rhs_scale=w2_planes[v][:, g2, :],
-                    start=(g2 == 0),
-                    stop=(g2 == H_GROUPS - 1),
-                )
+        def second_layer(v, token_tiles):
+            logits_psum[v] = head_psum.tile([P, TOKEN_TILES, CLASSES], F32, name="logits_psum")
+            for tt in token_tiles:
+                for g in range(H_GROUPS):
+                    r, i = place[(v, tt, g)]
+                    nc.tensor.matmul_mx(
+                        out=logits_psum[v][:, tt, :],
+                        lhsT=h_codes[r][:, i, :].bitcast(FP8X4),
+                        lhsT_scale=h_planes[r][:, i, :],
+                        rhs=w2[v][:, g, :].bitcast(FP8X4),
+                        rhs_scale=w2_planes[v][:, g, :],
+                        start=(g == 0),
+                        stop=(g == H_GROUPS - 1),
+                    )
 
-        def exponentials(v):
-            for tt in range(TOKEN_TILES):
-                nc.vector.tensor_tensor(out=logits[v][:, tt, :], in0=logits_psum[(v, tt)][:], in1=b2[v][:], op=ALU.add)
+        def exponentials(v, tt):
+            column = slice(tt, tt + 1)
+            logits = keep.tile([P, CLASSES], F32, name="logits%d_%d" % (v, tt))
+            nc.vector.tensor_tensor(out=logits[:], in0=logits_psum[v][:, tt, :], in1=b2[:, v, :], op=ALU.add)
             nc.vector.tensor_reduce(
-                out=neg_max[v][:], in_=logits[v][:], axis=mybir.AxisListType.X, op=ALU.max, negate=True
+                out=neg_max[v][:, column], in_=logits[:], axis=mybir.AxisListType.X, op=ALU.max, negate=True
             )
-            for tt in range(TOKEN_TILES):
-                nc.scalar.activation(
-                    out=exps[v][:, tt, :], in_=logits[v][:, tt, :], func=ACT.Exp,
-                    bias=neg_max[v][:, tt : tt + 1], accum_out=exp_sum[v][:, tt : tt + 1],
-                )
+            exps[(v, tt)] = keep.tile([P, CLASSES], F32, name="exps%d_%d" % (v, tt))
+            nc.scalar.activation(
+                out=exps[(v, tt)][:], in_=logits[:], func=ACT.Exp,
+                bias=neg_max[v][:, column], accum_out=exp_sum[v][:, column],
+            )
 
         power = {}
         power_sum = [keep.tile([P, TOKEN_TILES], F32, name="power_sum%d" % i) for i in range(GATE_ROUNDS)]
@@ -266,7 +269,7 @@ def tile_combnethe_pa_kernel(
                 power[(i, tt)] = keep.tile([P, CLASSES], F32, name="power%d_%d" % (i, tt))
                 if i == 0:
                     nc.scalar.activation(
-                        out=power[(i, tt)][:], in_=exps[0][:, tt, :], func=ACT.Square,
+                        out=power[(i, tt)][:], in_=exps[(0, tt)][:], func=ACT.Square,
                         scale=inv_sum[0][:, column], accum_out=power_sum[i][:, column],
                     )
                 else:
@@ -303,7 +306,7 @@ def tile_combnethe_pa_kernel(
             for tt in range(TOKEN_TILES):
                 share1[tt] = keep.tile([P, CLASSES], F32, name="share1_%d" % tt)
                 nc.gpsimd.tensor_scalar(
-                    out=share1[tt][:], in0=exps[0][:, tt, :], scalar1=weight1[:, tt : tt + 1], scalar2=0.0,
+                    out=share1[tt][:], in0=exps[(0, tt)][:], scalar1=weight1[:, tt : tt + 1], scalar2=0.0,
                     op0=ALU.mult, op1=ALU.add,
                 )
 
@@ -313,39 +316,40 @@ def tile_combnethe_pa_kernel(
             nc.vector.tensor_tensor(out=weight2[:, column], in0=inv_sum[1][:, column], in1=cond[:, column], op=ALU.mult)
             mixed = keep.tile([P, CLASSES], F32, name="mixed%d" % tt)
             nc.vector.scalar_tensor_tensor(
-                out=mixed[:], in0=exps[1][:, tt, :], scalar=weight2[:, column], in1=share1[tt][:],
+                out=mixed[:], in0=exps[(1, tt)][:], scalar=weight2[:, column], in1=share1[tt][:],
                 op0=ALU.mult, op1=ALU.add,
             )
             nc.sync.dma_start(out=out[P * tt : P * (tt + 1), :], in_=mixed[:])
 
-        REGROUP_LAG, QUANTISE_LAG, SECOND_LAG = 3, 4, 5
-        HEAD_O = H_GROUPS - 1 + SECOND_LAG
-        HEAD_F = len(groups) - 1 + SECOND_LAG
-        GATE_STEP = HEAD_O + 1
-        SORT_AHEAD = 2
-
-        def prepare_w1(s):
-            if s == H_GROUPS:
-                sort_planes(1)
-            sort_w1(s)
-            if s < H_GROUPS and (K_PASS * (s + 1)) % W1_PIECE == 0:
-                load_w1(1, (K_PASS * s) // W1_PIECE)
-
-        for s in range(SORT_AHEAD):
-            prepare_w1(s)
-        for s in range(HEAD_F + 1):
-            if s + SORT_AHEAD < len(groups):
-                prepare_w1(s + SORT_AHEAD)
-            if s < len(groups):
+        LAG = 3
+        LAST_O = H_GROUPS - 1
+        GATE_STEP = LAST_O + LAG + 1
+        BLEND_STEP = GATE_STEP + GATE_ROUNDS + 2
+        for s in range(len(rounds) + LAG + 2):
+            done = s - LAG
+            done_f = [tt for tt in range(TOKEN_TILES) if place[(1, tt, H_GROUPS - 1)][0] == done]
+            before_f = [tt for tt in range(TOKEN_TILES) if place[(1, tt, H_GROUPS - 1)][0] == done - 1]
+            if s < len(rounds):
                 first_layer(s)
-            if 0 <= s - SECOND_LAG:
-                second_layer(s - SECOND_LAG)
-            if 0 <= s - REGROUP_LAG < len(groups):
-                regroup(s - REGROUP_LAG)
-            if 0 <= s - QUANTISE_LAG < len(groups):
-                quantise(s - QUANTISE_LAG)
-            if s == HEAD_O:
-                exponentials(0)
+            if s + AHEAD < H_GROUPS:
+                spread_b1(0, s + AHEAD)
+            if s < H_GROUPS:
+                spread_b1(1, s)
+            if s == H_GROUPS:
+                spread_b2()
+            if done == LAST_O:
+                second_layer(0, list(range(TOKEN_TILES)))
+            if done_f:
+                second_layer(1, done_f)
+            if 0 <= s - 1 < len(rounds):
+                turn(s - 1)
+            if 0 <= s - 2 < len(rounds):
+                quantise(s - 2)
+            if done == LAST_O:
+                for tt in range(TOKEN_TILES):
+                    exponentials(0, tt)
+            for tt in done_f:
+                exponentials(1, tt)
             if s == GATE_STEP:
                 nc.vector.reciprocal(out=inv_sum[0][:], in_=exp_sum[0][:])
             if 0 <= s - GATE_STEP < GATE_ROUNDS:
@@ -353,6 +357,10 @@ def tile_combnethe_pa_kernel(
                 gate_round(s - GATE_STEP)
             if s == GATE_STEP + GATE_ROUNDS:
                 gate_end()
-        exponentials(1)
-        for tt in range(TOKEN_TILES):
-            blend(tt)
+            if s == BLEND_STEP:
+                for tt in range(TOKEN_TILES):
+                    if place[(1, tt, H_GROUPS - 1)][0] < done - 1:
+                        blend(tt)
+            if s >= BLEND_STEP:
+                for tt in before_f:
+                    blend(tt)

@@ -13,12 +13,13 @@ ALU = mybir.AluOpType
 ACT = mybir.ActivationFunctionType
 
 P = 128
+PACK = 4
 K_PASS = 512
 TOKENS, D_IN, D_H, CLASSES = 512, 1024, 4096, 128
 TOKEN_TILES = TOKENS // P
 X_GROUPS = D_IN // K_PASS
 H_GROUPS = D_H // K_PASS
-TAU, GATE_ROUNDS, INVERSE_STEPS = 0.5, 3, 3
+TAU = 0.5
 
 FLOPS = 2 * (2 * TOKENS * D_IN * D_H + 2 * TOKENS * D_H * CLASSES)
 
@@ -33,40 +34,45 @@ def tile_combnethe_pa_kernel(
         dict(w1=W1f_words, s1=W1f_scales, b1=b1f, w2=W2f_words, s2=W2f_scales, b2=b2f),
     )
     NETS = len(given)
+    ROUNDS = NETS * H_GROUPS
 
     with ExitStack() as ctx:
         keep = ctx.enter_context(tc.tile_pool(name="keep", bufs=1))
-        ring = ctx.enter_context(tc.tile_pool(name="ring", bufs=8))
-        round_ring = ctx.enter_context(tc.tile_pool(name="round_ring", bufs=3))
+        ring = ctx.enter_context(tc.tile_pool(name="ring", bufs=3))
+        sorted_ring = ctx.enter_context(tc.tile_pool(name="sorted_ring", bufs=4))
         ctx.enter_context(tc.manual_schedule())
-        sums_psum = ctx.enter_context(tc.psum_pool(name="sums_psum", bufs=4))
-        turn_psum = ctx.enter_context(tc.psum_pool(name="turn_psum", bufs=3))
-        head_psum = ctx.enter_context(tc.psum_pool(name="head_psum", bufs=1))
+        sums_psum = ctx.enter_context(tc.psum_pool(name="sums_psum", bufs=6))
+        head_psum = ctx.enter_context(tc.psum_pool(name="head_psum", bufs=2))
 
         B2_ROW = NETS * H_GROUPS
         bias_rows = keep.tile([P, K_PASS], BF16, name="bias_rows")
         nc.vector.memset(bias_rows[:], 0.0)
+        w1_planes_raw = keep.tile([P, D_H], U8, name="w1_planes_raw", align_bytes=64)
+        nc.vector.memset(w1_planes_raw[:].bitcast(I32), 0)
         for v in range(NETS):
-            nc.scalar.dma_start(
+            nc.sync.dma_start(
                 out=bias_rows[H_GROUPS * v : H_GROUPS * (v + 1), :],
                 in_=given[v]["b1"].rearrange("(g n) -> g n", n=K_PASS),
             )
-            nc.scalar.dma_start(
+            nc.sync.dma_start(
                 out=bias_rows[B2_ROW : B2_ROW + 1, CLASSES * v : CLASSES * (v + 1)],
                 in_=given[v]["b2"].rearrange("(o c) -> o c", o=1),
             )
         x_rows = []
-        x_view = x.rearrange("(t p) k -> p t k", p=P)
-        for half in range(2):
-            x_rows.append(keep.tile([P, 2, D_IN], BF16, name="x_rows%d" % half))
-            nc.scalar.dma_start(out=x_rows[half][:], in_=x_view[:, 2 * half : 2 * half + 2, :])
+        for tt in range(TOKEN_TILES):
+            x_rows.append(keep.tile([P, D_IN], BF16, name="x_rows%d" % tt))
+            nc.scalar.dma_start(out=x_rows[tt][:], in_=x[P * tt : P * (tt + 1), :])
+        for v in range(NETS):
+            for quadrant in range(4):
+                first = 32 * quadrant + 4 * X_GROUPS * v
+                nc.sync.dma_start(
+                    out=w1_planes_raw[first : first + 4 * X_GROUPS, :].bitcast(I32),
+                    in_=given[v]["s1"][:, 4 * quadrant : 4 * quadrant + 4, :].bitcast(I32),
+                )
 
-        w1_planes = []
         w2_planes = []
         for v in range(NETS):
-            w1_planes.append(keep.tile([P, D_H], U8, name="w1_planes%d" % v, align_bytes=64))
             w2_planes.append(keep.tile([P, H_GROUPS, CLASSES], U8, name="w2_planes%d" % v, align_bytes=64))
-            nc.vector.memset(w1_planes[v][:].bitcast(I32), 0)
             nc.vector.memset(w2_planes[v][:].rearrange("p g c -> p (g c)").bitcast(I32), 0)
 
         ident = keep.tile([P, P], F32, name="ident")
@@ -74,22 +80,14 @@ def tile_combnethe_pa_kernel(
         ident_bf16 = keep.tile([P, P], BF16, name="ident_bf16")
         make_identity(nc, ident_bf16[:])
 
-        w1 = [[], []]
+        w1_raw = [[], []]
         w2 = []
-        b1 = []
-        b2 = keep.tile([P, NETS, CLASSES], F32, name="b2")
         for v in range(NETS):
-            for quadrant in range(4):
-                nc.sync.dma_start(
-                    out=w1_planes[v][32 * quadrant : 32 * quadrant + 4 * X_GROUPS, :].bitcast(I32),
-                    in_=given[v]["s1"][:, 4 * quadrant : 4 * quadrant + 4, :].bitcast(I32),
-                )
-            b1.append(keep.tile([P, H_GROUPS, K_PASS], BF16, name="b1_%d" % v))
             w1_bytes = given[v]["w1"].rearrange("g p n t -> p g (n t)")
             for piece in range(H_GROUPS):
-                w1[v].append(keep.tile([P, X_GROUPS, K_PASS], U32, name="w1_%d_%d" % (v, piece), align_bytes=64))
+                w1_raw[v].append(keep.tile([P, X_GROUPS, K_PASS], U32, name="w1_raw%d_%d" % (v, piece), align_bytes=64))
                 nc.sync.dma_start(
-                    out=w1[v][piece][:].bitcast(I32),
+                    out=w1_raw[v][piece][:].bitcast(I32),
                     in_=w1_bytes[:, :, 4 * K_PASS * piece : 4 * K_PASS * (piece + 1)].bitcast(I32),
                 )
             for quadrant in range(4):
@@ -108,156 +106,159 @@ def tile_combnethe_pa_kernel(
         nc.vector.memset(warm_in[:], 0.0)
         nc.scalar.activation(out=warm_out[:], in_=warm_in[:], func=ACT.Exp)
 
-        def spread(row):
-            wide = sums_psum.tile([P, K_PASS], F32, name="sums")
-            nc.tensor.matmul(
-                out=wide[:], lhsT=ident_bf16[:, row : row + 1].to_broadcast([P, P]), rhs=bias_rows[:],
-                start=True, stop=True,
-            )
-            return wide
+        bias_words = bias_rows[:].bitcast(F32)
+        bias_turned = sums_psum.tile([P, 2, P], F32, name="sums")
+        for u in range(2):
+            nc.tensor.transpose(bias_turned[:, u, :], bias_words[:, u : K_PASS // 2 : 2], ident[:])
+        b1_cols = keep.tile([P, PACK * ROUNDS], F32, name="b1_cols")
+        nc.vector.tensor_copy(
+            out=b1_cols[:].rearrange("p (r u e) -> p r u e", u=2, e=2),
+            in_=bias_turned[:, :, 0:ROUNDS].bitcast(BF16).rearrange("p u (r e) -> p r u e", e=2),
+        )
+        b2_wide = []
+        b2_banks = []
+        for v in range(NETS):
+            b2_banks.append(sums_psum.tile([P, TOKEN_TILES, CLASSES], F32, name="sums"))
+            for tt in range(TOKEN_TILES):
+                nc.tensor.matmul(
+                    out=b2_banks[v][:, tt, :], lhsT=ident_bf16[:, B2_ROW : B2_ROW + 1].to_broadcast([P, P]),
+                    rhs=bias_rows[:, CLASSES * v : CLASSES * (v + 1)], start=True, stop=True,
+                )
 
-        def spread_b1(v, piece):
-            wide = spread(H_GROUPS * v + piece)
-            nc.scalar.copy(
-                out=b1[v][:, piece, :].rearrange("k (u p e) -> k u p e", u=2, e=2),
-                in_=wide[:].rearrange("k (p u e) -> k u p e", u=2, e=2),
-            )
+        x_grouped = keep.tile([P, X_GROUPS, TOKENS, PACK], BF16, name="x_grouped", align_bytes=64)
+        x_codes = keep.tile([P, X_GROUPS, TOKENS], U32, name="x_codes", align_bytes=64)
+        x_planes = keep.tile([P, X_GROUPS, TOKENS], U8, name="x_planes", align_bytes=64)
 
-        def spread_b2():
-            wide = spread(B2_ROW)
-            nc.scalar.copy(out=b2[:].rearrange("k v c -> k (v c)"), in_=wide[:, 0 : NETS * CLASSES])
-
-        AHEAD = 2
-        for piece in range(AHEAD):
-            spread_b1(0, piece)
-
-        x_codes = []
-        x_planes = []
-        for tt in range(TOKEN_TILES):
-            x_words = x_rows[tt // 2][:, tt % 2, :].bitcast(F32)
-            turned = turn_psum.tile([P, 2 * X_GROUPS, P], F32, name="turned")
+        def turn_x(tt):
+            x_words = x_rows[tt][:].bitcast(F32)
+            turned = sums_psum.tile([P, 2 * X_GROUPS, P], F32, name="sums")
             for g in range(X_GROUPS):
                 for u in range(2):
                     nc.tensor.transpose(
                         turned[:, 2 * g + u, :], x_words[:, 256 * g + u : 256 * (g + 1) : 2], ident[:]
                     )
-            x_grouped = ring.tile([P, X_GROUPS, P, 4], BF16, name="x_grouped", align_bytes=64)
-            nc.vector.tensor_copy(
-                out=x_grouped[:].bitcast(F32), in_=turned[:].rearrange("p (g u) k -> p g k u", u=2)
-            )
-            x_codes.append(keep.tile([P, X_GROUPS, P], U32, name="x_codes%d" % tt, align_bytes=64))
-            x_planes.append(keep.tile([P, X_GROUPS, P], U8, name="x_planes%d" % tt, align_bytes=64))
-            nc.vector.quantize_mx(
-                out=x_codes[tt][:].rearrange("p g k -> p (g k)").bitcast(FP8X4),
-                scales=x_planes[tt][:].rearrange("p g k -> p (g k)"),
-                in_=x_grouped[:].rearrange("p g k t -> p (g k t)"),
+            nc.scalar.copy(
+                out=x_grouped[:, :, P * tt : P * (tt + 1), :].bitcast(F32),
+                in_=turned[:].rearrange("p (g u) k -> p g k u", u=2),
             )
 
-        rounds = [(0, [(tt, piece) for tt in range(TOKEN_TILES)]) for piece in range(H_GROUPS)]
-        rounds += [
-            (1, [(tt, piece) for piece in range(4 * half, 4 * half + 4)])
-            for tt in range(TOKEN_TILES)
-            for half in range(2)
-        ]
-        BLOCKS = 4
+        def quantise_x(tt):
+            for g in range(X_GROUPS):
+                nc.vector.quantize_mx(
+                    out=x_codes[:, g, P * tt : P * (tt + 1)].bitcast(FP8X4),
+                    scales=x_planes[:, g, P * tt : P * (tt + 1)],
+                    in_=x_grouped[:, g, P * tt : P * (tt + 1), :].rearrange("p k t -> p (k t)"),
+                )
+
+        w1_planes = keep.tile([P, D_H], U8, name="w1_planes", align_bytes=64)
+        w1_sorted = {}
+
+        def sort_planes(piece):
+            cols = slice(K_PASS * piece, K_PASS * (piece + 1))
+            nc.vector.tensor_copy(
+                out=w1_planes[:, cols].rearrange("p (t m) -> p m t", t=PACK),
+                in_=w1_planes_raw[:, cols].rearrange("p (m t) -> p m t", t=PACK),
+            )
+
+        def sort_codes(r, slices):
+            v, piece = divmod(r, H_GROUPS)
+            w1_sorted[r] = sorted_ring.tile([P, X_GROUPS, PACK, P], U32, name="w1_sorted", align_bytes=64)
+            source = w1_raw[v][piece][:].bitcast(I32).rearrange("p g (m t) -> p g t m", t=PACK)
+            width = PACK // slices
+            for i in range(slices):
+                nc.vector.tensor_copy(
+                    out=w1_sorted[r][:, :, width * i : width * (i + 1), :].bitcast(I32),
+                    in_=source[:, :, width * i : width * (i + 1), :],
+                )
+
+        banks = {}
         h_rows = {}
         h_grouped = {}
         h_codes = {}
         h_planes = {}
-        place = {}
-        for r in range(len(rounds)):
-            for i, (tt, piece) in enumerate(rounds[r][1]):
-                place[(rounds[r][0], tt, piece)] = (r, i)
 
         def first_layer(r):
-            v, blocks = rounds[r]
-            for i, (tt, piece) in enumerate(blocks):
-                sums = sums_psum.tile([P, K_PASS], F32, name="sums")
+            v, piece = divmod(r, H_GROUPS)
+            for t in range(PACK):
+                banks[(r, t)] = sums_psum.tile([P, TOKENS], F32, name="sums")
+                first = K_PASS * piece + P * t
                 for g in range(X_GROUPS):
                     nc.tensor.matmul_mx(
-                        out=sums[:],
-                        lhsT=x_codes[tt][:, g, :].bitcast(FP8X4),
-                        lhsT_scale=x_planes[tt][:, g, :],
-                        rhs=w1[v][piece][:, g, :].bitcast(FP8X4),
-                        rhs_scale=w1_planes[v][4 * g : P, K_PASS * piece : K_PASS * (piece + 1)],
+                        out=banks[(r, t)][:],
+                        lhsT=w1_sorted[r][:, g, t, :].bitcast(FP8X4),
+                        lhsT_scale=w1_planes[4 * (X_GROUPS * v + g) : P, first : first + P],
+                        rhs=x_codes[:, g, :].bitcast(FP8X4),
+                        rhs_scale=x_planes[:, g, :],
                         start=(g == 0),
                         stop=(g == X_GROUPS - 1),
                     )
-                rows = ring.tile([P, K_PASS], BF16, name="rows")
-                nc.vector.tensor_tensor(
-                    out=rows[:].rearrange("k (u p e) -> k u p e", u=2, e=2),
-                    in0=sums[:].rearrange("k (p u e) -> k u p e", u=2, e=2),
-                    in1=b1[v][:, piece, :].rearrange("k (u p e) -> k u p e", u=2, e=2),
-                    op=ALU.add,
-                )
-                h_rows[(r, i)] = rows
 
-        def turn(r):
-            h_grouped[r] = round_ring.tile([P, BLOCKS, P, 4], BF16, name="grouped", align_bytes=64)
-            for first in range(0, BLOCKS, 2):
-                turned = turn_psum.tile([P, 4, P], F32, name="turned")
-                for i in range(2):
-                    words = h_rows[(r, first + i)][:].bitcast(F32)
-                    for u in range(2):
-                        nc.tensor.transpose(turned[:, 2 * i + u, :], words[:, P * u : P * (u + 1)], ident[:])
-                for i in range(2):
-                    nc.scalar.activation(
-                        out=h_grouped[r][:, first + i, :, :].rearrange("p k (u e) -> p k u e", u=2),
-                        in_=turned[:, 2 * i : 2 * i + 2, :].bitcast(BF16).rearrange("p u (k e) -> p k u e", e=2),
-                        func=ACT.Relu,
-                    )
+        def fetch(r):
+            h_rows[r] = ring.tile([P, PACK, TOKENS], BF16, name="h_rows")
+            for t in range(PACK):
+                nc.scalar.activation(
+                    out=h_rows[r][:, t, :], in_=banks[(r, t)][:], func=ACT.Relu,
+                    bias=b1_cols[:, PACK * r + t : PACK * r + t + 1],
+                )
+
+        def interleave(r):
+            h_grouped[r] = ring.tile([P, TOKENS, PACK], BF16, name="h_grouped", align_bytes=64)
+            nc.vector.tensor_copy(out=h_grouped[r][:], in_=h_rows[r][:].rearrange("p t k -> p k t"))
 
         def quantise(r):
-            h_codes[r] = keep.tile([P, BLOCKS, P], U32, name="h_codes%d" % r, align_bytes=64)
-            h_planes[r] = keep.tile([P, BLOCKS, P], U8, name="h_planes%d" % r, align_bytes=64)
+            h_codes[r] = keep.tile([P, TOKENS], U32, name="h_codes%d" % r, align_bytes=64)
+            h_planes[r] = keep.tile([P, TOKENS], U8, name="h_planes%d" % r, align_bytes=64)
             nc.vector.quantize_mx(
-                out=h_codes[r][:].rearrange("p i k -> p (i k)").bitcast(FP8X4),
-                scales=h_planes[r][:].rearrange("p i k -> p (i k)"),
-                in_=h_grouped[r][:].rearrange("p i k t -> p (i k t)"),
+                out=h_codes[r][:].bitcast(FP8X4),
+                scales=h_planes[r][:],
+                in_=h_grouped[r][:].rearrange("p k t -> p (k t)"),
             )
 
         neg_max = [keep.tile([P, TOKEN_TILES], F32, name="neg_max%d" % v) for v in range(NETS)]
         exp_sum = [keep.tile([P, TOKEN_TILES], F32, name="exp_sum%d" % v) for v in range(NETS)]
         inv_sum = [keep.tile([P, TOKEN_TILES], F32, name="inv_sum%d" % v) for v in range(NETS)]
-        logits_psum = {}
         exps = {}
 
-        def second_layer(v, token_tiles):
-            logits_psum[v] = head_psum.tile([P, TOKEN_TILES, CLASSES], F32, name="logits_psum")
-            for tt in token_tiles:
-                for g in range(H_GROUPS):
-                    r, i = place[(v, tt, g)]
+        def second_layer(v, pieces):
+            sums = head_psum.tile([P, TOKEN_TILES, CLASSES], F32, name="logits_psum")
+            for tt in range(TOKEN_TILES):
+                for g in pieces:
+                    r = H_GROUPS * v + g
                     nc.tensor.matmul_mx(
-                        out=logits_psum[v][:, tt, :],
-                        lhsT=h_codes[r][:, i, :].bitcast(FP8X4),
-                        lhsT_scale=h_planes[r][:, i, :],
+                        out=sums[:, tt, :],
+                        lhsT=h_codes[r][:, P * tt : P * (tt + 1)].bitcast(FP8X4),
+                        lhsT_scale=h_planes[r][:, P * tt : P * (tt + 1)],
                         rhs=w2[v][:, g, :].bitcast(FP8X4),
                         rhs_scale=w2_planes[v][:, g, :],
-                        start=(g == 0),
-                        stop=(g == H_GROUPS - 1),
+                        start=(g == pieces[0]),
+                        stop=(g == pieces[-1]),
                     )
+            return sums
 
-        def exponentials(v, tt):
+        def exponential(v, tt, logits):
             column = slice(tt, tt + 1)
-            logits = keep.tile([P, CLASSES], F32, name="logits%d_%d" % (v, tt))
-            nc.vector.tensor_tensor(out=logits[:], in0=logits_psum[v][:, tt, :], in1=b2[:, v, :], op=ALU.add)
-            nc.vector.tensor_reduce(
-                out=neg_max[v][:, column], in_=logits[:], axis=mybir.AxisListType.X, op=ALU.max, negate=True
-            )
             exps[(v, tt)] = keep.tile([P, CLASSES], F32, name="exps%d_%d" % (v, tt))
             nc.scalar.activation(
-                out=exps[(v, tt)][:], in_=logits[:], func=ACT.Exp,
+                out=exps[(v, tt)][:], in_=logits, func=ACT.Exp,
                 bias=neg_max[v][:, column], accum_out=exp_sum[v][:, column],
             )
 
+        GATE_ROUNDS = 3
+        rate = [2.0 / (2.0 + TAU * TAU), 1.0, 1.0]
+        tau_power = [TAU ** (2 ** (i + 1)) for i in range(GATE_ROUNDS)]
+        lead = [1.0]
+        for i in range(GATE_ROUNDS):
+            lead.append(lead[i] * lead[i] * rate[i])
         power = {}
         power_sum = [keep.tile([P, TOKEN_TILES], F32, name="power_sum%d" % i) for i in range(GATE_ROUNDS)]
-        factor = keep.tile([P, TOKEN_TILES], F32, name="factor")
-        factor_sq = keep.tile([P, TOKEN_TILES], F32, name="factor_sq")
-        row_sum = keep.tile([P, TOKEN_TILES], F32, name="row_sum")
-        a = keep.tile([P, TOKEN_TILES], F32, name="a")
-        b = keep.tile([P, TOKEN_TILES], F32, name="b")
-        b_plus_1 = keep.tile([P, TOKEN_TILES], F32, name="b_plus_1")
+        slope = [keep.tile([P, TOKEN_TILES], F32, name="slope%d" % i) for i in range(GATE_ROUNDS)]
+        b_powers = [keep.tile([P, 4, TOKEN_TILES], F32, name="b_powers%d" % i) for i in range(GATE_ROUNDS)]
+        terms = [keep.tile([P, 4, TOKEN_TILES], F32, name="terms%d" % i) for i in range(GATE_ROUNDS)]
+        pairs = [keep.tile([P, 2, TOKEN_TILES], F32, name="pairs%d" % i) for i in range(GATE_ROUNDS)]
+        series = [keep.tile([P, TOKEN_TILES], F32, name="series%d" % i) for i in range(GATE_ROUNDS)]
+        body = [keep.tile([P, TOKEN_TILES], F32, name="body%d" % i) for i in range(GATE_ROUNDS + 1)]
+        body_sq = [keep.tile([P, TOKEN_TILES], F32, name="body_sq%d" % i) for i in range(GATE_ROUNDS)]
+        minus_u = keep.tile([P, TOKEN_TILES], F32, name="minus_u")
         cond = keep.tile([P, TOKEN_TILES], F32, name="cond")
         weight1 = keep.tile([P, TOKEN_TILES], F32, name="weight1")
         weight2 = keep.tile([P, TOKEN_TILES], F32, name="weight2")
@@ -279,30 +280,39 @@ def tile_combnethe_pa_kernel(
                     )
 
         def gate_round(i):
-            m = (2.0 + TAU * TAU) if i == 0 else 2.0
-            tau_power = TAU ** (2 ** (i + 1))
+            k = -rate[i] * lead[i] * lead[i]
+            first = b_powers[i][:, 0, :]
+            if i == 0:
+                nc.gpsimd.tensor_scalar(
+                    out=first, in0=power_sum[i][:], scalar1=k, scalar2=1.0 + k * tau_power[i], op0=ALU.mult, op1=ALU.add
+                )
+            else:
+                nc.gpsimd.tensor_scalar(
+                    out=slope[i][:], in0=power_sum[i][:], scalar1=k, scalar2=k * tau_power[i], op0=ALU.mult, op1=ALU.add
+                )
+                nc.gpsimd.tensor_tensor(out=body_sq[i][:], in0=body[i][:], in1=body[i][:], op=ALU.mult)
+                nc.gpsimd.tensor_tensor(out=minus_u[:], in0=body_sq[i][:], in1=slope[i][:], op=ALU.mult)
+                nc.gpsimd.tensor_scalar(out=first, in0=minus_u[:], scalar1=1.0, scalar2=1.0, op0=ALU.mult, op1=ALU.add)
+            for j in range(1, 4):
+                nc.gpsimd.tensor_tensor(
+                    out=b_powers[i][:, j, :], in0=b_powers[i][:, j - 1, :], in1=b_powers[i][:, j - 1, :], op=ALU.mult
+                )
             nc.gpsimd.tensor_scalar(
-                out=row_sum[:], in0=power_sum[i][:], scalar1=1.0, scalar2=tau_power, op0=ALU.mult, op1=ALU.add
+                out=terms[i][:], in0=b_powers[i][:], scalar1=1.0, scalar2=1.0, op0=ALU.mult, op1=ALU.add
             )
-            if i > 0:
-                nc.gpsimd.tensor_tensor(out=factor_sq[:], in0=factor[:], in1=factor[:], op=ALU.mult)
-                nc.gpsimd.tensor_tensor(out=row_sum[:], in0=row_sum[:], in1=factor_sq[:], op=ALU.mult)
-            nc.gpsimd.tensor_scalar(out=a[:], in0=row_sum[:], scalar1=-2.0 / m, scalar2=2.0, op0=ALU.mult, op1=ALU.add)
-            nc.gpsimd.tensor_scalar(out=b[:], in0=row_sum[:], scalar1=-2.0 / m, scalar2=1.0, op0=ALU.mult, op1=ALU.add)
-            for step in range(INVERSE_STEPS):
-                nc.gpsimd.tensor_tensor(out=b[:], in0=b[:], in1=b[:], op=ALU.mult)
-                nc.gpsimd.tensor_scalar(out=b_plus_1[:], in0=b[:], scalar1=1.0, scalar2=1.0, op0=ALU.mult, op1=ALU.add)
-                nc.gpsimd.tensor_tensor(out=a[:], in0=a[:], in1=b_plus_1[:], op=ALU.mult)
-            nc.gpsimd.tensor_scalar(out=factor[:], in0=a[:], scalar1=2.0 / m, scalar2=0.0, op0=ALU.mult, op1=ALU.add)
-            if i > 0:
-                nc.gpsimd.tensor_tensor(out=factor[:], in0=factor[:], in1=factor_sq[:], op=ALU.mult)
+            nc.gpsimd.tensor_tensor(out=pairs[i][:], in0=terms[i][:, 0:2, :], in1=terms[i][:, 2:4, :], op=ALU.mult)
+            nc.gpsimd.tensor_tensor(out=series[i][:], in0=pairs[i][:, 0, :], in1=pairs[i][:, 1, :], op=ALU.mult)
+            if i == 0:
+                body[i + 1] = series[i]
+            else:
+                nc.gpsimd.tensor_tensor(out=body[i + 1][:], in0=body_sq[i][:], in1=series[i][:], op=ALU.mult)
 
         def gate_end():
-            nc.gpsimd.tensor_scalar(
-                out=cond[:], in0=factor[:], scalar1=TAU ** (2 ** GATE_ROUNDS), scalar2=0.0, op0=ALU.mult, op1=ALU.add
-            )
-            nc.gpsimd.tensor_scalar(out=weight1[:], in0=cond[:], scalar1=-1.0, scalar2=1.0, op0=ALU.mult, op1=ALU.add)
+            k = lead[GATE_ROUNDS] * TAU ** (2 ** GATE_ROUNDS)
+            last = body[GATE_ROUNDS]
+            nc.gpsimd.tensor_scalar(out=weight1[:], in0=last[:], scalar1=-k, scalar2=1.0, op0=ALU.mult, op1=ALU.add)
             nc.gpsimd.tensor_tensor(out=weight1[:], in0=weight1[:], in1=inv_sum[0][:], op=ALU.mult)
+            nc.gpsimd.tensor_scalar(out=cond[:], in0=last[:], scalar1=k, scalar2=0.0, op0=ALU.mult, op1=ALU.add)
             for tt in range(TOKEN_TILES):
                 share1[tt] = keep.tile([P, CLASSES], F32, name="share1_%d" % tt)
                 nc.gpsimd.tensor_scalar(
@@ -321,46 +331,76 @@ def tile_combnethe_pa_kernel(
             )
             nc.sync.dma_start(out=out[P * tt : P * (tt + 1), :], in_=mixed[:])
 
-        LAG = 3
+        for tt in range(TOKEN_TILES):
+            turn_x(tt)
+        for v in range(NETS):
+            b2_wide.append(keep.tile([P, TOKEN_TILES, CLASSES], F32, name="b2_wide%d" % v))
+            nc.scalar.copy(out=b2_wide[v][:], in_=b2_banks[v][:])
+        quantise_x(0)
+        quantise_x(1)
+        sort_planes(0)
+        quantise_x(2)
+        quantise_x(3)
+        sort_codes(0, PACK)
+        sort_planes(1)
+        sort_codes(1, 1)
+
         LAST_O = H_GROUPS - 1
-        GATE_STEP = LAST_O + LAG + 1
-        BLEND_STEP = GATE_STEP + GATE_ROUNDS + 2
-        for s in range(len(rounds) + LAG + 2):
-            done = s - LAG
-            done_f = [tt for tt in range(TOKEN_TILES) if place[(1, tt, H_GROUPS - 1)][0] == done]
-            before_f = [tt for tt in range(TOKEN_TILES) if place[(1, tt, H_GROUPS - 1)][0] == done - 1]
-            if s < len(rounds):
+        EARLY_F = list(range(H_GROUPS - 2))
+        LATE_F = list(range(H_GROUPS - 2, H_GROUPS))
+        logits0 = keep.tile([P, TOKEN_TILES, CLASSES], F32, name="logits0")
+        early1 = keep.tile([P, TOKEN_TILES, CLASSES], F32, name="early1")
+        head_banks = {}
+        for s in range(ROUNDS + 2):
+            if s < ROUNDS:
                 first_layer(s)
-            if s + AHEAD < H_GROUPS:
-                spread_b1(0, s + AHEAD)
-            if s < H_GROUPS:
-                spread_b1(1, s)
-            if s == H_GROUPS:
-                spread_b2()
-            if done == LAST_O:
-                second_layer(0, list(range(TOKEN_TILES)))
-            if done_f:
-                second_layer(1, done_f)
-            if 0 <= s - 1 < len(rounds):
-                turn(s - 1)
-            if 0 <= s - 2 < len(rounds):
+                fetch(s)
+            if s >= 2:
                 quantise(s - 2)
-            if done == LAST_O:
+            if s - 2 == LAST_O:
+                head_banks[0] = second_layer(0, list(range(H_GROUPS)))
+            if s - 2 == H_GROUPS + EARLY_F[-1]:
+                head_banks[1] = second_layer(1, EARLY_F)
+            if s + 2 < ROUNDS:
+                sort_codes(s + 2, 1)
+                if s + 2 < H_GROUPS:
+                    sort_planes(s + 2)
+            if s - 3 == LAST_O:
+                nc.vector.tensor_tensor(out=logits0[:], in0=head_banks[0][:], in1=b2_wide[0][:], op=ALU.add)
+                nc.vector.tensor_reduce(
+                    out=neg_max[0][:], in_=logits0[:], axis=mybir.AxisListType.X, op=ALU.max, negate=True
+                )
+            if 1 <= s <= ROUNDS:
+                interleave(s - 1)
+            if s - 4 == LAST_O:
                 for tt in range(TOKEN_TILES):
-                    exponentials(0, tt)
-            for tt in done_f:
-                exponentials(1, tt)
-            if s == GATE_STEP:
+                    exponential(0, tt, logits0[:, tt, :])
+            if s - 5 == LAST_O:
                 nc.vector.reciprocal(out=inv_sum[0][:], in_=exp_sum[0][:])
-            if 0 <= s - GATE_STEP < GATE_ROUNDS:
-                gate_powers(s - GATE_STEP)
-                gate_round(s - GATE_STEP)
-            if s == GATE_STEP + GATE_ROUNDS:
+            if 0 <= s - 5 - LAST_O < GATE_ROUNDS:
+                gate_powers(s - 5 - LAST_O)
+                gate_round(s - 5 - LAST_O)
+            if s - 5 - LAST_O == GATE_ROUNDS:
                 gate_end()
-            if s == BLEND_STEP:
-                for tt in range(TOKEN_TILES):
-                    if place[(1, tt, H_GROUPS - 1)][0] < done - 1:
-                        blend(tt)
-            if s >= BLEND_STEP:
-                for tt in before_f:
-                    blend(tt)
+            if s == ROUNDS:
+                nc.vector.tensor_tensor(out=early1[:], in0=head_banks[1][:], in1=b2_wide[1][:], op=ALU.add)
+
+        late = second_layer(1, LATE_F)
+        logits1 = {}
+
+        def maximum(tt):
+            logits1[tt] = keep.tile([P, CLASSES], F32, name="logits1_%d" % tt)
+            nc.vector.tensor_tensor(out=logits1[tt][:], in0=late[:, tt, :], in1=early1[:, tt, :], op=ALU.add)
+            nc.vector.tensor_reduce(
+                out=neg_max[1][:, tt : tt + 1], in_=logits1[tt][:], axis=mybir.AxisListType.X, op=ALU.max, negate=True
+            )
+            exponential(1, tt, logits1[tt][:])
+
+        maximum(0)
+        maximum(1)
+        maximum(2)
+        blend(0)
+        maximum(3)
+        blend(1)
+        blend(2)
+        blend(3)

@@ -201,9 +201,15 @@ def tile_combnethe_pa_kernel(
                     bias=b1_cols[:, PACK * r + t : PACK * r + t + 1],
                 )
 
-        def interleave(r):
+        def interleave(r, parts):
             h_grouped[r] = ring.tile([P, TOKENS, PACK], BF16, name="h_grouped", align_bytes=64)
-            nc.vector.tensor_copy(out=h_grouped[r][:], in_=h_rows[r][:].rearrange("p t k -> p k t"))
+            width = TOKENS // parts
+            for i in range(parts):
+                nc.vector.tensor_copy(
+                    out=h_grouped[r][:, width * i : width * (i + 1), :],
+                    in_=h_rows[r][:, :, width * i : width * (i + 1)].rearrange("p t k -> p k t"),
+                )
+                gap()
 
         def quantise(r):
             h_codes[r] = keep.tile([P, TOKENS], U32, name="h_codes%d" % r, align_bytes=64)
@@ -251,14 +257,6 @@ def tile_combnethe_pa_kernel(
             lead.append(lead[i] * lead[i] * rate[i])
         power = {}
         power_sum = [keep.tile([P, TOKEN_TILES], F32, name="power_sum%d" % i) for i in range(GATE_ROUNDS)]
-        slope = [keep.tile([P, TOKEN_TILES], F32, name="slope%d" % i) for i in range(GATE_ROUNDS)]
-        b_powers = [keep.tile([P, 4, TOKEN_TILES], F32, name="b_powers%d" % i) for i in range(GATE_ROUNDS)]
-        terms = [keep.tile([P, 4, TOKEN_TILES], F32, name="terms%d" % i) for i in range(GATE_ROUNDS)]
-        pairs = [keep.tile([P, 2, TOKEN_TILES], F32, name="pairs%d" % i) for i in range(GATE_ROUNDS)]
-        series = [keep.tile([P, TOKEN_TILES], F32, name="series%d" % i) for i in range(GATE_ROUNDS)]
-        body = [keep.tile([P, TOKEN_TILES], F32, name="body%d" % i) for i in range(GATE_ROUNDS + 1)]
-        body_sq = [keep.tile([P, TOKEN_TILES], F32, name="body_sq%d" % i) for i in range(GATE_ROUNDS)]
-        minus_u = keep.tile([P, TOKEN_TILES], F32, name="minus_u")
         cond = keep.tile([P, TOKEN_TILES], F32, name="cond")
         weight1 = keep.tile([P, TOKEN_TILES], F32, name="weight1")
         weight2 = keep.tile([P, TOKEN_TILES], F32, name="weight2")
@@ -279,45 +277,78 @@ def tile_combnethe_pa_kernel(
                         accum_out=power_sum[i][:, column],
                     )
 
-        def gate_round(i):
-            k = -rate[i] * lead[i] * lead[i]
-            first = b_powers[i][:, 0, :]
-            if i == 0:
-                nc.gpsimd.tensor_scalar(
-                    out=first, in0=power_sum[i][:], scalar1=k, scalar2=1.0 + k * tau_power[i], op0=ALU.mult, op1=ALU.add
-                )
-            else:
-                nc.gpsimd.tensor_scalar(
-                    out=slope[i][:], in0=power_sum[i][:], scalar1=k, scalar2=k * tau_power[i], op0=ALU.mult, op1=ALU.add
-                )
-                nc.gpsimd.tensor_tensor(out=body_sq[i][:], in0=body[i][:], in1=body[i][:], op=ALU.mult)
-                nc.gpsimd.tensor_tensor(out=minus_u[:], in0=body_sq[i][:], in1=slope[i][:], op=ALU.mult)
-                nc.gpsimd.tensor_scalar(out=first, in0=minus_u[:], scalar1=1.0, scalar2=1.0, op0=ALU.mult, op1=ALU.add)
-            for j in range(1, 4):
-                nc.gpsimd.tensor_tensor(
-                    out=b_powers[i][:, j, :], in0=b_powers[i][:, j - 1, :], in1=b_powers[i][:, j - 1, :], op=ALU.mult
-                )
-            nc.gpsimd.tensor_scalar(
-                out=terms[i][:], in0=b_powers[i][:], scalar1=1.0, scalar2=1.0, op0=ALU.mult, op1=ALU.add
-            )
-            nc.gpsimd.tensor_tensor(out=pairs[i][:], in0=terms[i][:, 0:2, :], in1=terms[i][:, 2:4, :], op=ALU.mult)
-            nc.gpsimd.tensor_tensor(out=series[i][:], in0=pairs[i][:, 0, :], in1=pairs[i][:, 1, :], op=ALU.mult)
-            if i == 0:
-                body[i + 1] = series[i]
-            else:
-                nc.gpsimd.tensor_tensor(out=body[i + 1][:], in0=body_sq[i][:], in1=series[i][:], op=ALU.mult)
+        def small(name):
+            return keep.tile([P, TOKEN_TILES], F32, name=name)
 
-        def gate_end():
+        def affine(result, a, factor, shift):
+            return lambda: nc.vector.tensor_scalar(
+                out=result[:], in0=a[:], scalar1=factor, scalar2=shift, op0=ALU.mult, op1=ALU.add
+            )
+
+        def product(result, a, b):
+            return lambda: nc.vector.tensor_tensor(out=result[:], in0=a[:], in1=b[:], op=ALU.mult)
+
+        def plus_two_times(result, a, b):
+            return lambda: nc.vector.scalar_tensor_tensor(
+                out=result[:], in0=a[:], scalar=2.0, in1=b[:], op0=ALU.add, op1=ALU.mult
+            )
+
+        waiting = []
+        issued = [0]
+
+        def gap():
+            if issued[0] < len(waiting):
+                for instruction in waiting[issued[0]]:
+                    instruction()
+                issued[0] += 1
+
+        minus_u = [small("minus_u%d" % i) for i in range(GATE_ROUNDS)]
+        series = [small("series%d" % i) for i in range(GATE_ROUNDS)]
+        slope = [small("slope%d" % i) for i in range(GATE_ROUNDS)]
+        body_sq = [small("body_sq%d" % i) for i in range(GATE_ROUNDS)]
+        body2 = small("body2")
+        body3 = small("body3")
+        rest = small("rest")
+
+        def slope_of(i):
+            k = -rate[i] * lead[i] * lead[i]
+            return affine(slope[i], power_sum[i], k, k * tau_power[i])
+
+        def series_groups(i):
+            less = [minus_u[i]] + [small("less%d_%d" % (i, j)) for j in range(1, 4)]
+            part = [small("part%d_%d" % (i, j)) for j in range(3)] + [series[i]]
+            return [
+                [affine(part[0], less[0], 1.0, 2.0), plus_two_times(less[1], less[0], less[0])],
+                [plus_two_times(less[2], less[1], less[1]), plus_two_times(part[1], less[1], part[0])],
+                [plus_two_times(less[3], less[2], less[2]), plus_two_times(part[2], less[2], part[1])],
+                [plus_two_times(part[3], less[3], part[2])],
+            ]
+
+        def gate_groups(i):
+            if i == 0:
+                k = -rate[0]
+                return [[affine(minus_u[0], power_sum[0], k, k * tau_power[0])]] + series_groups(0)
+            if i == 1:
+                return [
+                    [product(body_sq[1], series[0], series[0]), slope_of(1)],
+                    [product(minus_u[1], body_sq[1], slope[1])],
+                ] + series_groups(1)
             k = lead[GATE_ROUNDS] * TAU ** (2 ** GATE_ROUNDS)
-            last = body[GATE_ROUNDS]
-            nc.gpsimd.tensor_scalar(out=weight1[:], in0=last[:], scalar1=-k, scalar2=1.0, op0=ALU.mult, op1=ALU.add)
-            nc.gpsimd.tensor_tensor(out=weight1[:], in0=weight1[:], in1=inv_sum[0][:], op=ALU.mult)
-            nc.gpsimd.tensor_scalar(out=cond[:], in0=last[:], scalar1=k, scalar2=0.0, op0=ALU.mult, op1=ALU.add)
+            return [
+                [product(body2, body_sq[1], series[1]), slope_of(2)],
+                [product(body_sq[2], body2, body2)],
+                [product(minus_u[2], body_sq[2], slope[2])],
+            ] + series_groups(2) + [
+                [product(body3, body_sq[2], series[2])],
+                [affine(cond, body3, k, 0.0), affine(rest, body3, -k, 1.0)],
+                [product(weight1, rest, inv_sum[0])],
+            ]
+
+        def first_share():
             for tt in range(TOKEN_TILES):
                 share1[tt] = keep.tile([P, CLASSES], F32, name="share1_%d" % tt)
-                nc.gpsimd.tensor_scalar(
-                    out=share1[tt][:], in0=exps[(0, tt)][:], scalar1=weight1[:, tt : tt + 1], scalar2=0.0,
-                    op0=ALU.mult, op1=ALU.add,
+                nc.scalar.activation(
+                    out=share1[tt][:], in_=exps[(0, tt)][:], func=ACT.Copy, scale=weight1[:, tt : tt + 1]
                 )
 
         def blend(tt):
@@ -345,52 +376,59 @@ def tile_combnethe_pa_kernel(
         sort_planes(1)
         sort_codes(1, 1)
 
-        LAST_O = H_GROUPS - 1
-        EARLY_F = list(range(H_GROUPS - 2))
-        LATE_F = list(range(H_GROUPS - 2, H_GROUPS))
+        EARLY = list(range(H_GROUPS - 2))
+        LATE = list(range(H_GROUPS - 2, H_GROUPS))
+        CHAIN = H_GROUPS + 2
+        early_sums = [keep.tile([P, TOKEN_TILES, CLASSES], F32, name="early_sums%d" % v) for v in range(NETS)]
         logits0 = keep.tile([P, TOKEN_TILES, CLASSES], F32, name="logits0")
-        early1 = keep.tile([P, TOKEN_TILES, CLASSES], F32, name="early1")
-        head_banks = {}
+        early_banks = {}
+        late_banks = {}
         for s in range(ROUNDS + 2):
             if s < ROUNDS:
                 first_layer(s)
                 fetch(s)
+            if s in (CHAIN + 1, CHAIN + 2):
+                gate_powers(s - CHAIN)
+                waiting.extend(gate_groups(s - CHAIN))
             if s >= 2:
                 quantise(s - 2)
-            if s - 2 == LAST_O:
-                head_banks[0] = second_layer(0, list(range(H_GROUPS)))
-            if s - 2 == H_GROUPS + EARLY_F[-1]:
-                head_banks[1] = second_layer(1, EARLY_F)
+                gap()
+                v, piece = divmod(s - 2, H_GROUPS)
+                if piece == EARLY[-1]:
+                    early_banks[v] = second_layer(v, EARLY)
+                if piece == LATE[-1]:
+                    late_banks[v] = second_layer(v, LATE)
             if s + 2 < ROUNDS:
                 sort_codes(s + 2, 1)
+                gap()
                 if s + 2 < H_GROUPS:
                     sort_planes(s + 2)
-            if s - 3 == LAST_O:
-                nc.vector.tensor_tensor(out=logits0[:], in0=head_banks[0][:], in1=b2_wide[0][:], op=ALU.add)
+            if s == CHAIN:
+                nc.vector.reciprocal(out=inv_sum[0][:], in_=exp_sum[0][:])
+                gate_powers(0)
+                waiting.extend(gate_groups(0))
+            if 1 <= s <= ROUNDS:
+                interleave(s - 1, 2 if s > CHAIN else 1)
+            if s in (H_GROUPS, 2 * H_GROUPS):
+                v = s // H_GROUPS - 1
+                nc.vector.tensor_tensor(out=early_sums[v][:], in0=early_banks[v][:], in1=b2_wide[v][:], op=ALU.add)
+                gap()
+            if s == H_GROUPS + 1:
+                nc.vector.tensor_tensor(out=logits0[:], in0=late_banks[0][:], in1=early_sums[0][:], op=ALU.add)
                 nc.vector.tensor_reduce(
                     out=neg_max[0][:], in_=logits0[:], axis=mybir.AxisListType.X, op=ALU.max, negate=True
                 )
-            if 1 <= s <= ROUNDS:
-                interleave(s - 1)
-            if s - 4 == LAST_O:
                 for tt in range(TOKEN_TILES):
                     exponential(0, tt, logits0[:, tt, :])
-            if s - 5 == LAST_O:
-                nc.vector.reciprocal(out=inv_sum[0][:], in_=exp_sum[0][:])
-            if 0 <= s - 5 - LAST_O < GATE_ROUNDS:
-                gate_powers(s - 5 - LAST_O)
-                gate_round(s - 5 - LAST_O)
-            if s - 5 - LAST_O == GATE_ROUNDS:
-                gate_end()
-            if s == ROUNDS:
-                nc.vector.tensor_tensor(out=early1[:], in0=head_banks[1][:], in1=b2_wide[1][:], op=ALU.add)
 
-        late = second_layer(1, LATE_F)
+        for i in range(len(waiting)):
+            gap()
+        first_share()
         logits1 = {}
 
         def maximum(tt):
             logits1[tt] = keep.tile([P, CLASSES], F32, name="logits1_%d" % tt)
-            nc.vector.tensor_tensor(out=logits1[tt][:], in0=late[:, tt, :], in1=early1[:, tt, :], op=ALU.add)
+            nc.vector.tensor_tensor(out=logits1[tt][:], in0=late_banks[1][:, tt, :], in1=early_sums[1][:, tt, :], op=ALU.add)
             nc.vector.tensor_reduce(
                 out=neg_max[1][:, tt : tt + 1], in_=logits1[tt][:], axis=mybir.AxisListType.X, op=ALU.max, negate=True
             )

@@ -163,11 +163,12 @@ def tile_combnethe_pa_kernel(
         def sort_codes(r, slices):
             v, piece = divmod(r, H_GROUPS)
             w1_sorted[r] = sorted_ring.tile([P, X_GROUPS, PACK, P], U32, name="w1_sorted", align_bytes=64)
-            source = w1_raw[v][piece][:].bitcast(I32).rearrange("p g (m t) -> p g t m", t=PACK)
-            width = PACK // slices
+            source = w1_raw[v][piece][:].bitcast(I32).rearrange("p g (m t) -> p g m t", t=PACK)
+            target = w1_sorted[r][:].bitcast(I32).rearrange("p g t m -> p g m t")
+            width = P // slices
             for i in range(slices):
                 nc.vector.tensor_copy(
-                    out=w1_sorted[r][:, :, width * i : width * (i + 1), :].bitcast(I32),
+                    out=target[:, :, width * i : width * (i + 1), :],
                     in_=source[:, :, width * i : width * (i + 1), :],
                 )
 
@@ -372,7 +373,7 @@ def tile_combnethe_pa_kernel(
         sort_planes(0)
         quantise_x(2)
         quantise_x(3)
-        sort_codes(0, PACK)
+        sort_codes(0, 1)
         sort_planes(1)
         sort_codes(1, 1)
 

@@ -45,6 +45,14 @@ def tile_combnethe_pa_kernel(
         head_psum = ctx.enter_context(tc.psum_pool(name="head_psum", bufs=2))
 
         B2_ROW = NETS * H_GROUPS
+        x_rows = []
+        for tt in range(TOKEN_TILES):
+            x_rows.append(keep.tile([P, D_IN], BF16, name="x_rows%d" % tt))
+            nc.scalar.dma_start(out=x_rows[tt][:], in_=x[P * tt : P * (tt + 1), :])
+        warm_in = keep.tile([P, 1], F32, name="warm_in")
+        warm_out = keep.tile([P, 1], F32, name="warm_out")
+        nc.vector.memset(warm_in[:], 0.0)
+        nc.scalar.activation(out=warm_out[:], in_=warm_in[:], func=ACT.Exp)
         bias_rows = keep.tile([P, K_PASS], BF16, name="bias_rows")
         nc.vector.memset(bias_rows[:], 0.0)
         w1_planes_raw = keep.tile([P, D_H], U8, name="w1_planes_raw", align_bytes=64)
@@ -58,10 +66,6 @@ def tile_combnethe_pa_kernel(
                 out=bias_rows[B2_ROW : B2_ROW + 1, CLASSES * v : CLASSES * (v + 1)],
                 in_=given[v]["b2"].rearrange("(o c) -> o c", o=1),
             )
-        x_rows = []
-        for tt in range(TOKEN_TILES):
-            x_rows.append(keep.tile([P, D_IN], BF16, name="x_rows%d" % tt))
-            nc.scalar.dma_start(out=x_rows[tt][:], in_=x[P * tt : P * (tt + 1), :])
         for v in range(NETS):
             for quadrant in range(4):
                 first = 32 * quadrant + 4 * X_GROUPS * v
@@ -101,29 +105,28 @@ def tile_combnethe_pa_kernel(
                 in_=given[v]["w2"].rearrange("g p n t -> p g (n t)").bitcast(I32),
             )
 
-        warm_in = keep.tile([P, 1], F32, name="warm_in")
-        warm_out = keep.tile([P, 1], F32, name="warm_out")
-        nc.vector.memset(warm_in[:], 0.0)
-        nc.scalar.activation(out=warm_out[:], in_=warm_in[:], func=ACT.Exp)
-
-        bias_words = bias_rows[:].bitcast(F32)
-        bias_turned = sums_psum.tile([P, 2, P], F32, name="sums")
-        for u in range(2):
-            nc.tensor.transpose(bias_turned[:, u, :], bias_words[:, u : K_PASS // 2 : 2], ident[:])
         b1_cols = keep.tile([P, PACK * ROUNDS], F32, name="b1_cols")
-        nc.vector.tensor_copy(
-            out=b1_cols[:].rearrange("p (r u e) -> p r u e", u=2, e=2),
-            in_=bias_turned[:, :, 0:ROUNDS].bitcast(BF16).rearrange("p u (r e) -> p r u e", e=2),
-        )
-        b2_wide = []
-        b2_banks = []
-        for v in range(NETS):
-            b2_banks.append(sums_psum.tile([P, TOKEN_TILES, CLASSES], F32, name="sums"))
-            for tt in range(TOKEN_TILES):
-                nc.tensor.matmul(
-                    out=b2_banks[v][:, tt, :], lhsT=ident_bf16[:, B2_ROW : B2_ROW + 1].to_broadcast([P, P]),
-                    rhs=bias_rows[:, CLASSES * v : CLASSES * (v + 1)], start=True, stop=True,
-                )
+        b2_wide = [keep.tile([P, TOKEN_TILES, CLASSES], F32, name="b2_wide%d" % v) for v in range(NETS)]
+        bias_banks = {}
+
+        def turn_biases():
+            bias_words = bias_rows[:].bitcast(F32)
+            bias_banks["b1"] = sums_psum.tile([P, 2, P], F32, name="sums")
+            for u in range(2):
+                nc.tensor.transpose(bias_banks["b1"][:, u, :], bias_words[:, u : K_PASS // 2 : 2], ident[:])
+            for v in range(NETS):
+                bias_banks[v] = sums_psum.tile([P, TOKEN_TILES, CLASSES], F32, name="sums")
+                for tt in range(TOKEN_TILES):
+                    nc.tensor.matmul(
+                        out=bias_banks[v][:, tt, :], lhsT=ident_bf16[:, B2_ROW : B2_ROW + 1].to_broadcast([P, P]),
+                        rhs=bias_rows[:, CLASSES * v : CLASSES * (v + 1)], start=True, stop=True,
+                    )
+
+        def fetch_b1():
+            nc.vector.tensor_copy(
+                out=b1_cols[:].rearrange("p (r u e) -> p r u e", u=2, e=2),
+                in_=bias_banks["b1"][:, :, 0:ROUNDS].bitcast(BF16).rearrange("p u (r e) -> p r u e", e=2),
+            )
 
         x_grouped = keep.tile([P, X_GROUPS, TOKENS, PACK], BF16, name="x_grouped", align_bytes=64)
         x_codes = keep.tile([P, X_GROUPS, TOKENS], U32, name="x_codes", align_bytes=64)
@@ -178,61 +181,62 @@ def tile_combnethe_pa_kernel(
         h_codes = {}
         h_planes = {}
 
-        def first_layer(r):
+        def first_layer(r, tokens):
             v, piece = divmod(r, H_GROUPS)
             for t in range(PACK):
-                banks[(r, t)] = sums_psum.tile([P, TOKENS], F32, name="sums")
+                banks[(r, t)] = sums_psum.tile([P, tokens.stop - tokens.start], F32, name="sums")
                 first = K_PASS * piece + P * t
                 for g in range(X_GROUPS):
                     nc.tensor.matmul_mx(
                         out=banks[(r, t)][:],
                         lhsT=w1_sorted[r][:, g, t, :].bitcast(FP8X4),
                         lhsT_scale=w1_planes[4 * (X_GROUPS * v + g) : P, first : first + P],
-                        rhs=x_codes[:, g, :].bitcast(FP8X4),
-                        rhs_scale=x_planes[:, g, :],
+                        rhs=x_codes[:, g, tokens].bitcast(FP8X4),
+                        rhs_scale=x_planes[:, g, tokens],
                         start=(g == 0),
                         stop=(g == X_GROUPS - 1),
                     )
 
-        def fetch(r):
-            h_rows[r] = ring.tile([P, PACK, TOKENS], BF16, name="h_rows")
+        def fetch(r, tokens):
+            if tokens.start == 0:
+                h_rows[r] = ring.tile([P, PACK, TOKENS], BF16, name="h_rows")
             for t in range(PACK):
                 nc.scalar.activation(
-                    out=h_rows[r][:, t, :], in_=banks[(r, t)][:], func=ACT.Relu,
+                    out=h_rows[r][:, t, tokens], in_=banks[(r, t)][:], func=ACT.Relu,
                     bias=b1_cols[:, PACK * r + t : PACK * r + t + 1],
                 )
 
-        def interleave(r, parts):
-            h_grouped[r] = ring.tile([P, TOKENS, PACK], BF16, name="h_grouped", align_bytes=64)
-            width = TOKENS // parts
-            for i in range(parts):
-                nc.vector.tensor_copy(
-                    out=h_grouped[r][:, width * i : width * (i + 1), :],
-                    in_=h_rows[r][:, :, width * i : width * (i + 1)].rearrange("p t k -> p k t"),
-                )
-                gap()
-
-        def quantise(r):
-            h_codes[r] = keep.tile([P, TOKENS], U32, name="h_codes%d" % r, align_bytes=64)
-            h_planes[r] = keep.tile([P, TOKENS], U8, name="h_planes%d" % r, align_bytes=64)
-            nc.vector.quantize_mx(
-                out=h_codes[r][:].bitcast(FP8X4),
-                scales=h_planes[r][:],
-                in_=h_grouped[r][:].rearrange("p k t -> p (k t)"),
+        def interleave(r, tokens):
+            if tokens.start == 0:
+                h_grouped[r] = ring.tile([P, TOKENS, PACK], BF16, name="h_grouped", align_bytes=64)
+            nc.vector.tensor_copy(
+                out=h_grouped[r][:, tokens, :], in_=h_rows[r][:, :, tokens].rearrange("p t k -> p k t")
             )
+            gap()
+
+        def quantise(r, tokens):
+            if tokens.start == 0:
+                h_codes[r] = keep.tile([P, TOKENS], U32, name="h_codes%d" % r, align_bytes=64)
+                h_planes[r] = keep.tile([P, TOKENS], U8, name="h_planes%d" % r, align_bytes=64)
+            nc.vector.quantize_mx(
+                out=h_codes[r][:, tokens].bitcast(FP8X4),
+                scales=h_planes[r][:, tokens],
+                in_=h_grouped[r][:, tokens, :].rearrange("p k t -> p (k t)"),
+            )
+            gap()
 
         neg_max = [keep.tile([P, TOKEN_TILES], F32, name="neg_max%d" % v) for v in range(NETS)]
         exp_sum = [keep.tile([P, TOKEN_TILES], F32, name="exp_sum%d" % v) for v in range(NETS)]
         inv_sum = [keep.tile([P, TOKEN_TILES], F32, name="inv_sum%d" % v) for v in range(NETS)]
         exps = {}
 
-        def second_layer(v, pieces):
-            sums = head_psum.tile([P, TOKEN_TILES, CLASSES], F32, name="logits_psum")
-            for tt in range(TOKEN_TILES):
+        def second_layer(v, pieces, token_tiles):
+            sums = head_psum.tile([P, len(token_tiles), CLASSES], F32, name="logits_psum")
+            for tt in token_tiles:
                 for g in pieces:
                     r = H_GROUPS * v + g
                     nc.tensor.matmul_mx(
-                        out=sums[:, tt, :],
+                        out=sums[:, tt - token_tiles[0], :],
                         lhsT=h_codes[r][:, P * tt : P * (tt + 1)].bitcast(FP8X4),
                         lhsT_scale=h_planes[r][:, P * tt : P * (tt + 1)],
                         rhs=w2[v][:, g, :].bitcast(FP8X4),
@@ -365,40 +369,47 @@ def tile_combnethe_pa_kernel(
 
         for tt in range(TOKEN_TILES):
             turn_x(tt)
+        turn_biases()
         for v in range(NETS):
-            b2_wide.append(keep.tile([P, TOKEN_TILES, CLASSES], F32, name="b2_wide%d" % v))
-            nc.scalar.copy(out=b2_wide[v][:], in_=b2_banks[v][:])
+            nc.scalar.copy(out=b2_wide[v][:], in_=bias_banks[v][:])
         quantise_x(0)
         quantise_x(1)
         sort_planes(0)
         quantise_x(2)
         quantise_x(3)
         sort_codes(0, 1)
+        fetch_b1()
         sort_planes(1)
         sort_codes(1, 1)
 
-        EARLY = list(range(H_GROUPS - 2))
-        LATE = list(range(H_GROUPS - 2, H_GROUPS))
+        EARLY = list(range(H_GROUPS - 3))
+        LATE = list(range(H_GROUPS - 3, H_GROUPS))
         CHAIN = H_GROUPS + 2
+        ALL = slice(0, TOKENS)
+        HALVES = (slice(0, TOKENS // 2), slice(TOKENS // 2, TOKENS))
+        ALL_TILES = list(range(TOKEN_TILES))
+        LAST = ROUNDS - 1
         early_sums = [keep.tile([P, TOKEN_TILES, CLASSES], F32, name="early_sums%d" % v) for v in range(NETS)]
         logits0 = keep.tile([P, TOKEN_TILES, CLASSES], F32, name="logits0")
         early_banks = {}
-        late_banks = {}
-        for s in range(ROUNDS + 2):
-            if s < ROUNDS:
-                first_layer(s)
-                fetch(s)
+        for s in range(ROUNDS + 1):
+            if s < LAST:
+                first_layer(s, ALL)
+                fetch(s, ALL)
+            if s == LAST:
+                for half in HALVES:
+                    first_layer(s, half)
+                    fetch(s, half)
             if s in (CHAIN + 1, CHAIN + 2):
                 gate_powers(s - CHAIN)
                 waiting.extend(gate_groups(s - CHAIN))
             if s >= 2:
-                quantise(s - 2)
-                gap()
+                quantise(s - 2, ALL)
                 v, piece = divmod(s - 2, H_GROUPS)
                 if piece == EARLY[-1]:
-                    early_banks[v] = second_layer(v, EARLY)
-                if piece == LATE[-1]:
-                    late_banks[v] = second_layer(v, LATE)
+                    early_banks[v] = second_layer(v, EARLY, ALL_TILES)
+                if s - 2 == H_GROUPS - 1:
+                    late0 = second_layer(0, LATE, ALL_TILES)
             if s + 2 < ROUNDS:
                 sort_codes(s + 2, 1)
                 gap()
@@ -408,38 +419,52 @@ def tile_combnethe_pa_kernel(
                 nc.vector.reciprocal(out=inv_sum[0][:], in_=exp_sum[0][:])
                 gate_powers(0)
                 waiting.extend(gate_groups(0))
-            if 1 <= s <= ROUNDS:
-                interleave(s - 1, 2 if s > CHAIN else 1)
-            if s in (H_GROUPS, 2 * H_GROUPS):
-                v = s // H_GROUPS - 1
+            if 1 <= s < ROUNDS:
+                if s > CHAIN:
+                    for half in HALVES:
+                        interleave(s - 1, half)
+                else:
+                    interleave(s - 1, ALL)
+            if s in (H_GROUPS - 1, 2 * H_GROUPS - 1):
+                v = s // H_GROUPS
                 nc.vector.tensor_tensor(out=early_sums[v][:], in0=early_banks[v][:], in1=b2_wide[v][:], op=ALU.add)
                 gap()
             if s == H_GROUPS + 1:
-                nc.vector.tensor_tensor(out=logits0[:], in0=late_banks[0][:], in1=early_sums[0][:], op=ALU.add)
+                nc.vector.tensor_tensor(out=logits0[:], in0=late0[:], in1=early_sums[0][:], op=ALU.add)
                 nc.vector.tensor_reduce(
                     out=neg_max[0][:], in_=logits0[:], axis=mybir.AxisListType.X, op=ALU.max, negate=True
                 )
                 for tt in range(TOKEN_TILES):
                     exponential(0, tt, logits0[:, tt, :])
 
-        for i in range(len(waiting)):
-            gap()
-        first_share()
         logits1 = {}
+        late1 = {}
 
         def maximum(tt):
             logits1[tt] = keep.tile([P, CLASSES], F32, name="logits1_%d" % tt)
-            nc.vector.tensor_tensor(out=logits1[tt][:], in0=late_banks[1][:, tt, :], in1=early_sums[1][:, tt, :], op=ALU.add)
+            nc.vector.tensor_tensor(
+                out=logits1[tt][:], in0=late1[tt // 2][:, tt % 2, :], in1=early_sums[1][:, tt, :], op=ALU.add
+            )
             nc.vector.tensor_reduce(
                 out=neg_max[1][:, tt : tt + 1], in_=logits1[tt][:], axis=mybir.AxisListType.X, op=ALU.max, negate=True
             )
             exponential(1, tt, logits1[tt][:])
 
+        interleave(LAST, HALVES[0])
+        gap()
+        quantise(LAST, HALVES[0])
+        late1[0] = second_layer(1, LATE, [0, 1])
+        interleave(LAST, HALVES[1])
+        for i in range(len(waiting)):
+            gap()
+        first_share()
         maximum(0)
+        quantise(LAST, HALVES[1])
+        late1[1] = second_layer(1, LATE, [2, 3])
         maximum(1)
-        maximum(2)
         blend(0)
-        maximum(3)
+        maximum(2)
         blend(1)
+        maximum(3)
         blend(2)
         blend(3)

@@ -210,7 +210,8 @@ def tile_combnethe_pa_kernel(
             if tokens.start == 0:
                 h_grouped[r] = ring.tile([P, TOKENS, PACK], BF16, name="h_grouped", align_bytes=64)
             nc.vector.tensor_copy(
-                out=h_grouped[r][:, tokens, :], in_=h_rows[r][:, :, tokens].rearrange("p t k -> p k t")
+                out=h_grouped[r][:, tokens, :].rearrange("p (c i) t -> p c t i", i=4),
+                in_=h_rows[r][:, :, tokens].rearrange("p t (c i) -> p c t i", i=4),
             )
             gap()
 

@@ -38,7 +38,7 @@ def tile_combnethe_pa_kernel(
 
     with ExitStack() as ctx:
         keep = ctx.enter_context(tc.tile_pool(name="keep", bufs=1))
-        ring = ctx.enter_context(tc.tile_pool(name="ring", bufs=3))
+        ring = ctx.enter_context(tc.tile_pool(name="ring", bufs=4))
         sorted_ring = ctx.enter_context(tc.tile_pool(name="sorted_ring", bufs=4))
         ctx.enter_context(tc.manual_schedule())
         sums_psum = ctx.enter_context(tc.psum_pool(name="sums_psum", bufs=6))
@@ -157,10 +157,10 @@ def tile_combnethe_pa_kernel(
         w1_sorted = {}
 
         def sort_planes(piece):
-            cols = slice(K_PASS * piece, K_PASS * (piece + 1))
+            cols = slice(K_PASS * piece, K_PASS * (piece + 2))
             nc.vector.tensor_copy(
-                out=w1_planes[:, cols].rearrange("p (t m) -> p m t", t=PACK),
-                in_=w1_planes_raw[:, cols].rearrange("p (m t) -> p m t", t=PACK),
+                out=w1_planes[:, cols].rearrange("p (q t m) -> p q m t", q=2, t=PACK),
+                in_=w1_planes_raw[:, cols].rearrange("p (q m t) -> p q m t", q=2, t=PACK),
             )
 
         def sort_codes(r, slices):
@@ -286,19 +286,6 @@ def tile_combnethe_pa_kernel(
         def small(name):
             return keep.tile([P, TOKEN_TILES], F32, name=name)
 
-        def affine(result, a, factor, shift):
-            return lambda: nc.vector.tensor_scalar(
-                out=result[:], in0=a[:], scalar1=factor, scalar2=shift, op0=ALU.mult, op1=ALU.add
-            )
-
-        def product(result, a, b):
-            return lambda: nc.vector.tensor_tensor(out=result[:], in0=a[:], in1=b[:], op=ALU.mult)
-
-        def plus_two_times(result, a, b):
-            return lambda: nc.vector.scalar_tensor_tensor(
-                out=result[:], in0=a[:], scalar=2.0, in1=b[:], op0=ALU.add, op1=ALU.mult
-            )
-
         waiting = []
         issued = [0]
 
@@ -308,46 +295,64 @@ def tile_combnethe_pa_kernel(
                     instruction()
                 issued[0] += 1
 
-        minus_u = [small("minus_u%d" % i) for i in range(GATE_ROUNDS)]
-        series = [small("series%d" % i) for i in range(GATE_ROUNDS)]
+        STEPS = 4
+        state = [
+            [keep.tile([P, 2, TOKEN_TILES], F32, name="state%d_%d" % (i, j)) for j in range(STEPS + 1)]
+            for i in range(GATE_ROUNDS)
+        ]
+        for i in range(GATE_ROUNDS):
+            nc.vector.memset(state[i][0][:, 1, :], 1.0)
         slope = [small("slope%d" % i) for i in range(GATE_ROUNDS)]
         body_sq = [small("body_sq%d" % i) for i in range(GATE_ROUNDS)]
         body2 = small("body2")
         body3 = small("body3")
         rest = small("rest")
 
-        def slope_of(i):
-            k = -rate[i] * lead[i] * lead[i]
-            return affine(slope[i], power_sum[i], k, k * tau_power[i])
+        def minus_u(i):
+            return state[i][0][:, 0, :]
+
+        def series(i):
+            return state[i][STEPS][:, 1, :]
+
+        def affine(result, a, factor, shift):
+            return lambda: nc.vector.tensor_scalar(
+                out=result, in0=a, scalar1=factor, scalar2=shift, op0=ALU.mult, op1=ALU.add
+            )
+
+        def product(result, a, b):
+            return lambda: nc.vector.tensor_tensor(out=result, in0=a, in1=b, op=ALU.mult)
+
+        def series_step(i, j):
+            return lambda: nc.vector.scalar_tensor_tensor(
+                out=state[i][j + 1][:], in0=state[i][j][:, 0:1, :].to_broadcast([P, 2, TOKEN_TILES]), scalar=2.0,
+                in1=state[i][j][:], op0=ALU.add, op1=ALU.mult,
+            )
 
         def series_groups(i):
-            less = [minus_u[i]] + [small("less%d_%d" % (i, j)) for j in range(1, 4)]
-            part = [small("part%d_%d" % (i, j)) for j in range(3)] + [series[i]]
-            return [
-                [affine(part[0], less[0], 1.0, 2.0), plus_two_times(less[1], less[0], less[0])],
-                [plus_two_times(less[2], less[1], less[1]), plus_two_times(part[1], less[1], part[0])],
-                [plus_two_times(less[3], less[2], less[2]), plus_two_times(part[2], less[2], part[1])],
-                [plus_two_times(part[3], less[3], part[2])],
-            ]
+            return [[series_step(i, j)] for j in range(STEPS)]
+
+        def slope_of(i):
+            k = -rate[i] * lead[i] * lead[i]
+            return affine(slope[i][:], power_sum[i][:], k, k * tau_power[i])
 
         def gate_groups(i):
             if i == 0:
                 k = -rate[0]
-                return [[affine(minus_u[0], power_sum[0], k, k * tau_power[0])]] + series_groups(0)
+                return [[affine(minus_u(0), power_sum[0][:], k, k * tau_power[0])]] + series_groups(0)
             if i == 1:
                 return [
-                    [product(body_sq[1], series[0], series[0]), slope_of(1)],
-                    [product(minus_u[1], body_sq[1], slope[1])],
+                    [product(body_sq[1][:], series(0), series(0)), slope_of(1)],
+                    [product(minus_u(1), body_sq[1][:], slope[1][:])],
                 ] + series_groups(1)
             k = lead[GATE_ROUNDS] * TAU ** (2 ** GATE_ROUNDS)
             return [
-                [product(body2, body_sq[1], series[1]), slope_of(2)],
-                [product(body_sq[2], body2, body2)],
-                [product(minus_u[2], body_sq[2], slope[2])],
+                [product(body2[:], body_sq[1][:], series(1)), slope_of(2)],
+                [product(body_sq[2][:], body2[:], body2[:])],
+                [product(minus_u(2), body_sq[2][:], slope[2][:])],
             ] + series_groups(2) + [
-                [product(body3, body_sq[2], series[2])],
-                [affine(cond, body3, k, 0.0), affine(rest, body3, -k, 1.0)],
-                [product(weight1, rest, inv_sum[0])],
+                [product(body3[:], body_sq[2][:], series(2))],
+                [affine(cond[:], body3[:], k, 0.0), affine(rest[:], body3[:], -k, 1.0)],
+                [product(weight1[:], rest[:], inv_sum[0][:])],
             ]
 
         def first_share():
@@ -356,17 +361,6 @@ def tile_combnethe_pa_kernel(
                 nc.scalar.activation(
                     out=share1[tt][:], in_=exps[(0, tt)][:], func=ACT.Copy, scale=weight1[:, tt : tt + 1]
                 )
-
-        def blend(tt):
-            column = slice(tt, tt + 1)
-            nc.vector.reciprocal(out=inv_sum[1][:, column], in_=exp_sum[1][:, column])
-            nc.vector.tensor_tensor(out=weight2[:, column], in0=inv_sum[1][:, column], in1=cond[:, column], op=ALU.mult)
-            mixed = keep.tile([P, CLASSES], F32, name="mixed%d" % tt)
-            nc.vector.scalar_tensor_tensor(
-                out=mixed[:], in0=exps[(1, tt)][:], scalar=weight2[:, column], in1=share1[tt][:],
-                op0=ALU.mult, op1=ALU.add,
-            )
-            nc.sync.dma_start(out=out[P * tt : P * (tt + 1), :], in_=mixed[:])
 
         for tt in range(TOKEN_TILES):
             turn_x(tt)
@@ -380,7 +374,6 @@ def tile_combnethe_pa_kernel(
         quantise_x(3)
         sort_codes(0, 1)
         fetch_b1()
-        sort_planes(1)
         sort_codes(1, 1)
 
         EARLY = list(range(H_GROUPS - 3))
@@ -414,18 +407,14 @@ def tile_combnethe_pa_kernel(
             if s + 2 < ROUNDS:
                 sort_codes(s + 2, 1)
                 gap()
-                if s + 2 < H_GROUPS:
+                if s + 2 < H_GROUPS and s % 2 == 0:
                     sort_planes(s + 2)
             if s == CHAIN:
                 nc.vector.reciprocal(out=inv_sum[0][:], in_=exp_sum[0][:])
                 gate_powers(0)
                 waiting.extend(gate_groups(0))
             if 1 <= s < ROUNDS:
-                if s > CHAIN:
-                    for half in HALVES:
-                        interleave(s - 1, half)
-                else:
-                    interleave(s - 1, ALL)
+                interleave(s - 1, ALL)
             if s in (H_GROUPS - 1, 2 * H_GROUPS - 1):
                 v = s // H_GROUPS
                 nc.vector.tensor_tensor(out=early_sums[v][:], in0=early_banks[v][:], in1=b2_wide[v][:], op=ALU.add)
@@ -441,15 +430,27 @@ def tile_combnethe_pa_kernel(
         logits1 = {}
         late1 = {}
 
-        def maximum(tt):
-            logits1[tt] = keep.tile([P, CLASSES], F32, name="logits1_%d" % tt)
-            nc.vector.tensor_tensor(
-                out=logits1[tt][:], in0=late1[tt // 2][:, tt % 2, :], in1=early_sums[1][:, tt, :], op=ALU.add
-            )
+        def maxima(half):
+            tiles = slice(2 * half, 2 * half + 2)
+            logits1[half] = keep.tile([P, 2, CLASSES], F32, name="logits1_%d" % half)
+            nc.vector.tensor_tensor(out=logits1[half][:], in0=late1[half][:], in1=early_sums[1][:, tiles, :], op=ALU.add)
             nc.vector.tensor_reduce(
-                out=neg_max[1][:, tt : tt + 1], in_=logits1[tt][:], axis=mybir.AxisListType.X, op=ALU.max, negate=True
+                out=neg_max[1][:, tiles], in_=logits1[half][:], axis=mybir.AxisListType.X, op=ALU.max, negate=True
             )
-            exponential(1, tt, logits1[tt][:])
+            for i in range(2):
+                exponential(1, 2 * half + i, logits1[half][:, i, :])
+
+        def blend(half):
+            tiles = slice(2 * half, 2 * half + 2)
+            nc.vector.reciprocal(out=inv_sum[1][:, tiles], in_=exp_sum[1][:, tiles])
+            nc.vector.tensor_tensor(out=weight2[:, tiles], in0=inv_sum[1][:, tiles], in1=cond[:, tiles], op=ALU.mult)
+            for tt in range(2 * half, 2 * half + 2):
+                mixed = keep.tile([P, CLASSES], F32, name="mixed%d" % tt)
+                nc.vector.scalar_tensor_tensor(
+                    out=mixed[:], in0=exps[(1, tt)][:], scalar=weight2[:, tt : tt + 1], in1=share1[tt][:],
+                    op0=ALU.mult, op1=ALU.add,
+                )
+                nc.sync.dma_start(out=out[P * tt : P * (tt + 1), :], in_=mixed[:])
 
         interleave(LAST, HALVES[0])
         gap()
@@ -459,13 +460,9 @@ def tile_combnethe_pa_kernel(
         for i in range(len(waiting)):
             gap()
         first_share()
-        maximum(0)
+        maxima(0)
         quantise(LAST, HALVES[1])
         late1[1] = second_layer(1, LATE, [2, 3])
-        maximum(1)
         blend(0)
-        maximum(2)
+        maxima(1)
         blend(1)
-        maximum(3)
-        blend(2)
-        blend(3)

@@ -44,19 +44,18 @@ def tile_combnethe_pa_kernel(
         sums_psum = ctx.enter_context(tc.psum_pool(name="sums_psum", bufs=6))
         head_psum = ctx.enter_context(tc.psum_pool(name="head_psum", bufs=2))
 
-        B2_ROW = NETS * H_GROUPS
         x_rows = []
-        for tt in range(TOKEN_TILES):
-            x_rows.append(keep.tile([P, D_IN], BF16, name="x_rows%d" % tt))
-            nc.scalar.dma_start(out=x_rows[tt][:], in_=x[P * tt : P * (tt + 1), :])
+        x_view = x.rearrange("(t p) k -> p t k", p=P)
+        for half in range(2):
+            x_rows.append(keep.tile([P, 2, D_IN], BF16, name="x_rows%d" % half))
+            nc.sync.dma_start(out=x_rows[half][:], in_=x_view[:, 2 * half : 2 * half + 2, :])
         warm_in = keep.tile([P, 1], F32, name="warm_in")
         warm_out = keep.tile([P, 1], F32, name="warm_out")
         nc.vector.memset(warm_in[:], 0.0)
         nc.scalar.activation(out=warm_out[:], in_=warm_in[:], func=ACT.Exp)
+        B2_ROW = NETS * H_GROUPS
         bias_rows = keep.tile([P, K_PASS], BF16, name="bias_rows")
         nc.vector.memset(bias_rows[:], 0.0)
-        w1_planes_raw = keep.tile([P, D_H], U8, name="w1_planes_raw", align_bytes=64)
-        nc.vector.memset(w1_planes_raw[:].bitcast(I32), 0)
         for v in range(NETS):
             nc.sync.dma_start(
                 out=bias_rows[H_GROUPS * v : H_GROUPS * (v + 1), :],
@@ -66,6 +65,29 @@ def tile_combnethe_pa_kernel(
                 out=bias_rows[B2_ROW : B2_ROW + 1, CLASSES * v : CLASSES * (v + 1)],
                 in_=given[v]["b2"].rearrange("(o c) -> o c", o=1),
             )
+
+        w1_raw = [[], []]
+
+        def load_w1(v, piece):
+            w1_bytes = given[v]["w1"].rearrange("g p n t -> p g (n t)")
+            w1_raw[v].append(keep.tile([P, X_GROUPS, K_PASS], U32, name="w1_raw%d_%d" % (v, piece), align_bytes=64))
+            nc.sync.dma_start(
+                out=w1_raw[v][piece][:].bitcast(I32),
+                in_=w1_bytes[:, :, 4 * K_PASS * piece : 4 * K_PASS * (piece + 1)].bitcast(I32),
+            )
+
+        load_w1(0, 0)
+        FIRST = 2
+        first_planes_raw = keep.tile([P, FIRST * K_PASS], U8, name="first_planes_raw", align_bytes=64)
+        nc.vector.memset(first_planes_raw[:].bitcast(I32), 0)
+        for quadrant in range(4):
+            nc.sync.dma_start(
+                out=first_planes_raw[32 * quadrant : 32 * quadrant + 4 * X_GROUPS, :].bitcast(I32),
+                in_=given[0]["s1"][:, 4 * quadrant : 4 * quadrant + 4, 0 : FIRST * K_PASS].bitcast(I32),
+            )
+        load_w1(0, 1)
+        w1_planes_raw = keep.tile([P, D_H], U8, name="w1_planes_raw", align_bytes=64)
+        nc.vector.memset(w1_planes_raw[:].bitcast(I32), 0)
         for v in range(NETS):
             for quadrant in range(4):
                 first = 32 * quadrant + 4 * X_GROUPS * v
@@ -84,16 +106,10 @@ def tile_combnethe_pa_kernel(
         ident_bf16 = keep.tile([P, P], BF16, name="ident_bf16")
         make_identity(nc, ident_bf16[:])
 
-        w1_raw = [[], []]
         w2 = []
         for v in range(NETS):
-            w1_bytes = given[v]["w1"].rearrange("g p n t -> p g (n t)")
-            for piece in range(H_GROUPS):
-                w1_raw[v].append(keep.tile([P, X_GROUPS, K_PASS], U32, name="w1_raw%d_%d" % (v, piece), align_bytes=64))
-                nc.sync.dma_start(
-                    out=w1_raw[v][piece][:].bitcast(I32),
-                    in_=w1_bytes[:, :, 4 * K_PASS * piece : 4 * K_PASS * (piece + 1)].bitcast(I32),
-                )
+            for piece in range(FIRST if v == 0 else 0, H_GROUPS):
+                load_w1(v, piece)
             for quadrant in range(4):
                 nc.sync.dma_start(
                     out=w2_planes[v][32 * quadrant : 32 * quadrant + 4, :, :].bitcast(I32),
@@ -133,7 +149,7 @@ def tile_combnethe_pa_kernel(
         x_planes = keep.tile([P, X_GROUPS, TOKENS], U8, name="x_planes", align_bytes=64)
 
         def turn_x(tt):
-            x_words = x_rows[tt][:].bitcast(F32)
+            x_words = x_rows[tt // 2][:, tt % 2, :].bitcast(F32)
             turned = sums_psum.tile([P, 2 * X_GROUPS, P], F32, name="sums")
             for g in range(X_GROUPS):
                 for u in range(2):
@@ -156,11 +172,13 @@ def tile_combnethe_pa_kernel(
         w1_planes = keep.tile([P, D_H], U8, name="w1_planes", align_bytes=64)
         w1_sorted = {}
 
-        def sort_planes(piece):
+        first_planes = keep.tile([P, FIRST * K_PASS], U8, name="first_planes", align_bytes=64)
+
+        def sort_planes(piece, target=w1_planes, source=w1_planes_raw):
             cols = slice(K_PASS * piece, K_PASS * (piece + 2))
             nc.vector.tensor_copy(
-                out=w1_planes[:, cols].rearrange("p (q t m) -> p q m t", q=2, t=PACK),
-                in_=w1_planes_raw[:, cols].rearrange("p (q m t) -> p q m t", q=2, t=PACK),
+                out=target[:, cols].rearrange("p (q t m) -> p q m t", q=2, t=PACK),
+                in_=source[:, cols].rearrange("p (q m t) -> p q m t", q=2, t=PACK),
             )
 
         def sort_codes(r, slices):
@@ -190,7 +208,7 @@ def tile_combnethe_pa_kernel(
                     nc.tensor.matmul_mx(
                         out=banks[(r, t)][:],
                         lhsT=w1_sorted[r][:, g, t, :].bitcast(FP8X4),
-                        lhsT_scale=w1_planes[4 * (X_GROUPS * v + g) : P, first : first + P],
+                        lhsT_scale=(first_planes if r < FIRST else w1_planes)[4 * (X_GROUPS * v + g) : P, first : first + P],
                         rhs=x_codes[:, g, tokens].bitcast(FP8X4),
                         rhs_scale=x_planes[:, g, tokens],
                         start=(g == 0),
@@ -369,7 +387,7 @@ def tile_combnethe_pa_kernel(
             nc.scalar.copy(out=b2_wide[v][:], in_=bias_banks[v][:])
         quantise_x(0)
         quantise_x(1)
-        sort_planes(0)
+        sort_planes(0, first_planes, first_planes_raw)
         quantise_x(2)
         quantise_x(3)
         sort_codes(0, 1)
@@ -407,8 +425,8 @@ def tile_combnethe_pa_kernel(
             if s + 2 < ROUNDS:
                 sort_codes(s + 2, 1)
                 gap()
-                if s + 2 < H_GROUPS and s % 2 == 0:
-                    sort_planes(s + 2)
+                if s < H_GROUPS and s % 2 == 0:
+                    sort_planes((s + 2) % H_GROUPS)
             if s == CHAIN:
                 nc.vector.reciprocal(out=inv_sum[0][:], in_=exp_sum[0][:])
                 gate_powers(0)

@@ -404,7 +404,17 @@ def tile_combnethe_pa_kernel(
         early_sums = [keep.tile([P, TOKEN_TILES, CLASSES], F32, name="early_sums%d" % v) for v in range(NETS)]
         logits0 = keep.tile([P, TOKEN_TILES, CLASSES], F32, name="logits0")
         early_banks = {}
-        for s in range(ROUNDS + 1):
+        late_banks = {}
+
+        def quantise_round(r):
+            quantise(r, ALL)
+            v, piece = divmod(r, H_GROUPS)
+            if piece == EARLY[-1]:
+                early_banks[v] = second_layer(v, EARLY, ALL_TILES)
+            if r == H_GROUPS - 1:
+                late_banks[0] = second_layer(0, LATE, ALL_TILES)
+
+        for s in range(ROUNDS):
             if s < LAST:
                 first_layer(s, ALL)
                 fetch(s, ALL)
@@ -415,30 +425,28 @@ def tile_combnethe_pa_kernel(
             if s in (CHAIN + 1, CHAIN + 2):
                 gate_powers(s - CHAIN)
                 waiting.extend(gate_groups(s - CHAIN))
-            if s >= 2:
-                quantise(s - 2, ALL)
-                v, piece = divmod(s - 2, H_GROUPS)
-                if piece == EARLY[-1]:
-                    early_banks[v] = second_layer(v, EARLY, ALL_TILES)
-                if s - 2 == H_GROUPS - 1:
-                    late0 = second_layer(0, LATE, ALL_TILES)
-            if s + 2 < ROUNDS:
+            sorts = s + 2 < ROUNDS
+            if sorts:
                 sort_codes(s + 2, 1)
                 gap()
                 if s < H_GROUPS and s % 2 == 0:
                     sort_planes((s + 2) % H_GROUPS)
+                if s >= 2:
+                    quantise_round(s - 2)
             if s == CHAIN:
                 nc.vector.reciprocal(out=inv_sum[0][:], in_=exp_sum[0][:])
                 gate_powers(0)
                 waiting.extend(gate_groups(0))
-            if 1 <= s < ROUNDS:
+            if s >= 1:
                 interleave(s - 1, ALL)
+            if not sorts:
+                quantise_round(s - 2)
             if s in (H_GROUPS - 1, 2 * H_GROUPS - 1):
                 v = s // H_GROUPS
                 nc.vector.tensor_tensor(out=early_sums[v][:], in0=early_banks[v][:], in1=b2_wide[v][:], op=ALU.add)
                 gap()
             if s == H_GROUPS + 1:
-                nc.vector.tensor_tensor(out=logits0[:], in0=late0[:], in1=early_sums[0][:], op=ALU.add)
+                nc.vector.tensor_tensor(out=logits0[:], in0=late_banks[0][:], in1=early_sums[0][:], op=ALU.add)
                 nc.vector.tensor_reduce(
                     out=neg_max[0][:], in_=logits0[:], axis=mybir.AxisListType.X, op=ALU.max, negate=True
                 )
@@ -448,19 +456,28 @@ def tile_combnethe_pa_kernel(
         logits1 = {}
         late1 = {}
 
-        def maxima(half):
-            tiles = slice(2 * half, 2 * half + 2)
+        def tiles_of(half):
+            return slice(2 * half, 2 * half + 2)
+
+        def sum_logits(half):
             logits1[half] = keep.tile([P, 2, CLASSES], F32, name="logits1_%d" % half)
-            nc.vector.tensor_tensor(out=logits1[half][:], in0=late1[half][:], in1=early_sums[1][:, tiles, :], op=ALU.add)
+            nc.vector.tensor_tensor(
+                out=logits1[half][:], in0=late1[half][:], in1=early_sums[1][:, tiles_of(half), :], op=ALU.add
+            )
+
+        def exponentials(half):
             nc.vector.tensor_reduce(
-                out=neg_max[1][:, tiles], in_=logits1[half][:], axis=mybir.AxisListType.X, op=ALU.max, negate=True
+                out=neg_max[1][:, tiles_of(half)], in_=logits1[half][:], axis=mybir.AxisListType.X, op=ALU.max,
+                negate=True,
             )
             for i in range(2):
                 exponential(1, 2 * half + i, logits1[half][:, i, :])
 
+        def invert_sums(half):
+            nc.vector.reciprocal(out=inv_sum[1][:, tiles_of(half)], in_=exp_sum[1][:, tiles_of(half)])
+
         def blend(half):
-            tiles = slice(2 * half, 2 * half + 2)
-            nc.vector.reciprocal(out=inv_sum[1][:, tiles], in_=exp_sum[1][:, tiles])
+            tiles = tiles_of(half)
             nc.vector.tensor_tensor(out=weight2[:, tiles], in0=inv_sum[1][:, tiles], in1=cond[:, tiles], op=ALU.mult)
             for tt in range(2 * half, 2 * half + 2):
                 mixed = keep.tile([P, CLASSES], F32, name="mixed%d" % tt)
@@ -471,16 +488,20 @@ def tile_combnethe_pa_kernel(
                 nc.sync.dma_start(out=out[P * tt : P * (tt + 1), :], in_=mixed[:])
 
         interleave(LAST, HALVES[0])
-        gap()
+        quantise_round(LAST - 1)
         quantise(LAST, HALVES[0])
         late1[0] = second_layer(1, LATE, [0, 1])
         interleave(LAST, HALVES[1])
         for i in range(len(waiting)):
             gap()
         first_share()
-        maxima(0)
+        sum_logits(0)
         quantise(LAST, HALVES[1])
         late1[1] = second_layer(1, LATE, [2, 3])
+        exponentials(0)
+        sum_logits(1)
+        invert_sums(0)
+        exponentials(1)
         blend(0)
-        maxima(1)
+        invert_sums(1)
         blend(1)

@@ -156,18 +156,18 @@ def tile_combnethe_pa_kernel(
                     nc.tensor.transpose(
                         turned[:, 2 * g + u, :], x_words[:, 256 * g + u : 256 * (g + 1) : 2], ident[:]
                     )
-            nc.scalar.copy(
+            copy = nc.vector.tensor_copy if tt == 1 else nc.scalar.copy
+            copy(
                 out=x_grouped[:, :, P * tt : P * (tt + 1), :].bitcast(F32),
                 in_=turned[:].rearrange("p (g u) k -> p g k u", u=2),
             )
 
-        def quantise_x(tt):
-            for g in range(X_GROUPS):
-                nc.vector.quantize_mx(
-                    out=x_codes[:, g, P * tt : P * (tt + 1)].bitcast(FP8X4),
-                    scales=x_planes[:, g, P * tt : P * (tt + 1)],
-                    in_=x_grouped[:, g, P * tt : P * (tt + 1), :].rearrange("p k t -> p (k t)"),
-                )
+        def quantise_x(tt, g):
+            nc.vector.quantize_mx(
+                out=x_codes[:, g, P * tt : P * (tt + 1)].bitcast(FP8X4),
+                scales=x_planes[:, g, P * tt : P * (tt + 1)],
+                in_=x_grouped[:, g, P * tt : P * (tt + 1), :].rearrange("p k t -> p (k t)"),
+            )
 
         w1_planes = keep.tile([P, D_H], U8, name="w1_planes", align_bytes=64)
         w1_sorted = {}
@@ -181,17 +181,13 @@ def tile_combnethe_pa_kernel(
                 in_=source[:, cols].rearrange("p (q m t) -> p q m t", q=2, t=PACK),
             )
 
-        def sort_codes(r, slices):
+        def sort_codes(r, groups=slice(0, X_GROUPS)):
             v, piece = divmod(r, H_GROUPS)
-            w1_sorted[r] = sorted_ring.tile([P, X_GROUPS, PACK, P], U32, name="w1_sorted", align_bytes=64)
+            if groups.start == 0:
+                w1_sorted[r] = sorted_ring.tile([P, X_GROUPS, PACK, P], U32, name="w1_sorted", align_bytes=64)
             source = w1_raw[v][piece][:].bitcast(I32).rearrange("p g (m t) -> p g m t", t=PACK)
             target = w1_sorted[r][:].bitcast(I32).rearrange("p g t m -> p g m t")
-            width = P // slices
-            for i in range(slices):
-                nc.vector.tensor_copy(
-                    out=target[:, :, width * i : width * (i + 1), :],
-                    in_=source[:, :, width * i : width * (i + 1), :],
-                )
+            nc.vector.tensor_copy(out=target[:, groups, :, :], in_=source[:, groups, :, :])
 
         banks = {}
         h_rows = {}
@@ -203,17 +199,21 @@ def tile_combnethe_pa_kernel(
             v, piece = divmod(r, H_GROUPS)
             for t in range(PACK):
                 banks[(r, t)] = sums_psum.tile([P, tokens.stop - tokens.start], F32, name="sums")
+            if r == 0:
+                order = [(t, g) for g in range(X_GROUPS) for t in range(PACK)]
+            else:
+                order = [(t, g) for t in range(PACK) for g in range(X_GROUPS)]
+            for t, g in order:
                 first = K_PASS * piece + P * t
-                for g in range(X_GROUPS):
-                    nc.tensor.matmul_mx(
-                        out=banks[(r, t)][:],
-                        lhsT=w1_sorted[r][:, g, t, :].bitcast(FP8X4),
-                        lhsT_scale=(first_planes if r < FIRST else w1_planes)[4 * (X_GROUPS * v + g) : P, first : first + P],
-                        rhs=x_codes[:, g, tokens].bitcast(FP8X4),
-                        rhs_scale=x_planes[:, g, tokens],
-                        start=(g == 0),
-                        stop=(g == X_GROUPS - 1),
-                    )
+                nc.tensor.matmul_mx(
+                    out=banks[(r, t)][:],
+                    lhsT=w1_sorted[r][:, g, t, :].bitcast(FP8X4),
+                    lhsT_scale=(first_planes if r < FIRST else w1_planes)[4 * (X_GROUPS * v + g) : P, first : first + P],
+                    rhs=x_codes[:, g, tokens].bitcast(FP8X4),
+                    rhs_scale=x_planes[:, g, tokens],
+                    start=(g == 0),
+                    stop=(g == X_GROUPS - 1),
+                )
 
         def fetch(r, tokens):
             if tokens.start == 0:
@@ -385,14 +385,17 @@ def tile_combnethe_pa_kernel(
         turn_biases()
         for v in range(NETS):
             nc.scalar.copy(out=b2_wide[v][:], in_=bias_banks[v][:])
-        quantise_x(0)
-        quantise_x(1)
+        quantise_x(0, 0)
+        quantise_x(1, 0)
+        sort_codes(0, slice(0, 1))
         sort_planes(0, first_planes, first_planes_raw)
-        quantise_x(2)
-        quantise_x(3)
-        sort_codes(0, 1)
+        quantise_x(2, 0)
+        quantise_x(3, 0)
+        for tt in range(TOKEN_TILES):
+            quantise_x(tt, 1)
+        sort_codes(0, slice(1, X_GROUPS))
         fetch_b1()
-        sort_codes(1, 1)
+        sort_codes(1)
 
         EARLY = list(range(H_GROUPS - 3))
         LATE = list(range(H_GROUPS - 3, H_GROUPS))
@@ -406,11 +409,15 @@ def tile_combnethe_pa_kernel(
         early_banks = {}
         late_banks = {}
 
+        def add_b2(v):
+            nc.vector.tensor_tensor(out=early_sums[v][:], in0=early_banks[v][:], in1=b2_wide[v][:], op=ALU.add)
+            gap()
+
         def quantise_round(r):
             quantise(r, ALL)
             v, piece = divmod(r, H_GROUPS)
-            if piece == EARLY[-1]:
-                early_banks[v] = second_layer(v, EARLY, ALL_TILES)
+            if r == EARLY[-1]:
+                early_banks[0] = second_layer(0, EARLY, ALL_TILES)
             if r == H_GROUPS - 1:
                 late_banks[0] = second_layer(0, LATE, ALL_TILES)
 
@@ -427,7 +434,7 @@ def tile_combnethe_pa_kernel(
                 waiting.extend(gate_groups(s - CHAIN))
             sorts = s + 2 < ROUNDS
             if sorts:
-                sort_codes(s + 2, 1)
+                sort_codes(s + 2)
                 gap()
                 if s < H_GROUPS and s % 2 == 0:
                     sort_planes((s + 2) % H_GROUPS)
@@ -441,10 +448,10 @@ def tile_combnethe_pa_kernel(
                 interleave(s - 1, ALL)
             if not sorts:
                 quantise_round(s - 2)
-            if s in (H_GROUPS - 1, 2 * H_GROUPS - 1):
-                v = s // H_GROUPS
-                nc.vector.tensor_tensor(out=early_sums[v][:], in0=early_banks[v][:], in1=b2_wide[v][:], op=ALU.add)
-                gap()
+            if s == H_GROUPS - 1:
+                add_b2(0)
+            if s == LAST:
+                early_banks[1] = second_layer(1, EARLY, ALL_TILES)
             if s == H_GROUPS + 1:
                 nc.vector.tensor_tensor(out=logits0[:], in0=late_banks[0][:], in1=early_sums[0][:], op=ALU.add)
                 nc.vector.tensor_reduce(
@@ -495,9 +502,10 @@ def tile_combnethe_pa_kernel(
         for i in range(len(waiting)):
             gap()
         first_share()
-        sum_logits(0)
         quantise(LAST, HALVES[1])
+        add_b2(1)
         late1[1] = second_layer(1, LATE, [2, 3])
+        sum_logits(0)
         exponentials(0)
         sum_logits(1)
         invert_sums(0)

from contextlib import ExitStack

import concourse.mybir as mybir
from concourse.masks import make_identity

F32 = mybir.dt.float32
BF16 = mybir.dt.bfloat16
I32 = mybir.dt.int32
U32 = mybir.dt.uint32
U8 = mybir.dt.uint8
FP8X4 = mybir.dt.float8_e4m3fn_x4
ALU = mybir.AluOpType
ACT = mybir.ActivationFunctionType

P = 128
PACK = 4
K_PASS = 512
TOKENS, D_IN, D_H, CLASSES = 512, 1024, 4096, 128
TOKEN_TILES = TOKENS // P
X_GROUPS = D_IN // K_PASS
H_GROUPS = D_H // K_PASS
TAU = 0.5

FLOPS = 2 * (2 * TOKENS * D_IN * D_H + 2 * TOKENS * D_H * CLASSES)


def tile_combnethe_pa_kernel(
    tc, x, W1o_words, W1o_scales, b1o, W2o_words, W2o_scales, b2o,
    W1f_words, W1f_scales, b1f, W2f_words, W2f_scales, b2f, out,
):
    nc = tc.nc
    given = (
        dict(w1=W1o_words, s1=W1o_scales, b1=b1o, w2=W2o_words, s2=W2o_scales, b2=b2o),
        dict(w1=W1f_words, s1=W1f_scales, b1=b1f, w2=W2f_words, s2=W2f_scales, b2=b2f),
    )
    NETS = len(given)
    ROUNDS = NETS * H_GROUPS

    with ExitStack() as ctx:
        keep = ctx.enter_context(tc.tile_pool(name="keep", bufs=1))
        ring = ctx.enter_context(tc.tile_pool(name="ring", bufs=4))
        sorted_ring = ctx.enter_context(tc.tile_pool(name="sorted_ring", bufs=4))
        ctx.enter_context(tc.manual_schedule())
        sums_psum = ctx.enter_context(tc.psum_pool(name="sums_psum", bufs=6))
        head_psum = ctx.enter_context(tc.psum_pool(name="head_psum", bufs=2))

        x_rows = []
        x_view = x.rearrange("(t p) k -> p t k", p=P)
        for half in range(2):
            x_rows.append(keep.tile([P, 2, D_IN], BF16, name="x_rows%d" % half))
            nc.sync.dma_start(out=x_rows[half][:], in_=x_view[:, 2 * half : 2 * half + 2, :])
        warm_in = keep.tile([P, 1], F32, name="warm_in")
        warm_out = keep.tile([P, 1], F32, name="warm_out")
        nc.vector.memset(warm_in[:], 0.0)
        nc.scalar.activation(out=warm_out[:], in_=warm_in[:], func=ACT.Exp)
        B2_ROW = NETS * H_GROUPS
        bias_rows = keep.tile([P, K_PASS], BF16, name="bias_rows")
        nc.vector.memset(bias_rows[:], 0.0)
        for v in range(NETS):
            nc.sync.dma_start(
                out=bias_rows[H_GROUPS * v : H_GROUPS * (v + 1), :],
                in_=given[v]["b1"].rearrange("(g n) -> g n", n=K_PASS),
            )
            nc.sync.dma_start(
                out=bias_rows[B2_ROW : B2_ROW + 1, CLASSES * v : CLASSES * (v + 1)],
                in_=given[v]["b2"].rearrange("(o c) -> o c", o=1),
            )

        w1_raw = [[], []]

        def load_w1(v, piece):
            w1_bytes = given[v]["w1"].rearrange("g p n t -> p g (n t)")
            w1_raw[v].append(keep.tile([P, X_GROUPS, K_PASS], U32, name="w1_raw%d_%d" % (v, piece), align_bytes=64))
            nc.sync.dma_start(
                out=w1_raw[v][piece][:].bitcast(I32),
                in_=w1_bytes[:, :, 4 * K_PASS * piece : 4 * K_PASS * (piece + 1)].bitcast(I32),
            )

        load_w1(0, 0)
        FIRST = 2
        first_planes_raw = keep.tile([P, FIRST * K_PASS], U8, name="first_planes_raw", align_bytes=64)
        nc.vector.memset(first_planes_raw[:].bitcast(I32), 0)
        for quadrant in range(4):
            nc.sync.dma_start(
                out=first_planes_raw[32 * quadrant : 32 * quadrant + 4 * X_GROUPS, :].bitcast(I32),
                in_=given[0]["s1"][:, 4 * quadrant : 4 * quadrant + 4, 0 : FIRST * K_PASS].bitcast(I32),
            )
        load_w1(0, 1)
        w1_planes_raw = keep.tile([P, D_H], U8, name="w1_planes_raw", align_bytes=64)
        nc.vector.memset(w1_planes_raw[:].bitcast(I32), 0)
        for v in range(NETS):
            for quadrant in range(4):
                first = 32 * quadrant + 4 * X_GROUPS * v
                nc.sync.dma_start(
                    out=w1_planes_raw[first : first + 4 * X_GROUPS, :].bitcast(I32),
                    in_=given[v]["s1"][:, 4 * quadrant : 4 * quadrant + 4, :].bitcast(I32),
                )

        w2_planes = []
        for v in range(NETS):
            w2_planes.append(keep.tile([P, H_GROUPS, CLASSES], U8, name="w2_planes%d" % v, align_bytes=64))
            nc.vector.memset(w2_planes[v][:].rearrange("p g c -> p (g c)").bitcast(I32), 0)

        ident = keep.tile([P, P], F32, name="ident")
        make_identity(nc, ident[:])
        ident_bf16 = keep.tile([P, P], BF16, name="ident_bf16")
        make_identity(nc, ident_bf16[:])

        w2 = []
        for v in range(NETS):
            for piece in range(FIRST if v == 0 else 0, H_GROUPS):
                load_w1(v, piece)
            for quadrant in range(4):
                nc.sync.dma_start(
                    out=w2_planes[v][32 * quadrant : 32 * quadrant + 4, :, :].bitcast(I32),
                    in_=given[v]["s2"][:, 4 * quadrant : 4 * quadrant + 4, :].rearrange("g r c -> r g c").bitcast(I32),
                )
            w2.append(keep.tile([P, H_GROUPS, CLASSES], U32, name="w2_%d" % v, align_bytes=64))
            nc.sync.dma_start(
                out=w2[v][:].bitcast(I32),
                in_=given[v]["w2"].rearrange("g p n t -> p g (n t)").bitcast(I32),
            )

        b1_cols = keep.tile([P, PACK * ROUNDS], F32, name="b1_cols")
        b2_wide = [keep.tile([P, TOKEN_TILES, CLASSES], F32, name="b2_wide%d" % v) for v in range(NETS)]
        bias_banks = {}

        def turn_biases():
            bias_words = bias_rows[:].bitcast(F32)
            bias_banks["b1"] = sums_psum.tile([P, 2, P], F32, name="sums")
            for u in range(2):
                nc.tensor.transpose(bias_banks["b1"][:, u, :], bias_words[:, u : K_PASS // 2 : 2], ident[:])
            for v in range(NETS):
                bias_banks[v] = sums_psum.tile([P, TOKEN_TILES, CLASSES], F32, name="sums")
                for tt in range(TOKEN_TILES):
                    nc.tensor.matmul(
                        out=bias_banks[v][:, tt, :], lhsT=ident_bf16[:, B2_ROW : B2_ROW + 1].to_broadcast([P, P]),
                        rhs=bias_rows[:, CLASSES * v : CLASSES * (v + 1)], start=True, stop=True,
                    )

        def fetch_b1():
            nc.vector.tensor_copy(
                out=b1_cols[:].rearrange("p (r u e) -> p r u e", u=2, e=2),
                in_=bias_banks["b1"][:, :, 0:ROUNDS].bitcast(BF16).rearrange("p u (r e) -> p r u e", e=2),
            )

        x_grouped = keep.tile([P, X_GROUPS, TOKENS, PACK], BF16, name="x_grouped", align_bytes=64)
        x_codes = keep.tile([P, X_GROUPS, TOKENS], U32, name="x_codes", align_bytes=64)
        x_planes = keep.tile([P, X_GROUPS, TOKENS], U8, name="x_planes", align_bytes=64)

        def turn_x(tt):
            x_words = x_rows[tt // 2][:, tt % 2, :].bitcast(F32)
            turned = sums_psum.tile([P, 2 * X_GROUPS, P], F32, name="sums")
            for g in range(X_GROUPS):
                for u in range(2):
                    nc.tensor.transpose(
                        turned[:, 2 * g + u, :], x_words[:, 256 * g + u : 256 * (g + 1) : 2], ident[:]
                    )
            copy = nc.vector.tensor_copy if tt == 1 else nc.scalar.copy
            copy(
                out=x_grouped[:, :, P * tt : P * (tt + 1), :].bitcast(F32),
                in_=turned[:].rearrange("p (g u) k -> p g k u", u=2),
            )

        def quantise_x(tt, g):
            nc.vector.quantize_mx(
                out=x_codes[:, g, P * tt : P * (tt + 1)].bitcast(FP8X4),
                scales=x_planes[:, g, P * tt : P * (tt + 1)],
                in_=x_grouped[:, g, P * tt : P * (tt + 1), :].rearrange("p k t -> p (k t)"),
            )

        w1_planes = keep.tile([P, D_H], U8, name="w1_planes", align_bytes=64)
        w1_sorted = {}

        first_planes = keep.tile([P, FIRST * K_PASS], U8, name="first_planes", align_bytes=64)

        def sort_planes(piece, target=w1_planes, source=w1_planes_raw):
            cols = slice(K_PASS * piece, K_PASS * (piece + 2))
            nc.vector.tensor_copy(
                out=target[:, cols].rearrange("p (q t m) -> p q m t", q=2, t=PACK),
                in_=source[:, cols].rearrange("p (q m t) -> p q m t", q=2, t=PACK),
            )

        def sort_codes(r, groups=slice(0, X_GROUPS)):
            v, piece = divmod(r, H_GROUPS)
            if groups.start == 0:
                w1_sorted[r] = sorted_ring.tile([P, X_GROUPS, PACK, P], U32, name="w1_sorted", align_bytes=64)
            source = w1_raw[v][piece][:].bitcast(I32).rearrange("p g (m t) -> p g m t", t=PACK)
            target = w1_sorted[r][:].bitcast(I32).rearrange("p g t m -> p g m t")
            nc.vector.tensor_copy(out=target[:, groups, :, :], in_=source[:, groups, :, :])

        banks = {}
        h_rows = {}
        h_grouped = {}
        h_codes = {}
        h_planes = {}

        def first_layer(r, tokens):
            v, piece = divmod(r, H_GROUPS)
            for t in range(PACK):
                banks[(r, t)] = sums_psum.tile([P, tokens.stop - tokens.start], F32, name="sums")
            if r == 0:
                order = [(t, g) for g in range(X_GROUPS) for t in range(PACK)]
            else:
                order = [(t, g) for t in range(PACK) for g in range(X_GROUPS)]
            for t, g in order:
                first = K_PASS * piece + P * t
                nc.tensor.matmul_mx(
                    out=banks[(r, t)][:],
                    lhsT=w1_sorted[r][:, g, t, :].bitcast(FP8X4),
                    lhsT_scale=(first_planes if r < FIRST else w1_planes)[4 * (X_GROUPS * v + g) : P, first : first + P],
                    rhs=x_codes[:, g, tokens].bitcast(FP8X4),
                    rhs_scale=x_planes[:, g, tokens],
                    start=(g == 0),
                    stop=(g == X_GROUPS - 1),
                )

        def fetch(r, tokens):
            if tokens.start == 0:
                h_rows[r] = ring.tile([P, PACK, TOKENS], BF16, name="h_rows")
            for t in range(PACK):
                nc.scalar.activation(
                    out=h_rows[r][:, t, tokens], in_=banks[(r, t)][:], func=ACT.Relu,
                    bias=b1_cols[:, PACK * r + t : PACK * r + t + 1],
                )

        def interleave(r, tokens):
            if tokens.start == 0:
                h_grouped[r] = ring.tile([P, TOKENS, PACK], BF16, name="h_grouped", align_bytes=64)
            nc.vector.tensor_copy(
                out=h_grouped[r][:, tokens, :].rearrange("p (c i) t -> p c t i", i=4),
                in_=h_rows[r][:, :, tokens].rearrange("p t (c i) -> p c t i", i=4),
            )
            gap()

        def quantise(r, tokens):
            if tokens.start == 0:
                h_codes[r] = keep.tile([P, TOKENS], U32, name="h_codes%d" % r, align_bytes=64)
                h_planes[r] = keep.tile([P, TOKENS], U8, name="h_planes%d" % r, align_bytes=64)
            nc.vector.quantize_mx(
                out=h_codes[r][:, tokens].bitcast(FP8X4),
                scales=h_planes[r][:, tokens],
                in_=h_grouped[r][:, tokens, :].rearrange("p k t -> p (k t)"),
            )
            gap()

        neg_max = [keep.tile([P, TOKEN_TILES], F32, name="neg_max%d" % v) for v in range(NETS)]
        exp_sum = [keep.tile([P, TOKEN_TILES], F32, name="exp_sum%d" % v) for v in range(NETS)]
        inv_sum = [keep.tile([P, TOKEN_TILES], F32, name="inv_sum%d" % v) for v in range(NETS)]
        exps = {}

        def second_layer(v, pieces, token_tiles):
            sums = head_psum.tile([P, len(token_tiles), CLASSES], F32, name="logits_psum")
            for tt in token_tiles:
                for g in pieces:
                    r = H_GROUPS * v + g
                    nc.tensor.matmul_mx(
                        out=sums[:, tt - token_tiles[0], :],
                        lhsT=h_codes[r][:, P * tt : P * (tt + 1)].bitcast(FP8X4),
                        lhsT_scale=h_planes[r][:, P * tt : P * (tt + 1)],
                        rhs=w2[v][:, g, :].bitcast(FP8X4),
                        rhs_scale=w2_planes[v][:, g, :],
                        start=(g == pieces[0]),
                        stop=(g == pieces[-1]),
                    )
            return sums

        def exponential(v, tt, logits):
            column = slice(tt, tt + 1)
            exps[(v, tt)] = keep.tile([P, CLASSES], F32, name="exps%d_%d" % (v, tt))
            nc.scalar.activation(
                out=exps[(v, tt)][:], in_=logits, func=ACT.Exp,
                bias=neg_max[v][:, column], accum_out=exp_sum[v][:, column],
            )

        GATE_ROUNDS = 3
        rate = [2.0 / (2.0 + TAU * TAU), 1.0, 1.0]
        tau_power = [TAU ** (2 ** (i + 1)) for i in range(GATE_ROUNDS)]
        lead = [1.0]
        for i in range(GATE_ROUNDS):
            lead.append(lead[i] * lead[i] * rate[i])
        power = {}
        power_sum = [keep.tile([P, TOKEN_TILES], F32, name="power_sum%d" % i) for i in range(GATE_ROUNDS)]
        cond = keep.tile([P, TOKEN_TILES], F32, name="cond")
        weight1 = keep.tile([P, TOKEN_TILES], F32, name="weight1")
        weight2 = keep.tile([P, TOKEN_TILES], F32, name="weight2")
        share1 = {}

        def gate_powers(i):
            for tt in range(TOKEN_TILES):
                column = slice(tt, tt + 1)
                power[(i, tt)] = keep.tile([P, CLASSES], F32, name="power%d_%d" % (i, tt))
                if i == 0:
                    nc.scalar.activation(
                        out=power[(i, tt)][:], in_=exps[(0, tt)][:], func=ACT.Square,
                        scale=inv_sum[0][:, column], accum_out=power_sum[i][:, column],
                    )
                else:
                    nc.scalar.activation(
                        out=power[(i, tt)][:], in_=power[(i - 1, tt)][:], func=ACT.Square,
                        accum_out=power_sum[i][:, column],
                    )

        def small(name):
            return keep.tile([P, TOKEN_TILES], F32, name=name)

        waiting = []
        issued = [0]

        def gap():
            if issued[0] < len(waiting):
                for instruction in waiting[issued[0]]:
                    instruction()
                issued[0] += 1

        STEPS = 4
        state = [
            [keep.tile([P, 2, TOKEN_TILES], F32, name="state%d_%d" % (i, j)) for j in range(STEPS + 1)]
            for i in range(GATE_ROUNDS)
        ]
        for i in range(GATE_ROUNDS):
            nc.vector.memset(state[i][0][:, 1, :], 1.0)
        slope = [small("slope%d" % i) for i in range(GATE_ROUNDS)]
        body_sq = [small("body_sq%d" % i) for i in range(GATE_ROUNDS)]
        body2 = small("body2")
        body3 = small("body3")
        rest = small("rest")

        def minus_u(i):
            return state[i][0][:, 0, :]

        def series(i):
            return state[i][STEPS][:, 1, :]

        def affine(result, a, factor, shift):
            return lambda: nc.vector.tensor_scalar(
                out=result, in0=a, scalar1=factor, scalar2=shift, op0=ALU.mult, op1=ALU.add
            )

        def product(result, a, b):
            return lambda: nc.vector.tensor_tensor(out=result, in0=a, in1=b, op=ALU.mult)

        def series_step(i, j):
            return lambda: nc.vector.scalar_tensor_tensor(
                out=state[i][j + 1][:], in0=state[i][j][:, 0:1, :].to_broadcast([P, 2, TOKEN_TILES]), scalar=2.0,
                in1=state[i][j][:], op0=ALU.add, op1=ALU.mult,
            )

        def series_groups(i):
            return [[series_step(i, j)] for j in range(STEPS)]

        def slope_of(i):
            k = -rate[i] * lead[i] * lead[i]
            return affine(slope[i][:], power_sum[i][:], k, k * tau_power[i])

        def gate_groups(i):
            if i == 0:
                k = -rate[0]
                return [[affine(minus_u(0), power_sum[0][:], k, k * tau_power[0])]] + series_groups(0)
            if i == 1:
                return [
                    [product(body_sq[1][:], series(0), series(0)), slope_of(1)],
                    [product(minus_u(1), body_sq[1][:], slope[1][:])],
                ] + series_groups(1)
            k = lead[GATE_ROUNDS] * TAU ** (2 ** GATE_ROUNDS)
            return [
                [product(body2[:], body_sq[1][:], series(1)), slope_of(2)],
                [product(body_sq[2][:], body2[:], body2[:])],
                [product(minus_u(2), body_sq[2][:], slope[2][:])],
            ] + series_groups(2) + [
                [product(body3[:], body_sq[2][:], series(2))],
                [affine(cond[:], body3[:], k, 0.0), affine(rest[:], body3[:], -k, 1.0)],
                [product(weight1[:], rest[:], inv_sum[0][:])],
            ]

        def first_share():
            for tt in range(TOKEN_TILES):
                share1[tt] = keep.tile([P, CLASSES], F32, name="share1_%d" % tt)
                nc.scalar.activation(
                    out=share1[tt][:], in_=exps[(0, tt)][:], func=ACT.Copy, scale=weight1[:, tt : tt + 1]
                )

        for tt in range(TOKEN_TILES):
            turn_x(tt)
        turn_biases()
        for v in range(NETS):
            nc.scalar.copy(out=b2_wide[v][:], in_=bias_banks[v][:])
        quantise_x(0, 0)
        quantise_x(1, 0)
        sort_codes(0, slice(0, 1))
        sort_planes(0, first_planes, first_planes_raw)
        quantise_x(2, 0)
        quantise_x(3, 0)
        for tt in range(TOKEN_TILES):
            quantise_x(tt, 1)
        sort_codes(0, slice(1, X_GROUPS))
        fetch_b1()
        sort_codes(1)

        EARLY = list(range(H_GROUPS - 3))
        LATE = list(range(H_GROUPS - 3, H_GROUPS))
        CHAIN = H_GROUPS + 2
        ALL = slice(0, TOKENS)
        HALVES = (slice(0, TOKENS // 2), slice(TOKENS // 2, TOKENS))
        ALL_TILES = list(range(TOKEN_TILES))
        LAST = ROUNDS - 1
        early_sums = [keep.tile([P, TOKEN_TILES, CLASSES], F32, name="early_sums%d" % v) for v in range(NETS)]
        logits0 = keep.tile([P, TOKEN_TILES, CLASSES], F32, name="logits0")
        early_banks = {}
        late_banks = {}

        def add_b2(v):
            nc.vector.tensor_tensor(out=early_sums[v][:], in0=early_banks[v][:], in1=b2_wide[v][:], op=ALU.add)
            gap()

        def quantise_round(r):
            quantise(r, ALL)
            v, piece = divmod(r, H_GROUPS)
            if r == EARLY[-1]:
                early_banks[0] = second_layer(0, EARLY, ALL_TILES)
            if r == H_GROUPS - 1:
                late_banks[0] = second_layer(0, LATE, ALL_TILES)

        for s in range(ROUNDS):
            if s < LAST:
                first_layer(s, ALL)
                fetch(s, ALL)
            if s == LAST:
                for half in HALVES:
                    first_layer(s, half)
                    fetch(s, half)
            if s in (CHAIN + 1, CHAIN + 2):
                gate_powers(s - CHAIN)
                waiting.extend(gate_groups(s - CHAIN))
            sorts = s + 2 < ROUNDS
            if sorts:
                sort_codes(s + 2)
                gap()
                if s < H_GROUPS and s % 2 == 0:
                    sort_planes((s + 2) % H_GROUPS)
                if s >= 2:
                    quantise_round(s - 2)
            if s == CHAIN:
                nc.vector.reciprocal(out=inv_sum[0][:], in_=exp_sum[0][:])
                gate_powers(0)
                waiting.extend(gate_groups(0))
            if s >= 1:
                interleave(s - 1, ALL)
            if not sorts:
                quantise_round(s - 2)
            if s == H_GROUPS - 1:
                add_b2(0)
            if s == LAST:
                early_banks[1] = second_layer(1, EARLY, ALL_TILES)
            if s == H_GROUPS + 1:
                nc.vector.tensor_tensor(out=logits0[:], in0=late_banks[0][:], in1=early_sums[0][:], op=ALU.add)
                nc.vector.tensor_reduce(
                    out=neg_max[0][:], in_=logits0[:], axis=mybir.AxisListType.X, op=ALU.max, negate=True
                )
                for tt in range(TOKEN_TILES):
                    exponential(0, tt, logits0[:, tt, :])

        logits1 = {}
        late1 = {}

        def tiles_of(half):
            return slice(2 * half, 2 * half + 2)

        def sum_logits(half):
            logits1[half] = keep.tile([P, 2, CLASSES], F32, name="logits1_%d" % half)
            nc.vector.tensor_tensor(
                out=logits1[half][:], in0=late1[half][:], in1=early_sums[1][:, tiles_of(half), :], op=ALU.add
            )

        def exponentials(half):
            nc.vector.tensor_reduce(
                out=neg_max[1][:, tiles_of(half)], in_=logits1[half][:], axis=mybir.AxisListType.X, op=ALU.max,
                negate=True,
            )
            for i in range(2):
                exponential(1, 2 * half + i, logits1[half][:, i, :])

        def invert_sums(half):
            nc.vector.reciprocal(out=inv_sum[1][:, tiles_of(half)], in_=exp_sum[1][:, tiles_of(half)])

        def blend(half):
            tiles = tiles_of(half)
            nc.vector.tensor_tensor(out=weight2[:, tiles], in0=inv_sum[1][:, tiles], in1=cond[:, tiles], op=ALU.mult)
            for tt in range(2 * half, 2 * half + 2):
                mixed = keep.tile([P, CLASSES], F32, name="mixed%d" % tt)
                nc.vector.scalar_tensor_tensor(
                    out=mixed[:], in0=exps[(1, tt)][:], scalar=weight2[:, tt : tt + 1], in1=share1[tt][:],
                    op0=ALU.mult, op1=ALU.add,
                )
                nc.sync.dma_start(out=out[P * tt : P * (tt + 1), :], in_=mixed[:])

        interleave(LAST, HALVES[0])
        quantise_round(LAST - 1)
        quantise(LAST, HALVES[0])
        late1[0] = second_layer(1, LATE, [0, 1])
        interleave(LAST, HALVES[1])
        for i in range(len(waiting)):
            gap()
        first_share()
        quantise(LAST, HALVES[1])
        add_b2(1)
        late1[1] = second_layer(1, LATE, [2, 3])
        sum_logits(0)
        exponentials(0)
        sum_logits(1)
        invert_sums(0)
        exponentials(1)
        blend(0)
        invert_sums(1)
        blend(1)
